import numpy as np
import ml_dtypes


def mxq(x, axis, fmt="e4m3"):
    dtype, down = {"e4m3": (ml_dtypes.float8_e4m3fn, 7), "e5m2": (ml_dtypes.float8_e5m2, 14)}[fmt]
    v = np.moveaxis(np.asarray(x, np.float32).astype(ml_dtypes.bfloat16).astype(np.float64), axis, -1)
    blocks = v.reshape(v.shape[:-1] + (-1, 32))
    amax = np.abs(blocks).max(-1, keepdims=True)
    byte = np.maximum(np.where(amax > 0, np.frexp(amax)[1] - 1 + 127, 0) - down, 1)
    scale = np.exp2(byte - 127.0)
    codes = (blocks / scale).astype(np.float32).astype(dtype).astype(np.float64)
    return np.moveaxis((codes * scale).reshape(v.shape), -1, axis)


WIDE = False


def mx_kscale(k):
    if not WIDE:
        return np.ones(k)
    levels = np.array([18, -18])
    if k % 512:
        return np.exp2(np.random.permutation(np.resize(levels, k // 32))).repeat(32)
    a = np.empty((k // 512, 16))
    for p in range(k // 512):
        a[p, :8] = np.random.permutation(np.resize(levels, 8))
        for g in range(8):
            far = levels[np.abs(levels - a[p, g]) >= 10]
            a[p, g + 8] = far[np.random.randint(len(far))]
    return np.exp2(a.ravel()).repeat(32)


BF16 = ml_dtypes.bfloat16


def bf(x):
    return np.asarray(x, np.float32).astype(BF16)


def f64(x):
    return np.asarray(x).astype(np.float64)


B, D, K = 1536, 512, 4


def setup_inputs():
    a = np.maximum(mx_kscale(B), 1.0)[:, None, None]
    u = mx_kscale(D)[None, :, None]
    x0 = bf(np.random.standard_normal((B, D, K)))
    mu = bf(np.random.standard_normal((D, K)) * 0.3)
    w0 = bf(np.eye(D)[None] + np.random.standard_normal((K, D, D)) * 0.7 / np.sqrt(D))
    g = bf(np.random.standard_normal((B, D, K)) * np.exp2(np.random.randint(-6, 1, (B, 1, 1))) / a * u)
    return {"x": bf(f64(x0) * a), "mu_track": mu, "Std_inv_track": bf(f64(w0) / u), "grad_out": g}


def reference(x, mu_track, Std_inv_track, grad_out):
    g = f64(grad_out)
    w = f64(Std_inv_track)
    x_cnt = f64(x) - f64(mu_track)[None]
    gd = mxq(g, 1, "e5m2").transpose(2, 0, 1)
    wd = mxq(w, 1, "e4m3")
    dx = (gd @ wd).transpose(1, 2, 0)
    gb = mxq(g, 0, "e5m2").transpose(2, 1, 0)
    xb = mxq(x_cnt, 0, "e4m3").transpose(2, 0, 1)
    dw = gb @ xb
    return dx, dw

@@ -1,0 +1,299 @@
+from contextlib import ExitStack
+
+import concourse.mybir as mybir
+from concourse.masks import make_identity
+
+B, D, K = 1536, 512, 4
+FLOPS = 2 * 2 * B * D * D * K
+
+F32 = mybir.dt.float32
+BF16 = mybir.dt.bfloat16
+U32 = mybir.dt.uint32
+U8 = mybir.dt.uint8
+E4M3 = mybir.dt.float8_e4m3fn_x4
+E5M2 = mybir.dt.float8_e5m2_x4
+ALU = mybir.AluOpType
+
+P = 128
+J = 4
+G = B // (P * J)
+DK = D * K
+N = G * J
+
+XS = [0,1,2,2,0,1,1,2,1,2,0,0]
+AS = [2,1,1,1,0,1,1,1,0,2,1,1]
+AE = "VVVVVVVVVVVV"
+XH = "PVPPVP"
+XI = "VVVVVVVVVVVV"
+IS = []
+FE = "SVSSVSSSVSVSVSSS"
+WE = "VVSV"
+DS = [10,11,13,13]
+FL = 0
+L1 = ["w0","g00","mu","w1","w2","w3","g01","g02","g03","x00","x01","bc","x10","x11","g10","g11","g12","g13"]
+L2 = ["x20","x21","g20","g21","g22","g23"]
+
+
+def tile_clusternorm1dv3_v_kernel(tc, x, mu, w, g, dx, dw):
+    nc = tc.nc
+    xv = x.rearrange("(g p j) d k -> g p j (d k)", p=P, j=J)
+    gv = g.rearrange("(g p j) d k -> g p j (d k)", p=P, j=J)
+    dxv = dx.rearrange("(g p j) d k -> g p j (d k)", p=P, j=J)
+
+    with ExitStack() as ctx:
+        keep = ctx.enter_context(tc.tile_pool(name="keep", bufs=1))
+        raw = ctx.enter_context(tc.tile_pool(name="raw", bufs=2))
+        stage = ctx.enter_context(tc.tile_pool(name="stage", bufs=2))
+        ptr = ctx.enter_context(tc.psum_pool(name="ptr", bufs=2))
+        pac = ctx.enter_context(tc.psum_pool(name="pac", bufs=6))
+
+        ident = keep.tile([P, P], F32)
+        make_identity(nc, ident[:])
+        identb = keep.tile([P, P], BF16)
+        make_identity(nc, identb[:])
+        gq = keep.tile([P, G, 4, K, P], U32, align_bytes=64)
+        gs = keep.tile([P, G, 4, K, P], U8, align_bytes=64)
+        xq = keep.tile([P, G, K, D], U32, align_bytes=64)
+        xs = keep.tile([P, G, K, D], U8, align_bytes=64)
+        wq = keep.tile([P, K, D], U32, align_bytes=64)
+        ws = keep.tile([P, K, D], U8, align_bytes=64)
+        murow = keep.tile([P, P], BF16)
+        nc.vector.memset(murow[:], 0.0)
+        negmu = keep.tile([P, 16], F32)
+        mub = keep.tile([P, DK], BF16)
+
+        g_raw, x_raw, w_raw = {}, {}, {}
+        gd, gdq, gds, ps, m, ga, xa, wa, tr = {}, {}, {}, {}, {}, {}, {}, {}, {}
+
+        def copier(e):
+            if e == "V":
+                return nc.vector.tensor_copy
+            if e == "S":
+                return nc.scalar.copy
+
+            def gcopy(out, in_):
+                nc.gpsimd.tensor_scalar(out=out, in0=in_, scalar1=1.0, scalar2=0.0, op0=ALU.mult, op1=ALU.add)
+            return gcopy
+
+        def load(s):
+            if s == "mu":
+                nc.sync.dma_start(out=murow[0:16, :], in_=mu.rearrange("(b d) k -> b (d k)", b=16))
+                return
+            if s == "bc":
+                nc.sync.dma_start(out=mub[:], in_=mu.rearrange("d k -> (d k)").partition_broadcast(P))
+                return
+            i = int(s[1])
+            if s[0] == "w":
+                if i % 2 == 0:
+                    t = stage.tile([P, 2, J, D], BF16, name="wraw", tag="o", bufs=3)
+                    w_raw[i // 2] = t
+                nc.sync.dma_start(out=w_raw[i // 2][:, i % 2], in_=w[i].rearrange("(p j) e -> p j e", j=J))
+            elif s[0] == "g":
+                j = int(s[2])
+                if i not in g_raw:
+                    t = raw.tile([P, J, DK], BF16, name="graw", bufs=2)
+                    g_raw[i] = t
+                nc.sync.dma_start(out=g_raw[i][:, j, :], in_=gv[i, :, j, :])
+            else:
+                h = int(s[2])
+                if i not in x_raw:
+                    t = raw.tile([P, J, DK], BF16, name="xraw", bufs=2)
+                    x_raw[i] = t
+                nc.sync.dma_start(out=x_raw[i][:, :, h * 1024:(h + 1) * 1024], in_=xv[i, :, :, h * 1024:(h + 1) * 1024])
+
+        def wcopy(k):
+            t = stage.tile([P, D, J], BF16, align_bytes=64, name="wa", bufs=2)
+            wa[k] = t
+            copier(WE[k])(out=t[:], in_=w_raw[k // 2][:, k % 2].rearrange("p j e -> p e j"))
+
+        def wquant(k):
+            nc.vector.quantize_mx(out=wq[:, k, :].bitcast(E4M3), scales=ws[:, k, :], in_=wa[k][:].rearrange("p e j -> p (e j)"))
+
+        def T(n):
+            i, j = divmod(n, J)
+            gw = g_raw[i][:].bitcast(F32)
+            for kk in range(2):
+                t_ = ptr.tile([P, J, P], F32, name="tr")
+                tr[n, kk] = t_
+                for t in range(J):
+                    nc.tensor.transpose(t_[:, t, :], gw[:, j, 2 * t + kk:1024:8], ident[:])
+
+        def C(n):
+            gd_t = stage.tile([P, K, P, J], BF16, align_bytes=64, name="gd", bufs=2)
+            gd[n] = gd_t
+            for kk in range(2):
+                nc.scalar.copy(out=gd_t[:, 2 * kk:2 * kk + 2], in_=tr[n, kk][:].bitcast(BF16).rearrange("q t (m e) -> q e m t", e=2))
+
+        def Q(n):
+            q = stage.tile([P, K, P], U32, align_bytes=64, name="gdq")
+            s = stage.tile([P, K, P], U8, align_bytes=64, name="gds")
+            gdq[n], gds[n] = q, s
+            nc.vector.quantize_mx(out=q[:].rearrange("p k m -> p (k m)").bitcast(E5M2),
+                                  scales=s[:].rearrange("p k m -> p (k m)"),
+                                  in_=gd[n][:].rearrange("p k m t -> p (k m t)"))
+
+        def M(n):
+            for k in range(K):
+                a = pac.tile([P, D], F32, name="acc")
+                ps[n, k] = a
+                nc.tensor.matmul_mx(out=a[:], lhsT=gdq[n][:, k, :].bitcast(E5M2), lhsT_scale=gds[n][:, k, :],
+                                    rhs=wq[:, k, :].bitcast(E4M3), rhs_scale=ws[:, k, :], start=True, stop=True)
+
+        def E(n, ks, e):
+            if n not in m:
+                m_t = stage.tile([P, D // 4, K, 4], F32, name="m", bufs=2)
+                m[n] = m_t
+            for k in ks:
+                copier(e)(out=m[n][:, :, k, :], in_=ps[n, k][:].rearrange("p (q i) -> p q i", i=4))
+
+        def I(n):
+            i, j = divmod(n, J)
+            o_t = stage.tile([P, D, K], F32, name="o", tag="o", bufs=3)
+            copier("S" if n in IS else "V")(out=o_t[:].rearrange("p (q i) k -> p q i k", i=4), in_=m[n][:].rearrange("p q k i -> p q i k"))
+            nc.sync.dma_start(out=dxv[i, :, j, :], in_=o_t[:].rearrange("p e k -> p (e k)"))
+
+        def interleave(e, out, in_):
+            copier(e)(out=out.rearrange("p k (d a) j -> p d k a j", a=2), in_=in_.rearrange("p j (d a k) -> p d k a j", a=2, k=K))
+
+        def A(u):
+            i, c = divmod(u, 4)
+            t = stage.tile([P, K, P, J], BF16, align_bytes=64, name="ga", bufs=3)
+            ga[u] = t
+            interleave(AE[u], t[:], g_raw[i][:, :, c * 512:(c + 1) * 512])
+
+        def QG(u):
+            i, c = divmod(u, 4)
+            nc.vector.quantize_mx(out=gq[:, i, c].rearrange("p k d -> p (k d)").bitcast(E5M2),
+                                  scales=gs[:, i, c].rearrange("p k d -> p (k d)"),
+                                  in_=ga[u][:].rearrange("p k d j -> p (k d j)"))
+
+        def xtile(h):
+            if h not in xa:
+                t = stage.tile([P, K, 2 * P, J], BF16, align_bytes=64, name="xa", bufs=2)
+                xa[h] = t
+
+        def TN(h):
+            i, b = divmod(h, 2)
+            v = x_raw[i][:, :, b * 1024:(b + 1) * 1024]
+            nc.vector.tensor_sub(out=v, in0=v, in1=mub[:, b * 1024:(b + 1) * 1024].unsqueeze(1).to_broadcast([P, J, 1024]))
+
+        def IX(h, z):
+            i, b = divmod(h, 2)
+            xtile(h)
+            lo = (2 * b + z) * 512
+            interleave(XI[2 * h + z], xa[h][:, :, z * P:(z + 1) * P, :], x_raw[i][:, :, lo:lo + 512])
+
+        def mu_columns():
+            t = pac.tile([P, P], BF16, name="acc")
+            nc.tensor.transpose(t[:], murow[:], identb[:])
+            nc.vector.tensor_scalar(out=negmu[:], in0=t[:, 0:16], scalar1=-1.0, scalar2=None, op0=ALU.mult)
+
+        def XP(h, z):
+            i, b = divmod(h, 2)
+            xtile(h)
+            for v in range(4 * z, 4 * z + 4):
+                lo = b * 1024 + v * P
+                t = pac.tile([P, J, P], F32, name="acc")
+                ps["x", h, v] = t
+                col = negmu[:, lo // P:lo // P + 1].to_broadcast([P, P])
+                for j in range(J):
+                    nc.tensor.matmul(t[:, j, :], lhsT=col, rhs=ident[:], start=(j == 0), stop=False, is_transpose=True)
+                for j in range(J):
+                    nc.tensor.matmul(t[:, j, :], lhsT=identb[:], rhs=x_raw[i][:, j, lo:lo + P], start=False, stop=(j == J - 1))
+
+        def XPE(h, z):
+            for v in range(4 * z, 4 * z + 4):
+                nc.scalar.copy(out=xa[h][:, :, v * 32:(v + 1) * 32, :], in_=ps["x", h, v][:].rearrange("p j (e k) -> p k e j", k=K))
+
+        def QX(h):
+            i, b = divmod(h, 2)
+            for k in range(K):
+                nc.vector.quantize_mx(out=xq[:, i, k, b * 256:(b + 1) * 256].bitcast(E4M3), scales=xs[:, i, k, b * 256:(b + 1) * 256],
+                                      in_=xa[h][:, k].rearrange("p e j -> p (e j)"))
+
+        def Dw(c):
+            for k in range(K):
+                a = pac.tile([P, D], F32, name="acc")
+                ps["w", c, k] = a
+                for i in range(G):
+                    nc.tensor.matmul_mx(out=a[:], lhsT=gq[:, i, c, k, :].bitcast(E5M2), lhsT_scale=gs[:, i, c, k, :],
+                                        rhs=xq[:, i, k, :].bitcast(E4M3), rhs_scale=xs[:, i, k, :],
+                                        start=(i == 0), stop=(i == G - 1))
+
+        def Fw(c):
+            o_t = stage.tile([P, K, D], F32, name="ow", tag="o", bufs=3)
+            for k in range(K):
+                copier(FE[4 * c + k])(out=o_t[:, k, :], in_=ps["w", c, k][:])
+                if k % 2:
+                    nc.sync.dma_start(out=dw[k - 1:k + 1, c * P:(c + 1) * P, :].rearrange("k p e -> p k e"), in_=o_t[:, k - 1:k + 1, :])
+
+        with tc.manual_schedule():
+            for s in L1:
+                load(s)
+            T(0)
+            mu_columns()
+            C(0)
+            wcopy(0)
+            wcopy(1)
+            wquant(0)
+            wcopy(2)
+            wquant(1)
+            Q(0)
+            wcopy(3)
+            wquant(2)
+            wquant(3)
+            an, xn, pend_a, pend_x = 0, 0, [], []
+            for s in range(N + 3):
+                na, nx = (AS[s], XS[s]) if s < N else (0, 0)
+                at, xt = list(range(an, an + na)), [divmod(p, 2) for p in range(xn, xn + nx)]
+                an += na
+                xn += nx
+                if s + 1 < N:
+                    T(s + 1)
+                if 0 < s < N:
+                    Q(s)
+                if s < N:
+                    M(s)
+                for h, z in xt:
+                    if XH[h] == "P":
+                        XP(h, z)
+                if s + 1 < N:
+                    C(s + 1)
+                if 0 < s <= N and (s - 1) not in IS:
+                    I(s - 1)
+                for h in pend_x:
+                    QX(h)
+                for u in pend_a:
+                    QG(u)
+                for c in range(4):
+                    if DS[c] == s:
+                        Dw(c)
+                for h, z in xt:
+                    if XH[h] == "V" and z == 0:
+                        TN(h)
+                for u in at:
+                    if AE[u] == "V":
+                        A(u)
+                for h, z in xt:
+                    if XH[h] == "V" and XI[2 * h + z] == "V":
+                        IX(h, z)
+                if s < N:
+                    E(s, [0, 1, 2, 3], "S")
+                for h, z in xt:
+                    if XH[h] == "P":
+                        XPE(h, z)
+                    elif XI[2 * h + z] == "S":
+                        IX(h, z)
+                for u in at:
+                    if AE[u] == "S":
+                        A(u)
+                if 0 < s <= N and (s - 1) in IS:
+                    I(s - 1)
+                for c in range(4):
+                    if DS[c] + FL == s:
+                        Fw(c)
+                pend_x = [h for h, z in xt if z == 1]
+                pend_a = at
+                if s == 4:
+                    for l in L2:
+                        load(l)

@@ -19,19 +19,8 @@ J = 4
 G = B // (P * J)
 DK = D * K
 N = G * J
-
-XS = [0,1,2,2,0,1,1,2,1,2,0,0]
-AS = [2,1,1,1,0,1,1,1,0,2,1,1]
-AE = "VVVVVVVVVVVV"
-XH = "PVPPVP"
-XI = "VVVVVVVVVVVV"
-IS = []
-FE = "SVSSVSSSVSVSVSSS"
-WE = "VVSV"
-DS = [10,11,13,13]
-FL = 0
-L1 = ["w0","g00","mu","w1","w2","w3","g01","g02","g03","x00","x01","bc","x10","x11","g10","g11","g12","g13"]
-L2 = ["x20","x21","g20","g21","g22","g23"]
+HALF = DK // 2
+NF = 5
 
 
 def tile_clusternorm1dv3_v_kernel(tc, x, mu, w, g, dx, dw):
@@ -42,10 +31,8 @@ def tile_clusternorm1dv3_v_kernel(tc, x, mu, w, g, dx, dw):
 
     with ExitStack() as ctx:
         keep = ctx.enter_context(tc.tile_pool(name="keep", bufs=1))
-        raw = ctx.enter_context(tc.tile_pool(name="raw", bufs=2))
         stage = ctx.enter_context(tc.tile_pool(name="stage", bufs=2))
-        ptr = ctx.enter_context(tc.psum_pool(name="ptr", bufs=2))
-        pac = ctx.enter_context(tc.psum_pool(name="pac", bufs=6))
+        psum = ctx.enter_context(tc.psum_pool(name="psum", bufs=2))
 
         ident = keep.tile([P, P], F32)
         make_identity(nc, ident[:])
@@ -59,241 +46,261 @@ def tile_clusternorm1dv3_v_kernel(tc, x, mu, w, g, dx, dw):
         ws = keep.tile([P, K, D], U8, align_bytes=64)
         murow = keep.tile([P, P], BF16)
         nc.vector.memset(murow[:], 0.0)
+        mucol = keep.tile([P, 16, 2], BF16)
         negmu = keep.tile([P, 16], F32)
-        mub = keep.tile([P, DK], BF16)
+        mu4 = keep.tile([P, 2, (8 - NF) * P, J], BF16)
 
-        g_raw, x_raw, w_raw = {}, {}, {}
-        gd, gdq, gds, ps, m, ga, xa, wa, tr = {}, {}, {}, {}, {}, {}, {}, {}, {}
+        g_raw, x_raw, w_raw, ga, gd, gdq, gds, acc, m, xa, wa, tr, xp, ow = ({} for i in range(14))
 
         def copier(e):
-            if e == "V":
-                return nc.vector.tensor_copy
-            if e == "S":
-                return nc.scalar.copy
+            return nc.vector.tensor_copy if e == "V" else nc.scalar.copy
 
-            def gcopy(out, in_):
-                nc.gpsimd.tensor_scalar(out=out, in0=in_, scalar1=1.0, scalar2=0.0, op0=ALU.mult, op1=ALU.add)
-            return gcopy
+        def load_g(n):
+            i, j = divmod(n, J)
+            if j == 0:
+                g_raw[i] = stage.tile([P, J, DK], BF16, name="graw", bufs=2)
+            nc.sync.dma_start(out=g_raw[i][:, j, :], in_=gv[i, :, j, :])
 
-        def load(s):
-            if s == "mu":
-                nc.sync.dma_start(out=murow[0:16, :], in_=mu.rearrange("(b d) k -> b (d k)", b=16))
-                return
-            if s == "bc":
-                nc.sync.dma_start(out=mub[:], in_=mu.rearrange("d k -> (d k)").partition_broadcast(P))
-                return
-            i = int(s[1])
-            if s[0] == "w":
-                if i % 2 == 0:
-                    t = stage.tile([P, 2, J, D], BF16, name="wraw", tag="o", bufs=3)
-                    w_raw[i // 2] = t
-                nc.sync.dma_start(out=w_raw[i // 2][:, i % 2], in_=w[i].rearrange("(p j) e -> p j e", j=J))
-            elif s[0] == "g":
-                j = int(s[2])
-                if i not in g_raw:
-                    t = raw.tile([P, J, DK], BF16, name="graw", bufs=2)
-                    g_raw[i] = t
-                nc.sync.dma_start(out=g_raw[i][:, j, :], in_=gv[i, :, j, :])
-            else:
-                h = int(s[2])
-                if i not in x_raw:
-                    t = raw.tile([P, J, DK], BF16, name="xraw", bufs=2)
-                    x_raw[i] = t
-                nc.sync.dma_start(out=x_raw[i][:, :, h * 1024:(h + 1) * 1024], in_=xv[i, :, :, h * 1024:(h + 1) * 1024])
+        def load_x(h):
+            i, b = divmod(h, 2)
+            x_raw[h] = stage.tile([P, J, HALF], BF16, name="half", tag="half", bufs=3)
+            nc.sync.dma_start(out=x_raw[h][:], in_=xv[i, :, :, b * HALF:(b + 1) * HALF])
 
-        def wcopy(k):
-            t = stage.tile([P, D, J], BF16, align_bytes=64, name="wa", bufs=2)
-            wa[k] = t
-            copier(WE[k])(out=t[:], in_=w_raw[k // 2][:, k % 2].rearrange("p j e -> p e j"))
+        def load_w(k):
+            if k % 2 == 0:
+                w_raw[k // 2] = stage.tile([P, 2, J, D], BF16, name="wraw", tag="o", bufs=3)
+            nc.sync.dma_start(out=w_raw[k // 2][:, k % 2], in_=w[k].rearrange("(p j) e -> p j e", j=J))
 
-        def wquant(k):
+        def mu_columns():
+            t = psum.tile([P, P], BF16, name="bank", bufs=6)
+            nc.tensor.transpose(t[:], murow[:], identb[:])
+            nc.vector.tensor_scalar(out=negmu[:], in0=t[:, 0:16], scalar1=-1.0, scalar2=None, op0=ALU.mult)
+            nc.vector.tensor_copy(out=mucol[:], in_=t[:, 0:16].unsqueeze(2).to_broadcast([P, 16, 2]))
+
+        def mu_spread():
+            words = mucol[:].rearrange("p b v -> p (b v)").bitcast(F32)
+            for b in range(2):
+                t = psum.tile([P, 8 - NF, P], F32, name="bank", bufs=6)
+                for v in range(NF, 8):
+                    nc.tensor.transpose(t[:, v - NF, :], words[:, 8 * b + v:8 * b + v + 1].to_broadcast([P, P]), ident[:])
+                nc.scalar.copy(out=mu4[:, b].rearrange("p c j -> p (c j)").bitcast(F32).rearrange("p (c v) -> p c v", v=2),
+                               in_=t[:].rearrange("p b n -> p (b n)").unsqueeze(2).to_broadcast([P, (8 - NF) * P, 2]))
+
+        def w_sort(k, e):
+            wa[k] = stage.tile([P, D, J], BF16, align_bytes=64, name="wa", tag="m", bufs=2)
+            copier(e)(out=wa[k][:].rearrange("p (c i) j -> p c j i", i=4), in_=w_raw[k // 2][:, k % 2].rearrange("p j (c i) -> p c j i", i=4))
+
+        def w_quant(k):
             nc.vector.quantize_mx(out=wq[:, k, :].bitcast(E4M3), scales=ws[:, k, :], in_=wa[k][:].rearrange("p e j -> p (e j)"))
 
-        def T(n):
-            i, j = divmod(n, J)
-            gw = g_raw[i][:].bitcast(F32)
-            for kk in range(2):
-                t_ = ptr.tile([P, J, P], F32, name="tr")
-                tr[n, kk] = t_
-                for t in range(J):
-                    nc.tensor.transpose(t_[:, t, :], gw[:, j, 2 * t + kk:1024:8], ident[:])
+        def interleave(out, in_):
+            nc.vector.tensor_copy(out=out.rearrange("p k e j -> p e j k"), in_=in_.rearrange("p j (e k) -> p e j k", k=K))
 
-        def C(n):
-            gd_t = stage.tile([P, K, P, J], BF16, align_bytes=64, name="gd", bufs=2)
-            gd[n] = gd_t
-            for kk in range(2):
-                nc.scalar.copy(out=gd_t[:, 2 * kk:2 * kk + 2], in_=tr[n, kk][:].bitcast(BF16).rearrange("q t (m e) -> q e m t", e=2))
-
-        def Q(n):
-            q = stage.tile([P, K, P], U32, align_bytes=64, name="gdq")
-            s = stage.tile([P, K, P], U8, align_bytes=64, name="gds")
-            gdq[n], gds[n] = q, s
-            nc.vector.quantize_mx(out=q[:].rearrange("p k m -> p (k m)").bitcast(E5M2),
-                                  scales=s[:].rearrange("p k m -> p (k m)"),
-                                  in_=gd[n][:].rearrange("p k m t -> p (k m t)"))
-
-        def M(n):
-            for k in range(K):
-                a = pac.tile([P, D], F32, name="acc")
-                ps[n, k] = a
-                nc.tensor.matmul_mx(out=a[:], lhsT=gdq[n][:, k, :].bitcast(E5M2), lhsT_scale=gds[n][:, k, :],
-                                    rhs=wq[:, k, :].bitcast(E4M3), rhs_scale=ws[:, k, :], start=True, stop=True)
-
-        def E(n, ks, e):
-            if n not in m:
-                m_t = stage.tile([P, D // 4, K, 4], F32, name="m", bufs=2)
-                m[n] = m_t
-            for k in ks:
-                copier(e)(out=m[n][:, :, k, :], in_=ps[n, k][:].rearrange("p (q i) -> p q i", i=4))
-
-        def I(n):
-            i, j = divmod(n, J)
-            o_t = stage.tile([P, D, K], F32, name="o", tag="o", bufs=3)
-            copier("S" if n in IS else "V")(out=o_t[:].rearrange("p (q i) k -> p q i k", i=4), in_=m[n][:].rearrange("p q k i -> p q i k"))
-            nc.sync.dma_start(out=dxv[i, :, j, :], in_=o_t[:].rearrange("p e k -> p (e k)"))
-
-        def interleave(e, out, in_):
-            copier(e)(out=out.rearrange("p k (d a) j -> p d k a j", a=2), in_=in_.rearrange("p j (d a k) -> p d k a j", a=2, k=K))
-
-        def A(u):
+        def g_sort(u):
             i, c = divmod(u, 4)
-            t = stage.tile([P, K, P, J], BF16, align_bytes=64, name="ga", bufs=3)
-            ga[u] = t
-            interleave(AE[u], t[:], g_raw[i][:, :, c * 512:(c + 1) * 512])
+            ga[u] = stage.tile([P, K, P, J], BF16, align_bytes=64, name="ga", bufs=3)
+            interleave(ga[u][:], g_raw[i][:, :, 512 * c:512 * (c + 1)])
 
-        def QG(u):
+        def g_quant(u):
             i, c = divmod(u, 4)
             nc.vector.quantize_mx(out=gq[:, i, c].rearrange("p k d -> p (k d)").bitcast(E5M2),
                                   scales=gs[:, i, c].rearrange("p k d -> p (k d)"),
                                   in_=ga[u][:].rearrange("p k d j -> p (k d j)"))
 
-        def xtile(h):
+        def T(n, kk):
+            i, j = divmod(n, J)
+            words = g_raw[i][:].bitcast(F32)
+            tr[n, kk] = psum.tile([P, 4, P], F32, name="tr", bufs=2)
+            for t in range(4):
+                nc.tensor.transpose(tr[n, kk][:, t, :], words[:, j, 2 * t + kk:1024:8], ident[:])
+
+        def C(n, kk):
+            if kk == 0:
+                gd[n] = stage.tile([P, K, P, 4], BF16, align_bytes=64, name="gd", bufs=2)
+            nc.scalar.copy(out=gd[n][:, 2 * kk:2 * kk + 2], in_=tr[n, kk][:].bitcast(BF16).rearrange("q t (m e) -> q e m t", e=2))
+
+        def Q(n):
+            gdq[n] = stage.tile([P, K, P], U32, align_bytes=64, name="gdq", bufs=5)
+            gds[n] = stage.tile([P, K, P], U8, align_bytes=64, name="gds", bufs=5)
+            nc.vector.quantize_mx(out=gdq[n][:].rearrange("p k m -> p (k m)").bitcast(E5M2),
+                                  scales=gds[n][:].rearrange("p k m -> p (k m)"),
+                                  in_=gd[n][:].rearrange("p k m t -> p (k m t)"))
+
+        def M(n, ks=range(K)):
+            for k in ks:
+                acc[n, k] = psum.tile([P, D], F32, name="bank", bufs=6)
+                nc.tensor.matmul_mx(out=acc[n, k][:], lhsT=gdq[n][:, k, :].bitcast(E5M2), lhsT_scale=gds[n][:, k, :],
+                                    rhs=wq[:, k, :].bitcast(E4M3), rhs_scale=ws[:, k, :], start=True, stop=True)
+
+        def E(n, k, e):
+            if n not in m:
+                m[n] = stage.tile([P, D // 4, K, 4], F32, align_bytes=64, name="m", tag="m", bufs=2)
+            copier(e)(out=m[n][:, :, k, :], in_=acc[n, k][:].rearrange("p (q i) -> p q i", i=4))
+
+        def I(n, parts=1):
+            i, j = divmod(n, J)
+            o = stage.tile([P, D, K], F32, name="o", tag="o", bufs=3)
+            step = D // parts
+            for lo in range(0, D, step):
+                nc.vector.tensor_copy(out=o[:, lo:lo + step].rearrange("p (q i) k -> p q k i", i=4), in_=m[n][:, lo // 4:(lo + step) // 4])
+                nc.sync.dma_start(out=dxv[i, :, j, K * lo:K * (lo + step)], in_=o[:, lo:lo + step].rearrange("p e k -> p (e k)"))
+
+        def xa_tile(h):
             if h not in xa:
-                t = stage.tile([P, K, 2 * P, J], BF16, align_bytes=64, name="xa", bufs=2)
-                xa[h] = t
+                xa[h] = stage.tile([P, K, D // 2, J], BF16, align_bytes=64, name="xa", bufs=2)
+            return xa[h]
 
-        def TN(h):
-            i, b = divmod(h, 2)
-            v = x_raw[i][:, :, b * 1024:(b + 1) * 1024]
-            nc.vector.tensor_sub(out=v, in0=v, in1=mub[:, b * 1024:(b + 1) * 1024].unsqueeze(1).to_broadcast([P, J, 1024]))
+        def x_fill(f):
+            h, v = divmod(f, NF)
+            xp[f] = psum.tile([P, J, P], F32, name="bank", bufs=6)
+            col = negmu[:, 8 * (h % 2) + v:8 * (h % 2) + v + 1].to_broadcast([P, P])
+            for j in range(J):
+                nc.tensor.matmul(xp[f][:, j, :], lhsT=col, rhs=ident[:], start=(j == 0), stop=False, is_transpose=True)
+            nc.tensor.matmul(xp[f][:], lhsT=identb[:], rhs=x_raw[h][:, :, P * v:P * (v + 1)], start=False, stop=True)
 
-        def IX(h, z):
-            i, b = divmod(h, 2)
-            xtile(h)
-            lo = (2 * b + z) * 512
-            interleave(XI[2 * h + z], xa[h][:, :, z * P:(z + 1) * P, :], x_raw[i][:, :, lo:lo + 512])
+        def x_exit(f):
+            h, v = divmod(f, NF)
+            nc.scalar.copy(out=xa_tile(h)[:, :, 32 * v:32 * (v + 1), :], in_=xp[f][:].rearrange("p j (e k) -> p k e j", k=K))
 
-        def mu_columns():
-            t = pac.tile([P, P], BF16, name="acc")
-            nc.tensor.transpose(t[:], murow[:], identb[:])
-            nc.vector.tensor_scalar(out=negmu[:], in0=t[:, 0:16], scalar1=-1.0, scalar2=None, op0=ALU.mult)
+        def x_sort(h):
+            interleave(xa_tile(h)[:, :, 32 * NF:, :], x_raw[h][:, :, P * NF:])
 
-        def XP(h, z):
-            i, b = divmod(h, 2)
-            xtile(h)
-            for v in range(4 * z, 4 * z + 4):
-                lo = b * 1024 + v * P
-                t = pac.tile([P, J, P], F32, name="acc")
-                ps["x", h, v] = t
-                col = negmu[:, lo // P:lo // P + 1].to_broadcast([P, P])
-                for j in range(J):
-                    nc.tensor.matmul(t[:, j, :], lhsT=col, rhs=ident[:], start=(j == 0), stop=False, is_transpose=True)
-                for j in range(J):
-                    nc.tensor.matmul(t[:, j, :], lhsT=identb[:], rhs=x_raw[i][:, j, lo:lo + P], start=False, stop=(j == J - 1))
+        def x_sub(h):
+            v = xa[h][:, :, 32 * NF:, :].rearrange("p k e j -> p e k j")
+            nc.vector.tensor_tensor(out=v, in0=v, in1=mu4[:, h % 2].rearrange("p (e k) j -> p e k j", k=K), op=ALU.subtract)
 
-        def XPE(h, z):
-            for v in range(4 * z, 4 * z + 4):
-                nc.scalar.copy(out=xa[h][:, :, v * 32:(v + 1) * 32, :], in_=ps["x", h, v][:].rearrange("p j (e k) -> p k e j", k=K))
-
-        def QX(h):
+        def x_quant(h):
             i, b = divmod(h, 2)
             for k in range(K):
                 nc.vector.quantize_mx(out=xq[:, i, k, b * 256:(b + 1) * 256].bitcast(E4M3), scales=xs[:, i, k, b * 256:(b + 1) * 256],
                                       in_=xa[h][:, k].rearrange("p e j -> p (e j)"))
 
-        def Dw(c):
-            for k in range(K):
-                a = pac.tile([P, D], F32, name="acc")
-                ps["w", c, k] = a
-                for i in range(G):
-                    nc.tensor.matmul_mx(out=a[:], lhsT=gq[:, i, c, k, :].bitcast(E5M2), lhsT_scale=gs[:, i, c, k, :],
-                                        rhs=xq[:, i, k, :].bitcast(E4M3), rhs_scale=xs[:, i, k, :],
-                                        start=(i == 0), stop=(i == G - 1))
+        def dw_mm(b):
+            c, k = divmod(b, K)
+            acc["w", b] = psum.tile([P, D], F32, name="bank", bufs=6)
+            for i in range(G):
+                nc.tensor.matmul_mx(out=acc["w", b][:], lhsT=gq[:, i, c, k, :].bitcast(E5M2), lhsT_scale=gs[:, i, c, k, :],
+                                    rhs=xq[:, i, k, :].bitcast(E4M3), rhs_scale=xs[:, i, k, :], start=(i == 0), stop=(i == G - 1))
 
-        def Fw(c):
-            o_t = stage.tile([P, K, D], F32, name="ow", tag="o", bufs=3)
-            for k in range(K):
-                copier(FE[4 * c + k])(out=o_t[:, k, :], in_=ps["w", c, k][:])
-                if k % 2:
-                    nc.sync.dma_start(out=dw[k - 1:k + 1, c * P:(c + 1) * P, :].rearrange("k p e -> p k e"), in_=o_t[:, k - 1:k + 1, :])
+        def dw_out(b, e):
+            c, k = divmod(b, K)
+            if k == 0:
+                ow[c] = stage.tile([P, K, D], F32, name="ow", tag="half", bufs=3)
+            copier(e)(out=ow[c][:, k, :], in_=acc["w", b][:])
+            if k % 2 == 1:
+                nc.sync.dma_start(out=dw[k - 1:k + 1, c * P:(c + 1) * P, :].rearrange("k p e -> p k e"), in_=ow[c][:, k - 1:k + 1, :])
+
+        LEAD = 2
+
+        def TC(n):
+            for kk in range(2):
+                C(n, kk)
+                if n + 1 < N:
+                    T(n + 1, kk)
 
         with tc.manual_schedule():
-            for s in L1:
-                load(s)
-            T(0)
+            nc.sync.dma_start(out=murow[0:16, :], in_=mu.rearrange("(b d) k -> b (d k)", b=16))
+            load_w(0)
+            load_g(0)
+            load_w(1)
+            load_g(1)
+            load_g(2)
+            load_w(2)
+            load_w(3)
+            load_g(3)
+            load_x(0)
+            load_g(4)
+            load_x(1)
+            for n in range(5, 8):
+                load_g(n)
+            load_x(2)
             mu_columns()
-            C(0)
-            wcopy(0)
-            wcopy(1)
-            wquant(0)
-            wcopy(2)
-            wquant(1)
+            mu_spread()
+            T(0, 0)
+            T(0, 1)
+            w_sort(0, "V")
+            TC(0)
+            w_sort(1, "V")
+            w_quant(0)
+            w_quant(1)
+            TC(1)
             Q(0)
-            wcopy(3)
-            wquant(2)
-            wquant(3)
-            an, xn, pend_a, pend_x = 0, 0, [], []
-            for s in range(N + 3):
-                na, nx = (AS[s], XS[s]) if s < N else (0, 0)
-                at, xt = list(range(an, an + na)), [divmod(p, 2) for p in range(xn, xn + nx)]
-                an += na
-                xn += nx
-                if s + 1 < N:
-                    T(s + 1)
-                if 0 < s < N:
-                    Q(s)
+            w_sort(2, "V")
+            w_sort(3, "V")
+            for n in range(2, LEAD):
+                TC(n)
+            w_quant(2)
+            w_quant(3)
+            for n in range(1, LEAD):
+                Q(n)
+            chunks = list(range(4)) + [4 * i + c for c in range(4) for i in (1, 2)]
+            u, b = 0, 0
+            for s in range(N - 2):
+                h = s - 1
+                xs_ = 0 <= h < 2 * G
+                us = chunks[u:u + (1 if s < 7 else 2)]
+                u = u + len(us)
+                bs = list(range(b, min(16, b + (4 if s >= 7 else 0))))
+                b = b + len(bs)
                 if s < N:
                     M(s)
-                for h, z in xt:
-                    if XH[h] == "P":
-                        XP(h, z)
-                if s + 1 < N:
-                    C(s + 1)
-                if 0 < s <= N and (s - 1) not in IS:
-                    I(s - 1)
-                for h in pend_x:
-                    QX(h)
-                for u in pend_a:
-                    QG(u)
-                for c in range(4):
-                    if DS[c] == s:
-                        Dw(c)
-                for h, z in xt:
-                    if XH[h] == "V" and z == 0:
-                        TN(h)
-                for u in at:
-                    if AE[u] == "V":
-                        A(u)
-                for h, z in xt:
-                    if XH[h] == "V" and XI[2 * h + z] == "V":
-                        IX(h, z)
+                if xs_:
+                    x_fill(NF * h)
+                    x_fill(NF * h + 1)
+                if 0 <= h - 1 < 2 * G:
+                    x_quant(h - 1)
+                    if h + 2 < 2 * G:
+                        load_x(h + 2)
+                for q in bs[:2]:
+                    dw_mm(q)
+                if s + LEAD < N:
+                    TC(s + LEAD)
+                if xs_:
+                    x_sort(h)
+                for q in us[:1]:
+                    g_sort(q)
+                if xs_:
+                    x_sub(h)
+                if s + LEAD < N:
+                    Q(s + LEAD)
+                for z, q in enumerate(bs[:2]):
+                    dw_out(q, "V" if z == 0 else "S")
+                    if z + 2 < len(bs):
+                        dw_mm(bs[z + 2])
                 if s < N:
-                    E(s, [0, 1, 2, 3], "S")
-                for h, z in xt:
-                    if XH[h] == "P":
-                        XPE(h, z)
-                    elif XI[2 * h + z] == "S":
-                        IX(h, z)
-                for u in at:
-                    if AE[u] == "S":
-                        A(u)
-                if 0 < s <= N and (s - 1) in IS:
-                    I(s - 1)
-                for c in range(4):
-                    if DS[c] + FL == s:
-                        Fw(c)
-                pend_x = [h for h, z in xt if z == 1]
-                pend_a = at
-                if s == 4:
-                    for l in L2:
-                        load(l)
+                    for k in range(K):
+                        E(s, k, "S")
+                        if xs_ and 2 + k < NF:
+                            x_fill(NF * h + 2 + k)
+                for q in us[:1]:
+                    g_quant(q)
+                if s < N:
+                    I(s, 2 if s == N - 1 else 1)
+                for q in bs[2:]:
+                    dw_out(q, "S")
+                for q in us[1:]:
+                    g_sort(q)
+                if xs_:
+                    for v in range(NF):
+                        x_exit(NF * h + v)
+                for q in us[1:]:
+                    g_quant(q)
+                if 3 in us:
+                    for q in range(8, N):
+                        load_g(q)
+            M(N - 2)
+            dw_mm(12)
+            dw_mm(13)
+            for k in range(K):
+                E(N - 2, k, "S")
+            M(N - 1)
+            dw_out(12, "V")
+            dw_out(13, "V")
+            dw_mm(14)
+            dw_mm(15)
+            I(N - 2)
+            for k in range(K):
+                E(N - 1, k, "S")
+            I(N - 1, 2)
+            dw_out(14, "S")
+            dw_out(15, "S")

@@ -20,7 +20,8 @@ G = B // (P * J)
 DK = D * K
 N = G * J
 HALF = DK // 2
-NF = 5
+NF = 4
+NFS = [4, 5, 4, 5, 4, 5]
 
 
 def tile_clusternorm1dv3_v_kernel(tc, x, mu, w, g, dx, dw):
@@ -150,24 +151,27 @@ def tile_clusternorm1dv3_v_kernel(tc, x, mu, w, g, dx, dw):
                 xa[h] = stage.tile([P, K, D // 2, J], BF16, align_bytes=64, name="xa", bufs=2)
             return xa[h]
 
-        def x_fill(f):
-            h, v = divmod(f, NF)
-            xp[f] = psum.tile([P, J, P], F32, name="bank", bufs=6)
-            col = negmu[:, 8 * (h % 2) + v:8 * (h % 2) + v + 1].to_broadcast([P, P])
-            for j in range(J):
-                nc.tensor.matmul(xp[f][:, j, :], lhsT=col, rhs=ident[:], start=(j == 0), stop=False, is_transpose=True)
-            nc.tensor.matmul(xp[f][:], lhsT=identb[:], rhs=x_raw[h][:, :, P * v:P * (v + 1)], start=False, stop=True)
+        def x_fill(*fs):
+            for f in fs:
+                h, v = divmod(f, 8)
+                xp[f] = psum.tile([P, J, P], F32, name="bank", bufs=6)
+                col = negmu[:, 8 * (h % 2) + v:8 * (h % 2) + v + 1].to_broadcast([P, P])
+                for j in range(J):
+                    nc.tensor.matmul(xp[f][:, j, :], lhsT=col, rhs=ident[:], start=(j == 0), stop=False, is_transpose=True)
+            for f in fs:
+                h, v = divmod(f, 8)
+                nc.tensor.matmul(xp[f][:], lhsT=identb[:], rhs=x_raw[h][:, :, P * v:P * (v + 1)], start=False, stop=True)
 
         def x_exit(f):
-            h, v = divmod(f, NF)
+            h, v = divmod(f, 8)
             nc.scalar.copy(out=xa_tile(h)[:, :, 32 * v:32 * (v + 1), :], in_=xp[f][:].rearrange("p j (e k) -> p k e j", k=K))
 
         def x_sort(h):
-            interleave(xa_tile(h)[:, :, 32 * NF:, :], x_raw[h][:, :, P * NF:])
+            interleave(xa_tile(h)[:, :, 32 * NFS[h]:, :], x_raw[h][:, :, P * NFS[h]:])
 
         def x_sub(h):
-            v = xa[h][:, :, 32 * NF:, :].rearrange("p k e j -> p e k j")
-            nc.vector.tensor_tensor(out=v, in0=v, in1=mu4[:, h % 2].rearrange("p (e k) j -> p e k j", k=K), op=ALU.subtract)
+            v = xa[h][:, :, 32 * NFS[h]:, :].rearrange("p k e j -> p e k j")
+            nc.vector.tensor_tensor(out=v, in0=v, in1=mu4[:, h % 2, P * (NFS[h] - NF):].rearrange("p (e k) j -> p e k j", k=K), op=ALU.subtract)
 
         def x_quant(h):
             i, b = divmod(h, 2)
@@ -235,7 +239,7 @@ def tile_clusternorm1dv3_v_kernel(tc, x, mu, w, g, dx, dw):
                 Q(n)
             chunks = list(range(4)) + [4 * i + c for c in range(4) for i in (1, 2)]
             u, b = 0, 0
-            for s in range(N - 2):
+            for s in range(6):
                 h = s - 1
                 xs_ = 0 <= h < 2 * G
                 us = chunks[u:u + (1 if s < 7 else 2)]
@@ -245,8 +249,7 @@ def tile_clusternorm1dv3_v_kernel(tc, x, mu, w, g, dx, dw):
                 if s < N:
                     M(s)
                 if xs_:
-                    x_fill(NF * h)
-                    x_fill(NF * h + 1)
+                    x_fill(8 * h, 8 * h + 1)
                 if 0 <= h - 1 < 2 * G:
                     x_quant(h - 1)
                     if h + 2 < 2 * G:
@@ -270,8 +273,10 @@ def tile_clusternorm1dv3_v_kernel(tc, x, mu, w, g, dx, dw):
                 if s < N:
                     for k in range(K):
                         E(s, k, "S")
-                        if xs_ and 2 + k < NF:
-                            x_fill(NF * h + 2 + k)
+                        if xs_ and k == 1:
+                            x_fill(8 * h + 2, 8 * h + 3)
+                        if xs_ and NFS[h] > 4 and k == NFS[h] - 3:
+                            x_fill(*range(8 * h + 4, 8 * h + NFS[h]))
                 for q in us[:1]:
                     g_quant(q)
                 if s < N:
@@ -281,26 +286,106 @@ def tile_clusternorm1dv3_v_kernel(tc, x, mu, w, g, dx, dw):
                 for q in us[1:]:
                     g_sort(q)
                 if xs_:
-                    for v in range(NF):
-                        x_exit(NF * h + v)
+                    for v in range(NFS[h]):
+                        x_exit(8 * h + v)
                 for q in us[1:]:
                     g_quant(q)
                 if 3 in us:
                     for q in range(8, N):
                         load_g(q)
-            M(N - 2)
+            def sort_quant(first, second):
+                g_sort(first)
+                g_sort(second)
+                g_quant(first)
+                g_quant(second)
+
+            def empty(n, engines="SSSS"):
+                for k in range(K):
+                    E(n, k, engines[k])
+
+            f = 8 * 5
+            x_fill(f, f + 1)
+            x_fill(f + 2, f + 3)
+            x_quant(4)
+            x_sort(5)
+            C(8, 0)
+            x_exit(f)
+            x_exit(f + 1)
+            x_fill(*range(f + 4, f + NFS[5]))
+            x_sub(5)
+            C(8, 1)
+            M(6)
+            for v in range(2, NFS[5]):
+                x_exit(f + v)
+            T(9, 0)
+            T(9, 1)
+            Q(8)
+            x_quant(5)
+            dw_mm(0)
+            dw_mm(1)
+            empty(6)
+            M(7)
+            g_sort(5)
+            I(6)
+            g_sort(9)
+            dw_out(0, "S")
+            dw_out(1, "S")
+            dw_mm(2)
+            dw_mm(3)
+            g_quant(5)
+            g_quant(9)
+            empty(7)
+            I(7)
+            M(8)
+            dw_out(2, "S")
+            dw_out(3, "S")
+            dw_mm(4)
+            dw_mm(5)
+            TC(9)
+            g_sort(6)
+            g_sort(10)
+            Q(9)
+            empty(8)
+            dw_mm(6)
+            dw_mm(7)
+            dw_out(4, "S")
+            dw_out(5, "S")
+            M(9)
+            g_quant(6)
+            g_quant(10)
+            I(8)
+            dw_out(6, "S")
+            dw_out(7, "S")
+            dw_mm(8)
+            dw_mm(9)
+            TC(10)
+            g_sort(7)
+            g_sort(11)
+            Q(10)
+            empty(9)
+            dw_mm(10)
+            dw_mm(11)
+            dw_out(8, "S")
+            dw_out(9, "S")
+            M(10)
+            g_quant(7)
+            g_quant(11)
+            I(9)
+            dw_out(10, "V")
+            dw_out(11, "V")
             dw_mm(12)
             dw_mm(13)
-            for k in range(K):
-                E(N - 2, k, "S")
-            M(N - 1)
+            C(11, 0)
+            C(11, 1)
+            Q(11)
+            empty(10)
+            M(11)
             dw_out(12, "V")
             dw_out(13, "V")
             dw_mm(14)
             dw_mm(15)
-            I(N - 2)
-            for k in range(K):
-                E(N - 1, k, "S")
-            I(N - 1, 2)
+            I(10)
+            empty(11)
+            I(11, 2)
             dw_out(14, "S")
             dw_out(15, "S")

@@ -21,7 +21,7 @@ DK = D * K
 N = G * J
 HALF = DK // 2
 NF = 4
-NFS = [4, 5, 4, 5, 4, 5]
+NFS = [4, 4, 5, 4, 5, 5]
 
 
 def tile_clusternorm1dv3_v_kernel(tc, x, mu, w, g, dx, dw):
@@ -47,11 +47,13 @@ def tile_clusternorm1dv3_v_kernel(tc, x, mu, w, g, dx, dw):
         ws = keep.tile([P, K, D], U8, align_bytes=64)
         murow = keep.tile([P, P], BF16)
         nc.vector.memset(murow[:], 0.0)
-        mucol = keep.tile([P, 16, 2], BF16)
+        muwords = keep.tile([P, 2 * P], BF16)
+        nc.vector.memset(muwords[:], 0.0)
+        mucol = keep.tile([P, 8], F32)
         negmu = keep.tile([P, 16], F32)
-        mu4 = keep.tile([P, 2, (8 - NF) * P, J], BF16)
+        mub = keep.tile([P, 2, 4 * P], BF16)
 
-        g_raw, x_raw, w_raw, ga, gd, gdq, gds, acc, m, xa, wa, tr, xp, ow = ({} for i in range(14))
+        g_raw, x_raw, w_raw, ga, gd, gdq, gds, acc, m, xa, wa, tr, xp, ow, xc = ({} for i in range(15))
 
         def copier(e):
             return nc.vector.tensor_copy if e == "V" else nc.scalar.copy
@@ -76,16 +78,15 @@ def tile_clusternorm1dv3_v_kernel(tc, x, mu, w, g, dx, dw):
             t = psum.tile([P, P], BF16, name="bank", bufs=6)
             nc.tensor.transpose(t[:], murow[:], identb[:])
             nc.vector.tensor_scalar(out=negmu[:], in0=t[:, 0:16], scalar1=-1.0, scalar2=None, op0=ALU.mult)
-            nc.vector.tensor_copy(out=mucol[:], in_=t[:, 0:16].unsqueeze(2).to_broadcast([P, 16, 2]))
+            u = psum.tile([P, P], F32, name="bank", bufs=6)
+            nc.tensor.transpose(u[:], muwords[:].bitcast(F32), ident[:])
+            nc.vector.tensor_copy(out=mucol[:], in_=u[:, 0:8])
 
         def mu_spread():
-            words = mucol[:].rearrange("p b v -> p (b v)").bitcast(F32)
-            for b in range(2):
-                t = psum.tile([P, 8 - NF, P], F32, name="bank", bufs=6)
-                for v in range(NF, 8):
-                    nc.tensor.transpose(t[:, v - NF, :], words[:, 8 * b + v:8 * b + v + 1].to_broadcast([P, P]), ident[:])
-                nc.scalar.copy(out=mu4[:, b].rearrange("p c j -> p (c j)").bitcast(F32).rearrange("p (c v) -> p c v", v=2),
-                               in_=t[:].rearrange("p b n -> p (b n)").unsqueeze(2).to_broadcast([P, (8 - NF) * P, 2]))
+            t = psum.tile([P, 4, P], F32, name="bank", bufs=6)
+            for z, row in enumerate((2, 3, 6, 7)):
+                nc.tensor.transpose(t[:, z, :], mucol[:, row:row + 1].to_broadcast([P, P]), ident[:])
+            nc.scalar.copy(out=mub[:].rearrange("p b c -> p (b c)").bitcast(F32), in_=t[:].rearrange("p z n -> p (z n)"))
 
         def w_sort(k, e):
             wa[k] = stage.tile([P, D, J], BF16, align_bytes=64, name="wa", tag="m", bufs=2)
@@ -99,7 +100,7 @@ def tile_clusternorm1dv3_v_kernel(tc, x, mu, w, g, dx, dw):
 
         def g_sort(u):
             i, c = divmod(u, 4)
-            ga[u] = stage.tile([P, K, P, J], BF16, align_bytes=64, name="ga", bufs=3)
+            ga[u] = stage.tile([P, K, P, J], BF16, align_bytes=64, name="ga", tag="ga", bufs=3)
             interleave(ga[u][:], g_raw[i][:, :, 512 * c:512 * (c + 1)])
 
         def g_quant(u):
@@ -143,13 +144,19 @@ def tile_clusternorm1dv3_v_kernel(tc, x, mu, w, g, dx, dw):
             o = stage.tile([P, D, K], F32, name="o", tag="o", bufs=3)
             step = D // parts
             for lo in range(0, D, step):
-                nc.vector.tensor_copy(out=o[:, lo:lo + step].rearrange("p (q i) k -> p q k i", i=4), in_=m[n][:, lo // 4:(lo + step) // 4])
+                nc.vector.tensor_copy(out=o[:, lo:lo + step].rearrange("p (q i) (c k) -> p q c i k", i=4, k=2),
+                                      in_=m[n][:, lo // 4:(lo + step) // 4].rearrange("p q (c k) i -> p q c i k", k=2))
                 nc.sync.dma_start(out=dxv[i, :, j, K * lo:K * (lo + step)], in_=o[:, lo:lo + step].rearrange("p e k -> p (e k)"))
 
         def xa_tile(h):
-            if h not in xa:
-                xa[h] = stage.tile([P, K, D // 2, J], BF16, align_bytes=64, name="xa", bufs=2)
-            return xa[h]
+            i, b = divmod(h, 2)
+            if i == G - 1:
+                if (i, b) not in xa:
+                    xa[i, b] = stage.tile([P, K, D // 2, J], BF16, align_bytes=64, name="xa", bufs=2)
+                return xa[i, b][:]
+            if i not in xa:
+                xa[i] = stage.tile([P, K, D, J], BF16, align_bytes=64, name="xa", bufs=2)
+            return xa[i][:, :, b * D // 2:(b + 1) * D // 2, :]
 
         def x_fill(*fs):
             for f in fs:
@@ -167,17 +174,22 @@ def tile_clusternorm1dv3_v_kernel(tc, x, mu, w, g, dx, dw):
             nc.scalar.copy(out=xa_tile(h)[:, :, 32 * v:32 * (v + 1), :], in_=xp[f][:].rearrange("p j (e k) -> p k e j", k=K))
 
         def x_sort(h):
-            interleave(xa_tile(h)[:, :, 32 * NFS[h]:, :], x_raw[h][:, :, P * NFS[h]:])
+            interleave(xa_tile(h)[:, :, 32 * NFS[h]:, :], xc[h][:])
 
         def x_sub(h):
-            v = xa[h][:, :, 32 * NFS[h]:, :].rearrange("p k e j -> p e k j")
-            nc.vector.tensor_tensor(out=v, in0=v, in1=mu4[:, h % 2, P * (NFS[h] - NF):].rearrange("p (e k) j -> p e k j", k=K), op=ALU.subtract)
+            xc[h] = stage.tile([P, J, P * (8 - NFS[h])], BF16, align_bytes=64, name="xc", tag="ga", bufs=3)
+            nc.vector.tensor_tensor(out=xc[h][:], in0=x_raw[h][:, :, P * NFS[h]:], in1=mub[:, h % 2, P * (NFS[h] - NF):].unsqueeze(1).to_broadcast([P, J, P * (8 - NFS[h])]), op=ALU.subtract)
 
         def x_quant(h):
             i, b = divmod(h, 2)
-            for k in range(K):
-                nc.vector.quantize_mx(out=xq[:, i, k, b * 256:(b + 1) * 256].bitcast(E4M3), scales=xs[:, i, k, b * 256:(b + 1) * 256],
-                                      in_=xa[h][:, k].rearrange("p e j -> p (e j)"))
+            if i == G - 1:
+                for k in range(K):
+                    nc.vector.quantize_mx(out=xq[:, i, k, b * 256:(b + 1) * 256].bitcast(E4M3), scales=xs[:, i, k, b * 256:(b + 1) * 256],
+                                          in_=xa_tile(h)[:, k].rearrange("p e j -> p (e j)"))
+            elif b == 1:
+                for k in (0, 2):
+                    nc.vector.quantize_mx(out=xq[:, i, k:k + 2].rearrange("p k e -> p (k e)").bitcast(E4M3), scales=xs[:, i, k:k + 2].rearrange("p k e -> p (k e)"),
+                                          in_=xa[i][:, k:k + 2].rearrange("p k e j -> p (k e j)"))
 
         def dw_mm(b):
             c, k = divmod(b, K)
@@ -204,6 +216,7 @@ def tile_clusternorm1dv3_v_kernel(tc, x, mu, w, g, dx, dw):
 
         with tc.manual_schedule():
             nc.sync.dma_start(out=murow[0:16, :], in_=mu.rearrange("(b d) k -> b (d k)", b=16))
+            nc.sync.dma_start(out=muwords[0:8, :], in_=mu.rearrange("(b d) k -> b (d k)", b=8))
             load_w(0)
             load_g(0)
             load_w(1)
@@ -259,11 +272,11 @@ def tile_clusternorm1dv3_v_kernel(tc, x, mu, w, g, dx, dw):
                 if s + LEAD < N:
                     TC(s + LEAD)
                 if xs_:
-                    x_sort(h)
+                    x_sub(h)
                 for q in us[:1]:
                     g_sort(q)
                 if xs_:
-                    x_sub(h)
+                    x_sort(h)
                 if s + LEAD < N:
                     Q(s + LEAD)
                 for z, q in enumerate(bs[:2]):
@@ -279,6 +292,9 @@ def tile_clusternorm1dv3_v_kernel(tc, x, mu, w, g, dx, dw):
                             x_fill(*range(8 * h + 4, 8 * h + NFS[h]))
                 for q in us[:1]:
                     g_quant(q)
+                if 3 in us:
+                    for q in range(8, N):
+                        load_g(q)
                 if s < N:
                     I(s, 2 if s == N - 1 else 1)
                 for q in bs[2:]:
@@ -290,9 +306,6 @@ def tile_clusternorm1dv3_v_kernel(tc, x, mu, w, g, dx, dw):
                         x_exit(8 * h + v)
                 for q in us[1:]:
                     g_quant(q)
-                if 3 in us:
-                    for q in range(8, N):
-                        load_g(q)
             def sort_quant(first, second):
                 g_sort(first)
                 g_sort(second)
@@ -306,13 +319,13 @@ def tile_clusternorm1dv3_v_kernel(tc, x, mu, w, g, dx, dw):
             f = 8 * 5
             x_fill(f, f + 1)
             x_fill(f + 2, f + 3)
+            x_sub(5)
             x_quant(4)
-            x_sort(5)
             C(8, 0)
             x_exit(f)
             x_exit(f + 1)
             x_fill(*range(f + 4, f + NFS[5]))
-            x_sub(5)
+            x_sort(5)
             C(8, 1)
             M(6)
             for v in range(2, NFS[5]):

@@ -96,7 +96,7 @@ def tile_clusternorm1dv3_v_kernel(tc, x, mu, w, g, dx, dw):
             nc.vector.quantize_mx(out=wq[:, k, :].bitcast(E4M3), scales=ws[:, k, :], in_=wa[k][:].rearrange("p e j -> p (e j)"))
 
         def interleave(out, in_):
-            nc.vector.tensor_copy(out=out.rearrange("p k e j -> p e j k"), in_=in_.rearrange("p j (e k) -> p e j k", k=K))
+            nc.vector.tensor_copy(out=out.rearrange("p k e (c j) -> p e c k j", j=2), in_=in_.rearrange("p (c j) (e k) -> p e c k j", j=2, k=K))
 
         def g_sort(u):
             i, c = divmod(u, 4)
@@ -334,71 +334,71 @@ def tile_clusternorm1dv3_v_kernel(tc, x, mu, w, g, dx, dw):
             T(9, 1)
             Q(8)
             x_quant(5)
-            dw_mm(0)
-            dw_mm(1)
             empty(6)
             M(7)
+            dw_mm(0)
+            dw_mm(1)
             g_sort(5)
             I(6)
             g_sort(9)
+            empty(7)
+            M(8)
             dw_out(0, "S")
             dw_out(1, "S")
             dw_mm(2)
             dw_mm(3)
             g_quant(5)
             g_quant(9)
-            empty(7)
             I(7)
-            M(8)
-            dw_out(2, "S")
-            dw_out(3, "S")
+            empty(8)
             dw_mm(4)
             dw_mm(5)
-            TC(9)
-            g_sort(6)
-            g_sort(10)
-            Q(9)
-            empty(8)
+            dw_out(2, "S")
+            dw_out(3, "S")
             dw_mm(6)
             dw_mm(7)
+            TC(9)
+            g_sort(6)
+            I(8)
+            g_sort(10)
+            Q(9)
+            g_quant(6)
+            g_quant(10)
             dw_out(4, "S")
             dw_out(5, "S")
             M(9)
-            g_quant(6)
-            g_quant(10)
-            I(8)
             dw_out(6, "S")
             dw_out(7, "S")
             dw_mm(8)
             dw_mm(9)
-            TC(10)
             g_sort(7)
             g_sort(11)
-            Q(10)
             empty(9)
             dw_mm(10)
             dw_mm(11)
-            dw_out(8, "S")
-            dw_out(9, "S")
-            M(10)
+            TC(10)
+            I(9)
             g_quant(7)
             g_quant(11)
-            I(9)
-            dw_out(10, "V")
-            dw_out(11, "V")
+            Q(10)
+            dw_out(8, "S")
+            dw_out(9, "S")
             dw_mm(12)
             dw_mm(13)
+            dw_out(10, "V")
+            dw_out(11, "V")
+            M(10)
             C(11, 0)
             C(11, 1)
-            Q(11)
-            empty(10)
-            M(11)
             dw_out(12, "V")
             dw_out(13, "V")
             dw_mm(14)
             dw_mm(15)
+            Q(11)
+            empty(10)
+            M(11)
+            dw_out(14, "V")
+            dw_out(15, "V")
             I(10)
             empty(11)
             I(11, 2)
-            dw_out(14, "S")
-            dw_out(15, "S")

@@ -21,7 +21,9 @@ DK = D * K
 N = G * J
 HALF = DK // 2
 NF = 4
-NFS = [4, 4, 5, 4, 5, 5]
+NFS = [4, 5, 4, 5, 4, 5]
+NMM = [2, 2, 2, 2, 2, 1]
+RAW = tuple(range(8))
 
 
 def tile_clusternorm1dv3_v_kernel(tc, x, mu, w, g, dx, dw):
@@ -29,40 +31,37 @@ def tile_clusternorm1dv3_v_kernel(tc, x, mu, w, g, dx, dw):
     xv = x.rearrange("(g p j) d k -> g p j (d k)", p=P, j=J)
     gv = g.rearrange("(g p j) d k -> g p j (d k)", p=P, j=J)
     dxv = dx.rearrange("(g p j) d k -> g p j (d k)", p=P, j=J)
+    dwv = dw.rearrange("k (q t) e -> t q k e", t=4)
 
     with ExitStack() as ctx:
         keep = ctx.enter_context(tc.tile_pool(name="keep", bufs=1))
         stage = ctx.enter_context(tc.tile_pool(name="stage", bufs=2))
         psum = ctx.enter_context(tc.psum_pool(name="psum", bufs=2))
 
+        murow = keep.tile([P, P], BF16)
+        muwords = keep.tile([P, 2 * P], BF16)
         ident = keep.tile([P, P], F32)
-        make_identity(nc, ident[:])
         identb = keep.tile([P, P], BF16)
-        make_identity(nc, identb[:])
+        negb = keep.tile([P, P], BF16)
         gq = keep.tile([P, G, 4, K, P], U32, align_bytes=64)
         gs = keep.tile([P, G, 4, K, P], U8, align_bytes=64)
         xq = keep.tile([P, G, K, D], U32, align_bytes=64)
         xs = keep.tile([P, G, K, D], U8, align_bytes=64)
         wq = keep.tile([P, K, D], U32, align_bytes=64)
         ws = keep.tile([P, K, D], U8, align_bytes=64)
-        murow = keep.tile([P, P], BF16)
-        nc.vector.memset(murow[:], 0.0)
-        muwords = keep.tile([P, 2 * P], BF16)
-        nc.vector.memset(muwords[:], 0.0)
         mucol = keep.tile([P, 8], F32)
         negmu = keep.tile([P, 16], F32)
         mub = keep.tile([P, 2, 4 * P], BF16)
 
-        g_raw, x_raw, w_raw, ga, gd, gdq, gds, acc, m, xa, wa, tr, xp, ow, xc = ({} for i in range(15))
+        g_raw, x_raw, w_raw, ga, gd, gdq, gds, acc, m, xa, wa, tr, xp, ow, mt, o = ({} for i in range(16))
 
         def copier(e):
             return nc.vector.tensor_copy if e == "V" else nc.scalar.copy
 
-        def load_g(n):
-            i, j = divmod(n, J)
-            if j == 0:
-                g_raw[i] = stage.tile([P, J, DK], BF16, name="graw", bufs=2)
-            nc.sync.dma_start(out=g_raw[i][:, j, :], in_=gv[i, :, j, :])
+        def load_g(i, lo, hi):
+            if lo == 0:
+                g_raw[i] = stage.tile([P, J, DK], BF16, name="graw", bufs=3)
+            nc.sync.dma_start(out=g_raw[i][:, lo:hi, :], in_=gv[i, :, lo:hi, :])
 
         def load_x(h):
             i, b = divmod(h, 2)
@@ -74,331 +73,311 @@ def tile_clusternorm1dv3_v_kernel(tc, x, mu, w, g, dx, dw):
                 w_raw[k // 2] = stage.tile([P, 2, J, D], BF16, name="wraw", tag="o", bufs=3)
             nc.sync.dma_start(out=w_raw[k // 2][:, k % 2], in_=w[k].rearrange("(p j) e -> p j e", j=J))
 
-        def mu_columns():
-            t = psum.tile([P, P], BF16, name="bank", bufs=6)
-            nc.tensor.transpose(t[:], murow[:], identb[:])
-            nc.vector.tensor_scalar(out=negmu[:], in0=t[:, 0:16], scalar1=-1.0, scalar2=None, op0=ALU.mult)
-            u = psum.tile([P, P], F32, name="bank", bufs=6)
-            nc.tensor.transpose(u[:], muwords[:].bitcast(F32), ident[:])
-            nc.vector.tensor_copy(out=mucol[:], in_=u[:, 0:8])
+        def load_mu():
+            nc.sync.dma_start(out=murow[0:16, :], in_=mu.rearrange("(b d) k -> b (d k)", b=16))
+            nc.sync.dma_start(out=muwords[0:8, :], in_=mu.rearrange("(b d) k -> b (d k)", b=8))
+
+        def mu_turn():
+            mt[0] = psum.tile([P, P], BF16, name="bank", bufs=8)
+            nc.tensor.transpose(mt[0][:], murow[:], identb[:])
+            mt[1] = psum.tile([P, P], F32, name="bank", bufs=8)
+            nc.tensor.transpose(mt[1][:], muwords[:].bitcast(F32), ident[:])
+
+        def mu_cols():
+            nc.vector.tensor_scalar(out=negmu[:], in0=mt[0][:, 0:16], scalar1=-1.0, scalar2=None, op0=ALU.mult)
+            nc.vector.tensor_copy(out=mucol[:], in_=mt[1][:, 0:8])
 
         def mu_spread():
-            t = psum.tile([P, 4, P], F32, name="bank", bufs=6)
+            mt[2] = psum.tile([P, 4, P], F32, name="bank", bufs=8)
             for z, row in enumerate((2, 3, 6, 7)):
-                nc.tensor.transpose(t[:, z, :], mucol[:, row:row + 1].to_broadcast([P, P]), ident[:])
-            nc.scalar.copy(out=mub[:].rearrange("p b c -> p (b c)").bitcast(F32), in_=t[:].rearrange("p z n -> p (z n)"))
+                nc.tensor.transpose(mt[2][:, z, :], mucol[:, row:row + 1].to_broadcast([P, P]), ident[:])
 
-        def w_sort(k, e):
+        def mu_out(e):
+            copier(e)(out=mub[:].rearrange("p b c -> p (b c)").bitcast(F32), in_=mt[2][:].rearrange("p z n -> p (z n)"))
+
+        def w_sort(k):
             wa[k] = stage.tile([P, D, J], BF16, align_bytes=64, name="wa", tag="m", bufs=2)
-            copier(e)(out=wa[k][:].rearrange("p (c i) j -> p c j i", i=4), in_=w_raw[k // 2][:, k % 2].rearrange("p j (c i) -> p c j i", i=4))
+            nc.vector.tensor_copy(out=wa[k][:].rearrange("p (c i) j -> p c j i", i=4), in_=w_raw[k // 2][:, k % 2].rearrange("p j (c i) -> p c j i", i=4))
 
         def w_quant(k):
             nc.vector.quantize_mx(out=wq[:, k, :].bitcast(E4M3), scales=ws[:, k, :], in_=wa[k][:].rearrange("p e j -> p (e j)"))
 
         def interleave(out, in_):
-            nc.vector.tensor_copy(out=out.rearrange("p k e (c j) -> p e c k j", j=2), in_=in_.rearrange("p (c j) (e k) -> p e c k j", j=2, k=K))
+            nc.vector.tensor_copy(out=out.rearrange("p k e (c j) -> p e c k j", j=2), in_=in_.rearrange("p (c j) e k -> p e c k j", j=2))
 
-        def g_sort(u):
-            i, c = divmod(u, 4)
-            ga[u] = stage.tile([P, K, P, J], BF16, align_bytes=64, name="ga", tag="ga", bufs=3)
-            interleave(ga[u][:], g_raw[i][:, :, 512 * c:512 * (c + 1)])
+        def g_sort(i, t):
+            if i < G - 1:
+                ga[i, t] = stage.tile([P, K, P, J], BF16, align_bytes=64, name="ga", bufs=2)[:]
+            else:
+                if t % 2 == 0:
+                    ga["two", t // 2] = stage.tile([P, 2, K, P, J], BF16, align_bytes=64, name="gb", tag="xa", bufs=2)
+                ga[i, t] = ga["two", t // 2][:, t % 2]
+            interleave(ga[i, t], g_raw[i][:].rearrange("p j (q t k) -> p t j q k", t=4, k=K)[:, t])
 
-        def g_quant(u):
-            i, c = divmod(u, 4)
-            nc.vector.quantize_mx(out=gq[:, i, c].rearrange("p k d -> p (k d)").bitcast(E5M2),
-                                  scales=gs[:, i, c].rearrange("p k d -> p (k d)"),
-                                  in_=ga[u][:].rearrange("p k d j -> p (k d j)"))
+        def g_quant(i, t):
+            nc.vector.quantize_mx(out=gq[:, i, t].rearrange("p k d -> p (k d)").bitcast(E5M2),
+                                  scales=gs[:, i, t].rearrange("p k d -> p (k d)"),
+                                  in_=ga[i, t].rearrange("p k d j -> p (k d j)"))
 
-        def T(n, kk):
-            i, j = divmod(n, J)
-            words = g_raw[i][:].bitcast(F32)
-            tr[n, kk] = psum.tile([P, 4, P], F32, name="tr", bufs=2)
+        def T(u, z):
+            i, r = divmod(u, J)
+            tr[u, z] = psum.tile([P, 4, P], F32, name="bank", bufs=8)
             for t in range(4):
-                nc.tensor.transpose(tr[n, kk][:, t, :], words[:, j, 2 * t + kk:1024:8], ident[:])
+                if u in RAW:
+                    src = g_raw[i][:].bitcast(F32)[:, r, 2 * t + z:1024:8]
+                else:
+                    src = ga[i, t][:, 2 * (r % 2) + z].rearrange("p q j -> p (q j)").bitcast(F32)[:, r // 2:256:2]
+                nc.tensor.transpose(tr[u, z][:, t, :], src, ident[:])
 
-        def C(n, kk):
-            if kk == 0:
-                gd[n] = stage.tile([P, K, P, 4], BF16, align_bytes=64, name="gd", bufs=2)
-            nc.scalar.copy(out=gd[n][:, 2 * kk:2 * kk + 2], in_=tr[n, kk][:].bitcast(BF16).rearrange("q t (m e) -> q e m t", e=2))
+        def C(u, z, e):
+            if z == 0:
+                gd[u] = stage.tile([P, 2, 2, P, 4], BF16, align_bytes=64, name="gd", bufs=2)
+            copier(e)(out=gd[u][:, z], in_=tr[u, z][:].bitcast(BF16).rearrange("q t (m e) -> q e m t", e=2))
 
-        def Q(n):
-            gdq[n] = stage.tile([P, K, P], U32, align_bytes=64, name="gdq", bufs=5)
-            gds[n] = stage.tile([P, K, P], U8, align_bytes=64, name="gds", bufs=5)
-            nc.vector.quantize_mx(out=gdq[n][:].rearrange("p k m -> p (k m)").bitcast(E5M2),
-                                  scales=gds[n][:].rearrange("p k m -> p (k m)"),
-                                  in_=gd[n][:].rearrange("p k m t -> p (k m t)"))
+        def Q(u):
+            gdq[u] = stage.tile([P, 2, 2, P], U32, align_bytes=64, name="gdq", bufs=5)
+            gds[u] = stage.tile([P, 2, 2, P], U8, align_bytes=64, name="gds", bufs=5)
+            nc.vector.quantize_mx(out=gdq[u][:].rearrange("p a b m -> p (a b m)").bitcast(E5M2),
+                                  scales=gds[u][:].rearrange("p a b m -> p (a b m)"),
+                                  in_=gd[u][:].rearrange("p a b m t -> p (a b m t)"))
 
-        def M(n, ks=range(K)):
+        def M(n, *ks):
             for k in ks:
-                acc[n, k] = psum.tile([P, D], F32, name="bank", bufs=6)
-                nc.tensor.matmul_mx(out=acc[n, k][:], lhsT=gdq[n][:, k, :].bitcast(E5M2), lhsT_scale=gds[n][:, k, :],
+                u, a, b = (n, k // 2, k % 2) if n in RAW else (n - n % 2 + k // 2, k % 2, n % 2)
+                acc[n, k] = psum.tile([P, D], F32, name="bank", bufs=8)
+                nc.tensor.matmul_mx(out=acc[n, k][:], lhsT=gdq[u][:, a, b, :].bitcast(E5M2), lhsT_scale=gds[u][:, a, b, :],
                                     rhs=wq[:, k, :].bitcast(E4M3), rhs_scale=ws[:, k, :], start=True, stop=True)
 
-        def E(n, k, e):
+        def E(n, k, lo, hi, e):
             if n not in m:
                 m[n] = stage.tile([P, D // 4, K, 4], F32, align_bytes=64, name="m", tag="m", bufs=2)
-            copier(e)(out=m[n][:, :, k, :], in_=acc[n, k][:].rearrange("p (q i) -> p q i", i=4))
+            copier(e)(out=m[n][:, lo // 4:hi // 4, k, :], in_=acc[n, k][:, lo:hi].rearrange("p (q i) -> p q i", i=4))
 
-        def I(n, parts=1):
+        def I(n, lo, hi, e="V"):
+            if n not in o:
+                o[n] = stage.tile([P, D, K], F32, name="o", tag="o", bufs=3)
+            copier(e)(out=o[n][:, lo:hi].rearrange("p (q i) (c k) -> p q c i k", i=4, k=2),
+                      in_=m[n][:, lo // 4:hi // 4].rearrange("p q (c k) i -> p q c i k", k=2))
+
+        def store_x(n, lo, hi):
             i, j = divmod(n, J)
-            o = stage.tile([P, D, K], F32, name="o", tag="o", bufs=3)
-            step = D // parts
-            for lo in range(0, D, step):
-                nc.vector.tensor_copy(out=o[:, lo:lo + step].rearrange("p (q i) (c k) -> p q c i k", i=4, k=2),
-                                      in_=m[n][:, lo // 4:(lo + step) // 4].rearrange("p q (c k) i -> p q c i k", k=2))
-                nc.sync.dma_start(out=dxv[i, :, j, K * lo:K * (lo + step)], in_=o[:, lo:lo + step].rearrange("p e k -> p (e k)"))
+            nc.sync.dma_start(out=dxv[i, :, j, K * lo:K * hi], in_=o[n][:, lo:hi].rearrange("p e k -> p (e k)"))
 
         def xa_tile(h):
-            i, b = divmod(h, 2)
-            if i == G - 1:
-                if (i, b) not in xa:
-                    xa[i, b] = stage.tile([P, K, D // 2, J], BF16, align_bytes=64, name="xa", bufs=2)
-                return xa[i, b][:]
-            if i not in xa:
-                xa[i] = stage.tile([P, K, D, J], BF16, align_bytes=64, name="xa", bufs=2)
-            return xa[i][:, :, b * D // 2:(b + 1) * D // 2, :]
+            if h not in xa:
+                xa[h] = stage.tile([P, K, D // 2, J], BF16, align_bytes=64, name="xa", tag="xa", bufs=2)
+            return xa[h][:]
 
-        def x_fill(*fs):
-            for f in fs:
-                h, v = divmod(f, 8)
-                xp[f] = psum.tile([P, J, P], F32, name="bank", bufs=6)
-                col = negmu[:, 8 * (h % 2) + v:8 * (h % 2) + v + 1].to_broadcast([P, P])
-                for j in range(J):
-                    nc.tensor.matmul(xp[f][:, j, :], lhsT=col, rhs=ident[:], start=(j == 0), stop=False, is_transpose=True)
-            for f in fs:
-                h, v = divmod(f, 8)
-                nc.tensor.matmul(xp[f][:], lhsT=identb[:], rhs=x_raw[h][:, :, P * v:P * (v + 1)], start=False, stop=True)
+        def x_fill(h, *vs):
+            for v in vs:
+                r = 8 * (h % 2) + v
+                xp[h, v] = psum.tile([P, J, P], F32, name="bank", bufs=8)
+                if v >= NFS[h] - NMM[h]:
+                    nc.tensor.matmul(xp[h, v][:], lhsT=negb[:, r:r + 1].to_broadcast([P, P]), rhs=murow[:].unsqueeze(1).to_broadcast([P, J, P]), start=True, stop=False)
+                else:
+                    for j in range(J):
+                        nc.tensor.matmul(xp[h, v][:, j, :], lhsT=negmu[:, r:r + 1].to_broadcast([P, P]), rhs=ident[:], start=(j == 0), stop=False, is_transpose=True)
+            for v in vs:
+                nc.tensor.matmul(xp[h, v][:], lhsT=identb[:], rhs=x_raw[h][:, :, P * v:P * (v + 1)], start=False, stop=True)
 
-        def x_exit(f):
-            h, v = divmod(f, 8)
-            nc.scalar.copy(out=xa_tile(h)[:, :, 32 * v:32 * (v + 1), :], in_=xp[f][:].rearrange("p j (e k) -> p k e j", k=K))
-
-        def x_sort(h):
-            interleave(xa_tile(h)[:, :, 32 * NFS[h]:, :], xc[h][:])
+        def x_exit(h, v, e):
+            copier(e)(out=xa_tile(h)[:, :, 32 * v:32 * (v + 1), :], in_=xp[h, v][:].rearrange("p j (e k) -> p k e j", k=K))
 
         def x_sub(h):
-            xc[h] = stage.tile([P, J, P * (8 - NFS[h])], BF16, align_bytes=64, name="xc", tag="ga", bufs=3)
-            nc.vector.tensor_tensor(out=xc[h][:], in0=x_raw[h][:, :, P * NFS[h]:], in1=mub[:, h % 2, P * (NFS[h] - NF):].unsqueeze(1).to_broadcast([P, J, P * (8 - NFS[h])]), op=ALU.subtract)
+            part = x_raw[h][:, :, P * NFS[h]:]
+            nc.vector.tensor_tensor(out=part, in0=part, in1=mub[:, h % 2, P * (NFS[h] - NF):].unsqueeze(1).to_broadcast([P, J, P * (8 - NFS[h])]), op=ALU.subtract)
+
+        def x_sort(h):
+            interleave(xa_tile(h)[:, :, 32 * NFS[h]:, :], x_raw[h][:, :, P * NFS[h]:].rearrange("p j (e k) -> p j e k", k=K))
 
         def x_quant(h):
             i, b = divmod(h, 2)
-            if i == G - 1:
-                for k in range(K):
-                    nc.vector.quantize_mx(out=xq[:, i, k, b * 256:(b + 1) * 256].bitcast(E4M3), scales=xs[:, i, k, b * 256:(b + 1) * 256],
-                                          in_=xa_tile(h)[:, k].rearrange("p e j -> p (e j)"))
-            elif b == 1:
-                for k in (0, 2):
-                    nc.vector.quantize_mx(out=xq[:, i, k:k + 2].rearrange("p k e -> p (k e)").bitcast(E4M3), scales=xs[:, i, k:k + 2].rearrange("p k e -> p (k e)"),
-                                          in_=xa[i][:, k:k + 2].rearrange("p k e j -> p (k e j)"))
+            for k in range(K):
+                nc.vector.quantize_mx(out=xq[:, i, k, b * 256:(b + 1) * 256].bitcast(E4M3), scales=xs[:, i, k, b * 256:(b + 1) * 256],
+                                      in_=xa_tile(h)[:, k].rearrange("p e j -> p (e j)"))
 
-        def dw_mm(b):
-            c, k = divmod(b, K)
-            acc["w", b] = psum.tile([P, D], F32, name="bank", bufs=6)
-            for i in range(G):
-                nc.tensor.matmul_mx(out=acc["w", b][:], lhsT=gq[:, i, c, k, :].bitcast(E5M2), lhsT_scale=gs[:, i, c, k, :],
-                                    rhs=xq[:, i, k, :].bitcast(E4M3), rhs_scale=xs[:, i, k, :], start=(i == 0), stop=(i == G - 1))
+        def dw_mm(b, lo, hi):
+            t, k = divmod(b, K)
+            if lo == 0:
+                acc["w", b] = psum.tile([P, D], F32, name="bank", bufs=8)
+            for z in range(lo, hi):
+                i = G - 1 - z
+                nc.tensor.matmul_mx(out=acc["w", b][:], lhsT=gq[:, i, t, k, :].bitcast(E5M2), lhsT_scale=gs[:, i, t, k, :],
+                                    rhs=xq[:, i, k, :].bitcast(E4M3), rhs_scale=xs[:, i, k, :], start=(z == 0), stop=(z == G - 1))
 
         def dw_out(b, e):
-            c, k = divmod(b, K)
-            if k == 0:
-                ow[c] = stage.tile([P, K, D], F32, name="ow", tag="half", bufs=3)
-            copier(e)(out=ow[c][:, k, :], in_=acc["w", b][:])
-            if k % 2 == 1:
-                nc.sync.dma_start(out=dw[k - 1:k + 1, c * P:(c + 1) * P, :].rearrange("k p e -> p k e"), in_=ow[c][:, k - 1:k + 1, :])
+            t, k = divmod(b, K)
+            if t not in ow:
+                ow[t] = stage.tile([P, K, D], F32, name="ow", tag="half", bufs=3)
+            copier(e)(out=ow[t][:, k, :], in_=acc["w", b][:])
 
-        LEAD = 2
+        def store_w(lo, hi):
+            t, k = divmod(lo, K)
+            nc.sync.dma_start(out=dwv[t, :, k:k + hi - lo, :], in_=ow[t][:, k:k + hi - lo, :])
 
-        def TC(n):
-            for kk in range(2):
-                C(n, kk)
-                if n + 1 < N:
-                    T(n + 1, kk)
+        depth = {"bank": 8, "graw": 3, "o": 3, "m": 2, "half": 3, "ga": 2, "gd": 2, "gdq": 5, "xa": 2}
+
+        def unit_of(n, k):
+            return n if n in RAW else n - n % 2 + k // 2
+
+        def touches(step):
+            f, a = step[0], step[1:]
+            if f is load_g:
+                return [], [(("g", a[0], j), ("graw", a[0])) for j in range(a[1], a[2])]
+            if f is load_x:
+                return [], [(("x", a[0]), ("half", "x", a[0]))]
+            if f is load_w:
+                return [], [(("w", a[0]), ("o", "w", a[0] // 2))]
+            if f is load_mu:
+                return [], [(("mu",), None)]
+            if f is mu_turn:
+                return [("mu",)], [(("mt", z), ("bank", "mt", z)) for z in range(2)]
+            if f is mu_cols:
+                return [("mt", 0), ("mt", 1)], [(("mucol",), None)]
+            if f is mu_spread:
+                return [("mucol",)], [(("mt", 2), ("bank", "mt", 2))]
+            if f is mu_out:
+                return [("mt", 2)], [(("mub",), None)]
+            if f is w_sort:
+                return [("w", a[0])], [(("wa", a[0]), ("m", "wa", a[0]))]
+            if f is w_quant:
+                return [("wa", a[0])], [(("wq", a[0]), None)]
+            if f is g_sort:
+                return [("g", a[0], j) for j in range(J)], [(("ga",) + a, ("ga",) + a if a[0] < G - 1 else ("xa", "gb", a[1] // 2))]
+            if f is g_quant:
+                return [("ga",) + a], [(("gq",) + a, None)]
+            if f is T:
+                i, r = divmod(a[0], J)
+                return [("g", i, r)] if a[0] in RAW else [("ga", i, t) for t in range(4)], [(("tr",) + a, ("bank", "tr") + a)]
+            if f is C:
+                return [("tr",) + a[:2]], [(("gd",) + a[:2], ("gd", a[0]))]
+            if f is Q:
+                return [("gd", a[0], z) for z in range(2)], [(("gdq", a[0]), ("gdq", a[0]))]
+            if f is M:
+                return [("gdq", unit_of(a[0], k)) for k in a[1:]] + [("wq", k) for k in a[1:]], [(("acc", a[0], k), ("bank", "acc", a[0], k)) for k in a[1:]]
+            if f is E:
+                return [("acc",) + a[:2]], [(("m", a[0], a[1], c), ("m", a[0])) for c in range(a[2], a[3], P)]
+            if f is I:
+                return [("m", a[0], k, c) for k in range(K) for c in range(a[1], a[2], P)], [(("o", a[0], c), ("o", a[0])) for c in range(a[1], a[2], P)]
+            if f is store_x:
+                return [("o", a[0], c) for c in range(a[1], a[2], P)], []
+            if f is x_fill:
+                return [("x", a[0]), ("mucol",)], [(("xp", a[0], v), ("bank", "xp", a[0], v)) for v in a[1:]]
+            if f is x_exit:
+                return [("xp",) + a[:2]], [(("xa",) + a[:2], ("xa", a[0]))]
+            if f is x_sub:
+                return [("x", a[0]), ("mub",)], [(("xc", a[0]), ("half", "x", a[0]))]
+            if f is x_sort:
+                return [("xc", a[0])], [(("xa", a[0], NFS[a[0]]), ("xa", a[0]))]
+            if f is x_quant:
+                return [("xa", a[0], v) for v in range(min(8, NFS[a[0]] + 1))], [(("xq", a[0]), None)]
+            if f is dw_mm:
+                groups = [G - 1 - z for z in range(a[1], a[2])]
+                return ([("gq", i, a[0] // K) for i in groups] + [("xq", 2 * i + b) for i in groups for b in range(2)] + [("aw", a[0], z) for z in range(a[1])],
+                        [(("aw", a[0], z), ("bank", "aw", a[0])) for z in range(a[1], a[2])])
+            if f is dw_out:
+                return [("aw", a[0], z) for z in range(G)], [(("ow", a[0]), ("half", "ow", a[0] // K))]
+            return [("ow", b) for b in range(a[0], a[1])], []
+
+        def emit(queues):
+            writer, slot, users = {}, {}, {}
+            for q in queues:
+                for step in q:
+                    for piece, s in touches(step)[1]:
+                        writer[piece] = step
+                        slot[piece] = s
+            for q in queues:
+                for step in q:
+                    reads, writes = touches(step)
+                    for piece in reads + [piece for piece, s in writes]:
+                        users.setdefault(slot[piece], []).append(step)
+            done, taken, ring = set(), set(), {tag: [] for tag in depth}
+            at = [0] * len(queues)
+            while any(at[z] < len(q) for z, q in enumerate(queues)):
+                moved = False
+                for z, q in enumerate(queues):
+                    while at[z] < len(q):
+                        step = q[at[z]]
+                        reads, writes = touches(step)
+                        fresh = []
+                        for piece, s in writes:
+                            if s is not None and s not in taken and s not in fresh:
+                                fresh.append(s)
+                        before = [ring[s[0]][len(ring[s[0]]) + y - depth[s[0]]] for y, s in enumerate(fresh) if len(ring[s[0]]) + y >= depth[s[0]]]
+                        if any(writer[piece] not in done for piece in reads) or any(u not in done for s in before for u in users[s]):
+                            break
+                        step[0](*step[1:])
+                        done.add(step)
+                        for s in fresh:
+                            taken.add(s)
+                            ring[s[0]].append(s)
+                        at[z] = at[z] + 1
+                        moved = True
+                assert moved, [q[at[z]][1:] for z, q in enumerate(queues) if at[z] < len(q)]
 
         with tc.manual_schedule():
-            nc.sync.dma_start(out=murow[0:16, :], in_=mu.rearrange("(b d) k -> b (d k)", b=16))
-            nc.sync.dma_start(out=muwords[0:8, :], in_=mu.rearrange("(b d) k -> b (d k)", b=8))
-            load_w(0)
-            load_g(0)
-            load_w(1)
-            load_g(1)
-            load_g(2)
-            load_w(2)
-            load_w(3)
-            load_g(3)
-            load_x(0)
-            load_g(4)
-            load_x(1)
-            for n in range(5, 8):
-                load_g(n)
-            load_x(2)
-            mu_columns()
-            mu_spread()
-            T(0, 0)
-            T(0, 1)
-            w_sort(0, "V")
-            TC(0)
-            w_sort(1, "V")
-            w_quant(0)
-            w_quant(1)
-            TC(1)
-            Q(0)
-            w_sort(2, "V")
-            w_sort(3, "V")
-            for n in range(2, LEAD):
-                TC(n)
-            w_quant(2)
-            w_quant(3)
-            for n in range(1, LEAD):
-                Q(n)
-            chunks = list(range(4)) + [4 * i + c for c in range(4) for i in (1, 2)]
-            u, b = 0, 0
-            for s in range(6):
-                h = s - 1
-                xs_ = 0 <= h < 2 * G
-                us = chunks[u:u + (1 if s < 7 else 2)]
-                u = u + len(us)
-                bs = list(range(b, min(16, b + (4 if s >= 7 else 0))))
-                b = b + len(bs)
-                if s < N:
-                    M(s)
-                if xs_:
-                    x_fill(8 * h, 8 * h + 1)
-                if 0 <= h - 1 < 2 * G:
-                    x_quant(h - 1)
-                    if h + 2 < 2 * G:
-                        load_x(h + 2)
-                for q in bs[:2]:
-                    dw_mm(q)
-                if s + LEAD < N:
-                    TC(s + LEAD)
-                if xs_:
-                    x_sub(h)
-                for q in us[:1]:
-                    g_sort(q)
-                if xs_:
-                    x_sort(h)
-                if s + LEAD < N:
-                    Q(s + LEAD)
-                for z, q in enumerate(bs[:2]):
-                    dw_out(q, "V" if z == 0 else "S")
-                    if z + 2 < len(bs):
-                        dw_mm(bs[z + 2])
-                if s < N:
-                    for k in range(K):
-                        E(s, k, "S")
-                        if xs_ and k == 1:
-                            x_fill(8 * h + 2, 8 * h + 3)
-                        if xs_ and NFS[h] > 4 and k == NFS[h] - 3:
-                            x_fill(*range(8 * h + 4, 8 * h + NFS[h]))
-                for q in us[:1]:
-                    g_quant(q)
-                if 3 in us:
-                    for q in range(8, N):
-                        load_g(q)
-                if s < N:
-                    I(s, 2 if s == N - 1 else 1)
-                for q in bs[2:]:
-                    dw_out(q, "S")
-                for q in us[1:]:
-                    g_sort(q)
-                if xs_:
-                    for v in range(NFS[h]):
-                        x_exit(8 * h + v)
-                for q in us[1:]:
-                    g_quant(q)
-            def sort_quant(first, second):
-                g_sort(first)
-                g_sort(second)
-                g_quant(first)
-                g_quant(second)
+            nc.vector.memset(murow[:], 0.0)
+            nc.vector.memset(muwords[:], 0.0)
+            make_identity(nc, ident[:])
+            make_identity(nc, identb[:])
+            nc.vector.tensor_scalar(out=negb[:], in0=identb[:], scalar1=-1.0, scalar2=None, op0=ALU.mult)
 
-            def empty(n, engines="SSSS"):
-                for k in range(K):
-                    E(n, k, engines[k])
+            def Cs(u, e="S"):
+                return [(C, u, z, e) for z in range(2)]
 
-            f = 8 * 5
-            x_fill(f, f + 1)
-            x_fill(f + 2, f + 3)
-            x_sub(5)
-            x_quant(4)
-            C(8, 0)
-            x_exit(f)
-            x_exit(f + 1)
-            x_fill(*range(f + 4, f + NFS[5]))
-            x_sort(5)
-            C(8, 1)
-            M(6)
-            for v in range(2, NFS[5]):
-                x_exit(f + v)
-            T(9, 0)
-            T(9, 1)
-            Q(8)
-            x_quant(5)
-            empty(6)
-            M(7)
-            dw_mm(0)
-            dw_mm(1)
-            g_sort(5)
-            I(6)
-            g_sort(9)
-            empty(7)
-            M(8)
-            dw_out(0, "S")
-            dw_out(1, "S")
-            dw_mm(2)
-            dw_mm(3)
-            g_quant(5)
-            g_quant(9)
-            I(7)
-            empty(8)
-            dw_mm(4)
-            dw_mm(5)
-            dw_out(2, "S")
-            dw_out(3, "S")
-            dw_mm(6)
-            dw_mm(7)
-            TC(9)
-            g_sort(6)
-            I(8)
-            g_sort(10)
-            Q(9)
-            g_quant(6)
-            g_quant(10)
-            dw_out(4, "S")
-            dw_out(5, "S")
-            M(9)
-            dw_out(6, "S")
-            dw_out(7, "S")
-            dw_mm(8)
-            dw_mm(9)
-            g_sort(7)
-            g_sort(11)
-            empty(9)
-            dw_mm(10)
-            dw_mm(11)
-            TC(10)
-            I(9)
-            g_quant(7)
-            g_quant(11)
-            Q(10)
-            dw_out(8, "S")
-            dw_out(9, "S")
-            dw_mm(12)
-            dw_mm(13)
-            dw_out(10, "V")
-            dw_out(11, "V")
-            M(10)
-            C(11, 0)
-            C(11, 1)
-            dw_out(12, "V")
-            dw_out(13, "V")
-            dw_mm(14)
-            dw_mm(15)
-            Q(11)
-            empty(10)
-            M(11)
-            dw_out(14, "V")
-            dw_out(15, "V")
-            I(10)
-            empty(11)
-            I(11, 2)
+            def Ts(u):
+                return [(T, u, z) for z in range(2)]
+
+            def Es(n):
+                return [(E, n, k, 0, D, "S") for k in range(K)]
+
+            def Xs(h):
+                return [(x_exit, h, v, "S") for v in range(NFS[h])]
+
+            def Fs(h):
+                return [(x_fill, h) + tuple(range(v, min(v + 2, NFS[h]))) for v in range(0, NFS[h], 2)]
+
+            def Ms(n):
+                return [(M, n, 0, 1, 2, 3)]
+
+            def Ws(lo, hi):
+                return [(dw_mm, b, 0, G) for b in range(lo, hi)]
+
+            def xv_(h):
+                return [(x_sub, h), (x_sort, h)]
+
+            def Ds(lo, hi, e="S"):
+                return [(dw_out, b, e) for b in range(lo, hi)]
+
+            def St(n):
+                return [(store_x, n, 0, D)]
+
+            def Sw(lo):
+                return [(store_w, lo, lo + 2)]
+
+            def Iv(n):
+                return [(I, n, 0, D)]
+
+            def Sq(t):
+                return [(g_sort, 1, t), (g_sort, 0, t), (g_quant, 2, t), (g_quant, 1, t), (g_quant, 0, t)]
+
+            dq = [(load_g, 0, 0, 1), (load_w, 0), (load_mu,), (load_g, 0, 1, 2), (load_w, 1), (load_g, 0, 2, 3), (load_w, 2), (load_g, 0, 3, 4), (load_w, 3),
+                  (load_x, 0), (load_x, 1), (load_x, 2), (load_g, 1, 0, 2), (load_x, 3)] + St(0) + [(load_x, 4), (load_g, 1, 2, 4)] + St(1)
+            dq = dq + [(load_x, 5)] + St(2) + [(load_g, 2, 0, 2), (load_g, 2, 2, 4)] + St(3) + St(4) + St(5) + Sw(0) + St(6) + Sw(2) + St(7) + Sw(4) + St(8) + Sw(6) + St(9) + Sw(8) + Sw(10)
+            dq = dq + St(10) + [(store_x, N - 1, 0, 256), (store_x, N - 1, 256, D)] + Sw(12) + Sw(14)
+
+            tq = Ts(0) + [(mu_turn,)] + Ts(1) + [(mu_spread,)] + Ts(2) + Ts(3) + [(M, 0, k) for k in range(K)]
+            sq = Cs(0) + Cs(1) + Cs(2) + Cs(3)
+            sq = sq + Es(0) + Xs(0) + Es(1) + Xs(1) + Xs(2) + Cs(4) + Es(2) + Xs(3) + Cs(5) + Xs(4) + Es(3) + Xs(5)
+            tq = tq + Fs(0) + Ms(1) + Fs(1) + Fs(2) + Ts(4) + Ms(2) + Fs(3) + Ts(5) + Fs(4) + Ms(3) + Fs(5)
+            sq = sq + Cs(6) + Es(4) + Cs(7) + Es(5) + Es(6) + Ds(0, 4) + Cs(8) + Cs(9) + Es(7) + Ds(4, 6) + Es(8) + Es(9) + Cs(10) + Cs(11) + Ds(8, 12) + Es(10)
+            tq = tq + Ts(6) + Ms(4) + Ts(7) + Ms(5) + Ms(6) + Ws(0, 4) + Ts(8) + Ts(9) + Ms(7) + Ws(4, 8) + Ms(8) + Ms(9) + Ts(10) + Ts(11) + Ws(8, 12) + Ms(10) + Ms(11) + [(dw_mm, b, 0, 2) for b in range(12, 16)] + [(dw_mm, b, 2, 3) for b in range(12, 16)]
+            sq = sq + [(E, 11, k, lo, lo + 256, "S") for lo in (0, 256) for k in range(K)] + Ds(12, 13) + Ds(14, 15)
+
+            vq = [(w_sort, 0), (mu_cols,), (w_quant, 0), (w_sort, 1), (Q, 0), (w_quant, 1), (mu_out, "V"), (w_sort, 2), (Q, 1), (w_quant, 2), (w_sort, 3), (Q, 2), (w_quant, 3), (x_sub, 0), (Q, 3)]
+            vq = vq + [(x_sort, 0), (I, 0, 0, D), (x_sub, 1), (x_quant, 0), (x_sort, 1), (I, 1, 0, D), (x_sub, 2), (x_quant, 1), (x_sort, 2), (x_sub, 3), (x_quant, 2), (x_sort, 3), (Q, 4)]
+            vq = vq + [(x_sub, 4), (I, 2, 0, D), (x_sort, 4), (x_quant, 3), (x_sub, 5), (Q, 5), (x_sort, 5), (g_sort, 0, 0), (x_quant, 4), (I, 3, 0, D), (g_sort, 1, 0), (x_quant, 5), (g_quant, 0, 0), (Q, 6), (g_sort, 2, 0), (g_quant, 1, 0)]
+            vq = vq + Iv(4) + [(g_quant, 2, 0), (Q, 7), (g_sort, 2, 1), (g_sort, 2, 2)] + Iv(5) + [(g_sort, 2, 3), (g_sort, 1, 1)] + Iv(6)
+            vq = vq + [(g_sort, 0, 1), (g_quant, 2, 1), (g_quant, 1, 1), (Q, 8), (g_quant, 0, 1), (Q, 9), (g_sort, 1, 2)] + Iv(7) + [(g_sort, 0, 2)] + Ds(6, 8, "V") + Iv(8)
+            vq = vq + [(g_quant, 2, 2), (g_quant, 1, 2), (g_quant, 0, 2)] + Iv(9) + [(Q, 10), (g_sort, 1, 3), (Q, 11), (g_quant, 2, 3), (g_quant, 1, 3), (g_sort, 0, 3)] + Iv(10) + [(I, 11, 0, 256), (g_quant, 0, 3), (I, 11, 256, D)] + Ds(13, 14, "V") + Ds(15, 16, "V")
+            emit([dq, tq, sq, vq])

@@ -20,10 +20,7 @@ G = B // (P * J)
 DK = D * K
 N = G * J
 HALF = DK // 2
-NF = 4
-NFS = [4, 5, 4, 5, 4, 5]
-NMM = [2, 2, 2, 2, 2, 1]
-RAW = tuple(range(8))
+NA = [2, 2, 3]
 
 
 def tile_clusternorm1dv3_v_kernel(tc, x, mu, w, g, dx, dw):
@@ -31,11 +28,12 @@ def tile_clusternorm1dv3_v_kernel(tc, x, mu, w, g, dx, dw):
     xv = x.rearrange("(g p j) d k -> g p j (d k)", p=P, j=J)
     gv = g.rearrange("(g p j) d k -> g p j (d k)", p=P, j=J)
     dxv = dx.rearrange("(g p j) d k -> g p j (d k)", p=P, j=J)
-    dwv = dw.rearrange("k (q t) e -> t q k e", t=4)
+    dwv = dw.rearrange("k (t q) e -> t q k e", t=4)
 
     with ExitStack() as ctx:
         keep = ctx.enter_context(tc.tile_pool(name="keep", bufs=1))
         stage = ctx.enter_context(tc.tile_pool(name="stage", bufs=2))
+        turns = ctx.enter_context(tc.tile_pool(name="turns", bufs=1))
         psum = ctx.enter_context(tc.psum_pool(name="psum", bufs=2))
 
         murow = keep.tile([P, P], BF16)
@@ -43,29 +41,38 @@ def tile_clusternorm1dv3_v_kernel(tc, x, mu, w, g, dx, dw):
         ident = keep.tile([P, P], F32)
         identb = keep.tile([P, P], BF16)
         negb = keep.tile([P, P], BF16)
-        gq = keep.tile([P, G, 4, K, P], U32, align_bytes=64)
-        gs = keep.tile([P, G, 4, K, P], U8, align_bytes=64)
+        gq = keep.tile([P, 4, G, K, P], U32, align_bytes=64)
+        gs = keep.tile([P, 4, G, K, P], U8, align_bytes=64)
         xq = keep.tile([P, G, K, D], U32, align_bytes=64)
         xs = keep.tile([P, G, K, D], U8, align_bytes=64)
         wq = keep.tile([P, K, D], U32, align_bytes=64)
         ws = keep.tile([P, K, D], U8, align_bytes=64)
         mucol = keep.tile([P, 8], F32)
         negmu = keep.tile([P, 16], F32)
-        mub = keep.tile([P, 2, 4 * P], BF16)
+        mub = keep.tile([P, HALF], BF16)
 
         g_raw, x_raw, w_raw, ga, gd, gdq, gds, acc, m, xa, wa, tr, xp, ow, mt, o = ({} for i in range(16))
+
+        ROW = 8192
+        place = {("x", h): (ROW * (h % 5), ROW * (h % 5 + 1)) for h in range(2 * G)}
+        place["g", G - 1] = (ROW, 3 * ROW)
+        for t in range(4):
+            place["ow", t] = (ROW * (3, 4, 0)[t % 3], ROW * (3, 4, 0)[t % 3] + ROW)
 
         def copier(e):
             return nc.vector.tensor_copy if e == "V" else nc.scalar.copy
 
         def load_g(i, lo, hi):
             if lo == 0:
-                g_raw[i] = stage.tile([P, J, DK], BF16, name="graw", bufs=3)
+                if i < G - 1:
+                    g_raw[i] = stage.tile([P, J, DK], BF16, name="graw", bufs=2)
+                else:
+                    g_raw[i] = turns.tile([P, J, DK], BF16, name="g2", offset=place["g", i][0])
             nc.sync.dma_start(out=g_raw[i][:, lo:hi, :], in_=gv[i, :, lo:hi, :])
 
         def load_x(h):
             i, b = divmod(h, 2)
-            x_raw[h] = stage.tile([P, J, HALF], BF16, name="half", tag="half", bufs=3)
+            x_raw[h] = turns.tile([P, J, HALF], BF16, name="x%d" % h, offset=place["x", h][0])
             nc.sync.dma_start(out=x_raw[h][:], in_=xv[i, :, :, b * HALF:(b + 1) * HALF])
 
         def load_w(k):
@@ -89,45 +96,39 @@ def tile_clusternorm1dv3_v_kernel(tc, x, mu, w, g, dx, dw):
 
         def mu_spread():
             mt[2] = psum.tile([P, 4, P], F32, name="bank", bufs=8)
-            for z, row in enumerate((2, 3, 6, 7)):
+            for z, row in enumerate((4, 5, 6, 7)):
                 nc.tensor.transpose(mt[2][:, z, :], mucol[:, row:row + 1].to_broadcast([P, P]), ident[:])
 
         def mu_out(e):
-            copier(e)(out=mub[:].rearrange("p b c -> p (b c)").bitcast(F32), in_=mt[2][:].rearrange("p z n -> p (z n)"))
+            copier(e)(out=mub[:].bitcast(F32), in_=mt[2][:].rearrange("p z n -> p (z n)"))
 
-        def w_sort(k):
-            wa[k] = stage.tile([P, D, J], BF16, align_bytes=64, name="wa", tag="m", bufs=2)
-            nc.vector.tensor_copy(out=wa[k][:].rearrange("p (c i) j -> p c j i", i=4), in_=w_raw[k // 2][:, k % 2].rearrange("p j (c i) -> p c j i", i=4))
+        def w_sort(lo, hi):
+            if lo % 2 == 0:
+                wa[lo // 2] = stage.tile([P, 2, D, J], BF16, align_bytes=64, name="wa", tag="m", bufs=2)
+            a, b = lo % 2, lo % 2 + hi - lo
+            nc.vector.tensor_copy(out=wa[lo // 2][:, a:b].rearrange("p k (c i) j -> p k c j i", i=4), in_=w_raw[lo // 2][:, a:b].rearrange("p k j (c i) -> p k c j i", i=4))
 
-        def w_quant(k):
-            nc.vector.quantize_mx(out=wq[:, k, :].bitcast(E4M3), scales=ws[:, k, :], in_=wa[k][:].rearrange("p e j -> p (e j)"))
+        def w_quant(z):
+            nc.vector.quantize_mx(out=wq[:, 2 * z:2 * z + 2, :].rearrange("p k e -> p (k e)").bitcast(E4M3), scales=ws[:, 2 * z:2 * z + 2, :].rearrange("p k e -> p (k e)"),
+                                  in_=wa[z][:].rearrange("p k e j -> p (k e j)"))
 
         def interleave(out, in_):
             nc.vector.tensor_copy(out=out.rearrange("p k e (c j) -> p e c k j", j=2), in_=in_.rearrange("p (c j) e k -> p e c k j", j=2))
 
-        def g_sort(i, t):
-            if i < G - 1:
-                ga[i, t] = stage.tile([P, K, P, J], BF16, align_bytes=64, name="ga", bufs=2)[:]
-            else:
-                if t % 2 == 0:
-                    ga["two", t // 2] = stage.tile([P, 2, K, P, J], BF16, align_bytes=64, name="gb", tag="xa", bufs=2)
-                ga[i, t] = ga["two", t // 2][:, t % 2]
-            interleave(ga[i, t], g_raw[i][:].rearrange("p j (q t k) -> p t j q k", t=4, k=K)[:, t])
+        def g_sort(i, c):
+            if i == 0:
+                ga[c] = stage.tile([P, G, K, P, J], BF16, align_bytes=64, name="ga", bufs=1)
+            interleave(ga[c][:, i], g_raw[i][:, :, 512 * c:512 * (c + 1)].rearrange("p j (e k) -> p j e k", k=K))
 
-        def g_quant(i, t):
-            nc.vector.quantize_mx(out=gq[:, i, t].rearrange("p k d -> p (k d)").bitcast(E5M2),
-                                  scales=gs[:, i, t].rearrange("p k d -> p (k d)"),
-                                  in_=ga[i, t].rearrange("p k d j -> p (k d j)"))
+        def g_quant(c, lo, hi):
+            nc.vector.quantize_mx(out=gq[:, c, lo:hi].rearrange("p i k d -> p (i k d)").bitcast(E5M2), scales=gs[:, c, lo:hi].rearrange("p i k d -> p (i k d)"),
+                                  in_=ga[c][:, lo:hi].rearrange("p i k d j -> p (i k d j)"))
 
-        def T(u, z):
-            i, r = divmod(u, J)
-            tr[u, z] = psum.tile([P, 4, P], F32, name="bank", bufs=8)
+        def T(n, z):
+            i, j = divmod(n, J)
+            tr[n, z] = psum.tile([P, 4, P], F32, name="bank", bufs=8)
             for t in range(4):
-                if u in RAW:
-                    src = g_raw[i][:].bitcast(F32)[:, r, 2 * t + z:1024:8]
-                else:
-                    src = ga[i, t][:, 2 * (r % 2) + z].rearrange("p q j -> p (q j)").bitcast(F32)[:, r // 2:256:2]
-                nc.tensor.transpose(tr[u, z][:, t, :], src, ident[:])
+                nc.tensor.transpose(tr[n, z][:, t, :], g_raw[i][:].bitcast(F32)[:, j, 2 * t + z:1024:8], ident[:])
 
         def C(u, z, e):
             if z == 0:
@@ -143,7 +144,7 @@ def tile_clusternorm1dv3_v_kernel(tc, x, mu, w, g, dx, dw):
 
         def M(n, *ks):
             for k in ks:
-                u, a, b = (n, k // 2, k % 2) if n in RAW else (n - n % 2 + k // 2, k % 2, n % 2)
+                u, a, b = n, k // 2, k % 2
                 acc[n, k] = psum.tile([P, D], F32, name="bank", bufs=8)
                 nc.tensor.matmul_mx(out=acc[n, k][:], lhsT=gdq[u][:, a, b, :].bitcast(E5M2), lhsT_scale=gds[u][:, a, b, :],
                                     rhs=wq[:, k, :].bitcast(E4M3), rhs_scale=ws[:, k, :], start=True, stop=True)
@@ -163,69 +164,74 @@ def tile_clusternorm1dv3_v_kernel(tc, x, mu, w, g, dx, dw):
             i, j = divmod(n, J)
             nc.sync.dma_start(out=dxv[i, :, j, K * lo:K * hi], in_=o[n][:, lo:hi].rearrange("p e k -> p (e k)"))
 
-        def xa_tile(h):
-            if h not in xa:
-                xa[h] = stage.tile([P, K, D // 2, J], BF16, align_bytes=64, name="xa", tag="xa", bufs=2)
-            return xa[h][:]
+        def xa_tile(i):
+            if i not in xa:
+                xa[i] = stage.tile([P, K, D, J], BF16, align_bytes=64, name="xa", tag="xa", bufs=1)
+            return xa[i][:]
 
-        def x_fill(h, *vs):
+        def a_fill(i, z):
+            xp[i, "a", z] = psum.tile([P, 2, K, 32, J], BF16, name="bank", bufs=8)
+            for y in range(2):
+                v = 2 * z + y
+                part = xp[i, "a", z][:, y]
+                nc.tensor.matmul(part, lhsT=negb[:, v:v + 1].to_broadcast([P, P]), rhs=murow[:].rearrange("p (e k) -> p k e", k=K).unsqueeze(3).to_broadcast([P, K, 32, J]), start=True, stop=False)
+                nc.tensor.matmul(part.rearrange("p k e j -> p j e k"), lhsT=identb[:], rhs=x_raw[2 * i][:, :, P * v:P * (v + 1)].rearrange("p j (e k) -> p j e k", k=K), start=False, stop=True)
+
+        def a_exit(i, z, e):
+            copier(e)(out=xa_tile(i)[:, :, 64 * z:64 * (z + 1), :].rearrange("p k (y e) j -> p k y (e j)", y=2), in_=xp[i, "a", z][:].rearrange("p y k e j -> p k y (e j)"))
+
+        def x_fill(i, *vs):
             for v in vs:
-                r = 8 * (h % 2) + v
-                xp[h, v] = psum.tile([P, J, P], F32, name="bank", bufs=8)
-                if v >= NFS[h] - NMM[h]:
-                    nc.tensor.matmul(xp[h, v][:], lhsT=negb[:, r:r + 1].to_broadcast([P, P]), rhs=murow[:].unsqueeze(1).to_broadcast([P, J, P]), start=True, stop=False)
-                else:
-                    for j in range(J):
-                        nc.tensor.matmul(xp[h, v][:, j, :], lhsT=negmu[:, r:r + 1].to_broadcast([P, P]), rhs=ident[:], start=(j == 0), stop=False, is_transpose=True)
+                xp[i, v] = psum.tile([P, J, P], F32, name="bank", bufs=8)
+                for j in range(J):
+                    nc.tensor.matmul(xp[i, v][:, j, :], lhsT=negmu[:, v:v + 1].to_broadcast([P, P]), rhs=ident[:], start=(j == 0), stop=False, is_transpose=True)
             for v in vs:
-                nc.tensor.matmul(xp[h, v][:], lhsT=identb[:], rhs=x_raw[h][:, :, P * v:P * (v + 1)], start=False, stop=True)
+                nc.tensor.matmul(xp[i, v][:], lhsT=identb[:], rhs=x_raw[2 * i][:, :, P * v:P * (v + 1)], start=False, stop=True)
 
-        def x_exit(h, v, e):
-            copier(e)(out=xa_tile(h)[:, :, 32 * v:32 * (v + 1), :], in_=xp[h, v][:].rearrange("p j (e k) -> p k e j", k=K))
+        def x_exit(i, v, e):
+            copier(e)(out=xa_tile(i)[:, :, 32 * v:32 * (v + 1), :], in_=xp[i, v][:].rearrange("p j (e k) -> p k e j", k=K))
 
-        def x_sub(h):
-            part = x_raw[h][:, :, P * NFS[h]:]
-            nc.vector.tensor_tensor(out=part, in0=part, in1=mub[:, h % 2, P * (NFS[h] - NF):].unsqueeze(1).to_broadcast([P, J, P * (8 - NFS[h])]), op=ALU.subtract)
+        def x_sub(i):
+            part = x_raw[2 * i + 1][:]
+            nc.vector.tensor_tensor(out=part, in0=part, in1=mub[:].unsqueeze(1).to_broadcast([P, J, HALF]), op=ALU.subtract)
 
-        def x_sort(h):
-            interleave(xa_tile(h)[:, :, 32 * NFS[h]:, :], x_raw[h][:, :, P * NFS[h]:].rearrange("p j (e k) -> p j e k", k=K))
+        def x_sort(i):
+            interleave(xa_tile(i)[:, :, D // 2:, :], x_raw[2 * i + 1][:].rearrange("p j (e k) -> p j e k", k=K))
 
-        def x_quant(h):
-            i, b = divmod(h, 2)
-            for k in range(K):
-                nc.vector.quantize_mx(out=xq[:, i, k, b * 256:(b + 1) * 256].bitcast(E4M3), scales=xs[:, i, k, b * 256:(b + 1) * 256],
-                                      in_=xa_tile(h)[:, k].rearrange("p e j -> p (e j)"))
+        def x_quant(i, z):
+            nc.vector.quantize_mx(out=xq[:, i, 2 * z:2 * z + 2].rearrange("p k e -> p (k e)").bitcast(E4M3), scales=xs[:, i, 2 * z:2 * z + 2].rearrange("p k e -> p (k e)"),
+                                  in_=xa_tile(i)[:, 2 * z:2 * z + 2].rearrange("p k e j -> p (k e j)"))
 
         def dw_mm(b, lo, hi):
             t, k = divmod(b, K)
             if lo == 0:
                 acc["w", b] = psum.tile([P, D], F32, name="bank", bufs=8)
             for z in range(lo, hi):
-                i = G - 1 - z
-                nc.tensor.matmul_mx(out=acc["w", b][:], lhsT=gq[:, i, t, k, :].bitcast(E5M2), lhsT_scale=gs[:, i, t, k, :],
+                i = z
+                nc.tensor.matmul_mx(out=acc["w", b][:], lhsT=gq[:, t, i, k, :].bitcast(E5M2), lhsT_scale=gs[:, t, i, k, :],
                                     rhs=xq[:, i, k, :].bitcast(E4M3), rhs_scale=xs[:, i, k, :], start=(z == 0), stop=(z == G - 1))
 
         def dw_out(b, e):
             t, k = divmod(b, K)
             if t not in ow:
-                ow[t] = stage.tile([P, K, D], F32, name="ow", tag="half", bufs=3)
+                ow[t] = turns.tile([P, K, D], F32, name="ow%d" % t, offset=place["ow", t][0])
             copier(e)(out=ow[t][:, k, :], in_=acc["w", b][:])
 
         def store_w(lo, hi):
             t, k = divmod(lo, K)
             nc.sync.dma_start(out=dwv[t, :, k:k + hi - lo, :], in_=ow[t][:, k:k + hi - lo, :])
 
-        depth = {"bank": 8, "graw": 3, "o": 3, "m": 2, "half": 3, "ga": 2, "gd": 2, "gdq": 5, "xa": 2}
+        depth = {"bank": 8, "graw": 2, "o": 3, "m": 2, "ga": 1, "gd": 2, "gdq": 5, "xa": 1}
 
         def unit_of(n, k):
-            return n if n in RAW else n - n % 2 + k // 2
+            return n
 
         def touches(step):
             f, a = step[0], step[1:]
             if f is load_g:
-                return [], [(("g", a[0], j), ("graw", a[0])) for j in range(a[1], a[2])]
+                return [], [(("g", a[0], j), ("graw", a[0]) if a[0] < G - 1 else ("turns", "g", a[0])) for j in range(a[1], a[2])]
             if f is load_x:
-                return [], [(("x", a[0]), ("half", "x", a[0]))]
+                return [], [(("x", a[0]), ("turns", "x", a[0]))]
             if f is load_w:
                 return [], [(("w", a[0]), ("o", "w", a[0] // 2))]
             if f is load_mu:
@@ -239,16 +245,16 @@ def tile_clusternorm1dv3_v_kernel(tc, x, mu, w, g, dx, dw):
             if f is mu_out:
                 return [("mt", 2)], [(("mub",), None)]
             if f is w_sort:
-                return [("w", a[0])], [(("wa", a[0]), ("m", "wa", a[0]))]
+                return [("w", k) for k in range(*a)], [(("wa", k), ("m", "wa", k // 2)) for k in range(*a)]
             if f is w_quant:
-                return [("wa", a[0])], [(("wq", a[0]), None)]
+                return [("wa", 2 * a[0]), ("wa", 2 * a[0] + 1)], [(("wq", 2 * a[0]), None), (("wq", 2 * a[0] + 1), None)]
             if f is g_sort:
-                return [("g", a[0], j) for j in range(J)], [(("ga",) + a, ("ga",) + a if a[0] < G - 1 else ("xa", "gb", a[1] // 2))]
+                return [("g", a[0], j) for j in range(J)], [(("ga",) + a, ("ga", a[1]))]
             if f is g_quant:
-                return [("ga",) + a], [(("gq",) + a, None)]
+                return [("ga", i, a[0]) for i in range(a[1], a[2])], [(("gq", i, a[0]), None) for i in range(a[1], a[2])]
             if f is T:
                 i, r = divmod(a[0], J)
-                return [("g", i, r)] if a[0] in RAW else [("ga", i, t) for t in range(4)], [(("tr",) + a, ("bank", "tr") + a)]
+                return [("g", i, r)], [(("tr",) + a, ("bank", "tr") + a)]
             if f is C:
                 return [("tr",) + a[:2]], [(("gd",) + a[:2], ("gd", a[0]))]
             if f is Q:
@@ -262,21 +268,25 @@ def tile_clusternorm1dv3_v_kernel(tc, x, mu, w, g, dx, dw):
             if f is store_x:
                 return [("o", a[0], c) for c in range(a[1], a[2], P)], []
             if f is x_fill:
-                return [("x", a[0]), ("mucol",)], [(("xp", a[0], v), ("bank", "xp", a[0], v)) for v in a[1:]]
+                return [("x", 2 * a[0]), ("mucol",)], [(("xp", a[0], v), ("bank", "xp", a[0], v)) for v in a[1:]]
+            if f is a_fill:
+                return [("x", 2 * a[0]), ("mu",)], [(("ap",) + a, ("bank", "ap") + a)]
             if f is x_exit:
                 return [("xp",) + a[:2]], [(("xa",) + a[:2], ("xa", a[0]))]
+            if f is a_exit:
+                return [("ap",) + a[:2]], [(("xa", a[0], 2 * a[1] + y), ("xa", a[0])) for y in range(2)]
             if f is x_sub:
-                return [("x", a[0]), ("mub",)], [(("xc", a[0]), ("half", "x", a[0]))]
+                return [("x", 2 * a[0] + 1), ("mub",)], [(("xc", a[0]), ("turns", "x", 2 * a[0] + 1))]
             if f is x_sort:
-                return [("xc", a[0])], [(("xa", a[0], NFS[a[0]]), ("xa", a[0]))]
+                return [("xc", a[0])], [(("xa", a[0], 8), ("xa", a[0]))]
             if f is x_quant:
-                return [("xa", a[0], v) for v in range(min(8, NFS[a[0]] + 1))], [(("xq", a[0]), None)]
+                return [("xa", a[0], v) for v in range(9)], [(("xq", a[0], a[1]), None)]
             if f is dw_mm:
-                groups = [G - 1 - z for z in range(a[1], a[2])]
-                return ([("gq", i, a[0] // K) for i in groups] + [("xq", 2 * i + b) for i in groups for b in range(2)] + [("aw", a[0], z) for z in range(a[1])],
+                groups = [z for z in range(a[1], a[2])]
+                return ([("gq", i, a[0] // K) for i in groups] + [("xq", i, a[0] % K // 2) for i in groups] + [("aw", a[0], z) for z in range(a[1])],
                         [(("aw", a[0], z), ("bank", "aw", a[0])) for z in range(a[1], a[2])])
             if f is dw_out:
-                return [("aw", a[0], z) for z in range(G)], [(("ow", a[0]), ("half", "ow", a[0] // K))]
+                return [("aw", a[0], z) for z in range(G)], [(("ow", a[0]), ("turns", "ow", a[0] // K))]
             return [("ow", b) for b in range(a[0], a[1])], []
 
         def emit(queues):
@@ -291,7 +301,7 @@ def tile_clusternorm1dv3_v_kernel(tc, x, mu, w, g, dx, dw):
                     reads, writes = touches(step)
                     for piece in reads + [piece for piece, s in writes]:
                         users.setdefault(slot[piece], []).append(step)
-            done, taken, ring = set(), set(), {tag: [] for tag in depth}
+            done, taken, ring = set(), set(), {tag: [] for tag in list(depth) + ["turns"]}
             at = [0] * len(queues)
             while any(at[z] < len(q) for z, q in enumerate(queues)):
                 moved = False
@@ -303,7 +313,8 @@ def tile_clusternorm1dv3_v_kernel(tc, x, mu, w, g, dx, dw):
                         for piece, s in writes:
                             if s is not None and s not in taken and s not in fresh:
                                 fresh.append(s)
-                        before = [ring[s[0]][len(ring[s[0]]) + y - depth[s[0]]] for y, s in enumerate(fresh) if len(ring[s[0]]) + y >= depth[s[0]]]
+                        before = [ring[s[0]][len(ring[s[0]]) + y - depth[s[0]]] for y, s in enumerate(fresh) if s[0] in depth and len(ring[s[0]]) + y >= depth[s[0]]]
+                        before = before + [r for s in fresh if s[0] == "turns" for r in ring["turns"] if place[r[1:]][0] < place[s[1:]][1] and place[s[1:]][0] < place[r[1:]][1]]
                         if any(writer[piece] not in done for piece in reads) or any(u not in done for s in before for u in users[s]):
                             break
                         step[0](*step[1:])
@@ -331,20 +342,17 @@ def tile_clusternorm1dv3_v_kernel(tc, x, mu, w, g, dx, dw):
             def Es(n):
                 return [(E, n, k, 0, D, "S") for k in range(K)]
 
-            def Xs(h):
-                return [(x_exit, h, v, "S") for v in range(NFS[h])]
+            def Xs(i):
+                return [(a_exit, i, z, "S") for z in range(NA[i])] + [(x_exit, i, v, "S") for v in range(2 * NA[i], 8)]
 
-            def Fs(h):
-                return [(x_fill, h) + tuple(range(v, min(v + 2, NFS[h]))) for v in range(0, NFS[h], 2)]
+            def Fs(i):
+                return [(a_fill, i, z) for z in range(NA[i])] + [(x_fill, i, v, v + 1) for v in range(2 * NA[i], 8, 2)]
 
             def Ms(n):
                 return [(M, n, 0, 1, 2, 3)]
 
             def Ws(lo, hi):
                 return [(dw_mm, b, 0, G) for b in range(lo, hi)]
-
-            def xv_(h):
-                return [(x_sub, h), (x_sort, h)]
 
             def Ds(lo, hi, e="S"):
                 return [(dw_out, b, e) for b in range(lo, hi)]
@@ -358,26 +366,55 @@ def tile_clusternorm1dv3_v_kernel(tc, x, mu, w, g, dx, dw):
             def Iv(n):
                 return [(I, n, 0, D)]
 
-            def Sq(t):
-                return [(g_sort, 1, t), (g_sort, 0, t), (g_quant, 2, t), (g_quant, 1, t), (g_quant, 0, t)]
+            def weave(a, b):
+                out = []
+                for z in range(max(len(a), len(b))):
+                    out = out + a[z:z + 1] + b[z:z + 1]
+                return out
 
-            dq = [(load_g, 0, 0, 1), (load_w, 0), (load_mu,), (load_g, 0, 1, 2), (load_w, 1), (load_g, 0, 2, 3), (load_w, 2), (load_g, 0, 3, 4), (load_w, 3),
-                  (load_x, 0), (load_x, 1), (load_x, 2), (load_g, 1, 0, 2), (load_x, 3)] + St(0) + [(load_x, 4), (load_g, 1, 2, 4)] + St(1)
-            dq = dq + [(load_x, 5)] + St(2) + [(load_g, 2, 0, 2), (load_g, 2, 2, 4)] + St(3) + St(4) + St(5) + Sw(0) + St(6) + Sw(2) + St(7) + Sw(4) + St(8) + Sw(6) + St(9) + Sw(8) + Sw(10)
-            dq = dq + St(10) + [(store_x, N - 1, 0, 256), (store_x, N - 1, 256, D)] + Sw(12) + Sw(14)
+            def M1(n):
+                return [(M, n, k) for k in range(K)]
 
-            tq = Ts(0) + [(mu_turn,)] + Ts(1) + [(mu_spread,)] + Ts(2) + Ts(3) + [(M, 0, k) for k in range(K)]
+            def S3(c):
+                return [(g_sort, i, c) for i in range(G)]
+
+            dq = [(load_g, 0, 0, 1), (load_mu,), (load_w, 0), (load_g, 0, 1, 2), (load_w, 1), (load_g, 0, 2, 3), (load_w, 2), (load_g, 0, 3, 4), (load_w, 3),
+                  (load_x, 0), (load_x, 1), (load_g, 1, 0, 2), (load_x, 2), (load_x, 3)] + St(0) + [(load_g, 1, 2, 4), (load_x, 4)] + St(1)
+            dq = dq + [(load_x, 5)] + St(2) + [(load_g, 2, 0, 2), (load_g, 2, 2, 4)] + St(3) + St(4) + St(5)
+            NW = {5: 0, 6: 2, 7: 3, 8: 3, 9: 4, 10: 0, 11: 4}
+            ONV = (14, 15)
+            first = {n: sum(NW[z] for z in range(5, n)) for n in range(5, N + 1)}
+            for n in range(6, N - 1):
+                ws_ = [(store_w, b - 1, b + 1) for b in range(first[n], first[n + 1]) if b % 2 == 1]
+                dq = dq + ws_[:1] + St(n) + ws_[1:]
+            dq = dq + Sw(12) + Sw(14) + [(store_x, N - 1, 0, 256), (store_x, N - 1, 256, D)]
+
+            tq = Ts(0)[:1] + [(mu_turn,)] + Ts(0)[1:] + [(mu_spread,)] + Ts(1) + Ts(2) + Ts(3)
             sq = Cs(0) + Cs(1) + Cs(2) + Cs(3)
-            sq = sq + Es(0) + Xs(0) + Es(1) + Xs(1) + Xs(2) + Cs(4) + Es(2) + Xs(3) + Cs(5) + Xs(4) + Es(3) + Xs(5)
-            tq = tq + Fs(0) + Ms(1) + Fs(1) + Fs(2) + Ts(4) + Ms(2) + Fs(3) + Ts(5) + Fs(4) + Ms(3) + Fs(5)
-            sq = sq + Cs(6) + Es(4) + Cs(7) + Es(5) + Es(6) + Ds(0, 4) + Cs(8) + Cs(9) + Es(7) + Ds(4, 6) + Es(8) + Es(9) + Cs(10) + Cs(11) + Ds(8, 12) + Es(10)
-            tq = tq + Ts(6) + Ms(4) + Ts(7) + Ms(5) + Ms(6) + Ws(0, 4) + Ts(8) + Ts(9) + Ms(7) + Ws(4, 8) + Ms(8) + Ms(9) + Ts(10) + Ts(11) + Ws(8, 12) + Ms(10) + Ms(11) + [(dw_mm, b, 0, 2) for b in range(12, 16)] + [(dw_mm, b, 2, 3) for b in range(12, 16)]
-            sq = sq + [(E, 11, k, lo, lo + 256, "S") for lo in (0, 256) for k in range(K)] + Ds(12, 13) + Ds(14, 15)
+            XA, XB = [Xs(i)[:NA[i]] for i in range(G)], [Xs(i)[NA[i]:] for i in range(G)]
+            FA, FB = [Fs(i)[:NA[i]] for i in range(G)], [Fs(i)[NA[i]:] for i in range(G)]
+            sq = sq + Es(0)[:2] + XA[0][:1] + Es(0)[2:] + XB[0][:2] + Es(1)[:2] + XA[0][1:] + Es(1)[2:] + XB[0][2:] + Cs(4)
+            tq = tq + [(M, 0, 0, 1)] + FA[0][:1] + [(M, 0, 2, 3)] + FB[0][:1] + [(M, 1, 0, 1)] + FA[0][1:] + [(M, 1, 2, 3)] + FB[0][1:] + Ts(4)
+            sq = sq + Es(2)[:2] + XA[1][:1] + Es(2)[2:] + XA[1][1:] + XB[1] + Cs(5) + Es(3) + Cs(6) + weave(Es(4), XA[2]) + XB[2]
+            tq = tq + [(M, 2, 0, 1)] + FA[1][:1] + [(M, 2, 2, 3)] + FA[1][1:] + FB[1] + Ts(5) + Ms(3) + Ts(6) + weave(M1(4), FA[2]) + FB[2]
+            for n in range(5, N):
+                ds = [(dw_out, b, "S") for b in range(first[n], first[n + 1]) if b not in ONV]
+                if n + 2 < N - 1:
+                    sq = sq + Cs(n + 2)
+                    tq = tq + Ts(n + 2)
+                if n < N - 1:
+                    sq = sq + Es(n)[:2] + weave(Es(n)[2:], ds)
+                    tq = tq + M1(n)[:2] + weave(M1(n)[2:], Ws(first[n], first[n + 1]))
+                    if n == N - 2:
+                        sq = sq + Cs(N - 1)
+                        tq = tq + Ts(N - 1)
+                else:
+                    sq = sq + ds + [(E, n, k, lo, lo + 256, "S") for lo in (0, 256) for k in range(K)]
+                    tq = tq + [(dw_mm, b, 0, 2) for b in range(12, 16)] + [(dw_mm, b, 2, 3) for b in range(12, 16)] + Ms(n)
 
-            vq = [(w_sort, 0), (mu_cols,), (w_quant, 0), (w_sort, 1), (Q, 0), (w_quant, 1), (mu_out, "V"), (w_sort, 2), (Q, 1), (w_quant, 2), (w_sort, 3), (Q, 2), (w_quant, 3), (x_sub, 0), (Q, 3)]
-            vq = vq + [(x_sort, 0), (I, 0, 0, D), (x_sub, 1), (x_quant, 0), (x_sort, 1), (I, 1, 0, D), (x_sub, 2), (x_quant, 1), (x_sort, 2), (x_sub, 3), (x_quant, 2), (x_sort, 3), (Q, 4)]
-            vq = vq + [(x_sub, 4), (I, 2, 0, D), (x_sort, 4), (x_quant, 3), (x_sub, 5), (Q, 5), (x_sort, 5), (g_sort, 0, 0), (x_quant, 4), (I, 3, 0, D), (g_sort, 1, 0), (x_quant, 5), (g_quant, 0, 0), (Q, 6), (g_sort, 2, 0), (g_quant, 1, 0)]
-            vq = vq + Iv(4) + [(g_quant, 2, 0), (Q, 7), (g_sort, 2, 1), (g_sort, 2, 2)] + Iv(5) + [(g_sort, 2, 3), (g_sort, 1, 1)] + Iv(6)
-            vq = vq + [(g_sort, 0, 1), (g_quant, 2, 1), (g_quant, 1, 1), (Q, 8), (g_quant, 0, 1), (Q, 9), (g_sort, 1, 2)] + Iv(7) + [(g_sort, 0, 2)] + Ds(6, 8, "V") + Iv(8)
-            vq = vq + [(g_quant, 2, 2), (g_quant, 1, 2), (g_quant, 0, 2)] + Iv(9) + [(Q, 10), (g_sort, 1, 3), (Q, 11), (g_quant, 2, 3), (g_quant, 1, 3), (g_sort, 0, 3)] + Iv(10) + [(I, 11, 0, 256), (g_quant, 0, 3), (I, 11, 256, D)] + Ds(13, 14, "V") + Ds(15, 16, "V")
+            vq = [(mu_cols,), (w_sort, 0, 1), (mu_out, "V"), (w_sort, 1, 2), (Q, 0), (w_quant, 0), (Q, 1), (w_sort, 2, 3), (w_sort, 3, 4), (Q, 2), (w_quant, 1), (g_sort, 0, 0), (Q, 3), (x_sub, 0)]
+            vq = vq + Iv(0) + [(x_sort, 0), (g_quant, 0, 0, 1), (x_quant, 0, 0), (x_quant, 0, 1)] + Iv(1) + [(x_sub, 1), (Q, 4), (x_sort, 1)] + Iv(2) + [(x_quant, 1, 0), (x_quant, 1, 1), (x_sub, 2), (Q, 5), (x_sort, 2)]
+            vq = vq + Iv(3) + [(Q, 6), (g_sort, 1, 0), (g_sort, 2, 0)] + Iv(4) + [(x_quant, 2, 0), (x_quant, 2, 1), (g_quant, 0, 1, 3), (Q, 7)] + S3(1)[:2] + Iv(5)
+            vq = vq + [(g_quant, 1, 0, 2), (Q, 8)] + S3(1)[2:] + Iv(6) + [(g_quant, 1, 2, 3), (Q, 9)] + S3(2)[:2] + Iv(7) + S3(2)[2:] + [(g_quant, 2, 0, 2), (Q, 10), (g_quant, 2, 2, 3)] + Iv(8)
+            vq = vq + S3(3)[:2] + Iv(9) + [(g_quant, 3, 0, 2)] + S3(3)[2:] + Iv(10) + [(g_quant, 3, 2, 3), (Q, 11)] + Ds(14, 16, "V") + [(I, 11, 0, 256), (I, 11, 256, D)]
             emit([dq, tq, sq, vq])

@@ -178,7 +178,7 @@ def tile_clusternorm1dv3_v_kernel(tc, x, mu, w, g, dx, dw):
                 nc.tensor.matmul(part.rearrange("p k e j -> p j e k"), lhsT=identb[:], rhs=x_raw[2 * i][:, :, P * v:P * (v + 1)].rearrange("p j (e k) -> p j e k", k=K), start=False, stop=True)
 
         def a_exit(i, z, e):
-            copier(e)(out=xa_tile(i)[:, :, 64 * z:64 * (z + 1), :].rearrange("p k (y e) j -> p k y (e j)", y=2), in_=xp[i, "a", z][:].rearrange("p y k e j -> p k y (e j)"))
+            copier(e)(out=xa_tile(i)[:, :, 64 * z:64 * (z + 1), :].rearrange("p k (y e) j -> p y k e j", y=2), in_=xp[i, "a", z][:])
 
         def x_fill(i, *vs):
             for v in vs:

@@ -59,6 +59,13 @@ def tile_clusternorm1dv3_v_kernel(tc, x, mu, w, g, dx, dw):
         for t in range(4):
             place["ow", t] = (ROW * (3, 4, 0)[t % 3], ROW * (3, 4, 0)[t % 3] + ROW)
 
+        order, seats = [], []
+
+        def bank(shape, dtype):
+            b = seats[len(order)]
+            order.append(b)
+            return psum.tile(shape, dtype, name="bank%d" % b, bufs=1)
+
         def copier(e):
             return nc.vector.tensor_copy if e == "V" else nc.scalar.copy
 
@@ -85,9 +92,9 @@ def tile_clusternorm1dv3_v_kernel(tc, x, mu, w, g, dx, dw):
             nc.sync.dma_start(out=muwords[0:8, :], in_=mu.rearrange("(b d) k -> b (d k)", b=8))
 
         def mu_turn():
-            mt[0] = psum.tile([P, P], BF16, name="bank", bufs=8)
+            mt[0] = bank([P, P], BF16)
             nc.tensor.transpose(mt[0][:], murow[:], identb[:])
-            mt[1] = psum.tile([P, P], F32, name="bank", bufs=8)
+            mt[1] = bank([P, P], F32)
             nc.tensor.transpose(mt[1][:], muwords[:].bitcast(F32), ident[:])
 
         def mu_cols():
@@ -95,7 +102,7 @@ def tile_clusternorm1dv3_v_kernel(tc, x, mu, w, g, dx, dw):
             nc.vector.tensor_copy(out=mucol[:], in_=mt[1][:, 0:8])
 
         def mu_spread():
-            mt[2] = psum.tile([P, 4, P], F32, name="bank", bufs=8)
+            mt[2] = bank([P, 4, P], F32)
             for z, row in enumerate((4, 5, 6, 7)):
                 nc.tensor.transpose(mt[2][:, z, :], mucol[:, row:row + 1].to_broadcast([P, P]), ident[:])
 
@@ -126,7 +133,7 @@ def tile_clusternorm1dv3_v_kernel(tc, x, mu, w, g, dx, dw):
 
         def T(n, z):
             i, j = divmod(n, J)
-            tr[n, z] = psum.tile([P, 4, P], F32, name="bank", bufs=8)
+            tr[n, z] = bank([P, 4, P], F32)
             for t in range(4):
                 nc.tensor.transpose(tr[n, z][:, t, :], g_raw[i][:].bitcast(F32)[:, j, 2 * t + z:1024:8], ident[:])
 
@@ -145,7 +152,7 @@ def tile_clusternorm1dv3_v_kernel(tc, x, mu, w, g, dx, dw):
         def M(n, *ks):
             for k in ks:
                 u, a, b = n, k // 2, k % 2
-                acc[n, k] = psum.tile([P, D], F32, name="bank", bufs=8)
+                acc[n, k] = bank([P, D], F32)
                 nc.tensor.matmul_mx(out=acc[n, k][:], lhsT=gdq[u][:, a, b, :].bitcast(E5M2), lhsT_scale=gds[u][:, a, b, :],
                                     rhs=wq[:, k, :].bitcast(E4M3), rhs_scale=ws[:, k, :], start=True, stop=True)
 
@@ -170,19 +177,19 @@ def tile_clusternorm1dv3_v_kernel(tc, x, mu, w, g, dx, dw):
             return xa[i][:]
 
         def a_fill(i, z):
-            xp[i, "a", z] = psum.tile([P, 2, K, 32, J], BF16, name="bank", bufs=8)
+            xp[i, "a", z] = bank([P, 2, K, 32, J], BF16)
             for y in range(2):
                 v = 2 * z + y
                 part = xp[i, "a", z][:, y]
-                nc.tensor.matmul(part, lhsT=negb[:, v:v + 1].to_broadcast([P, P]), rhs=murow[:].rearrange("p (e k) -> p k e", k=K).unsqueeze(3).to_broadcast([P, K, 32, J]), start=True, stop=False)
-                nc.tensor.matmul(part.rearrange("p k e j -> p j e k"), lhsT=identb[:], rhs=x_raw[2 * i][:, :, P * v:P * (v + 1)].rearrange("p j (e k) -> p j e k", k=K), start=False, stop=True)
+                nc.tensor.matmul(part.rearrange("p k e j -> p j e k"), lhsT=identb[:], rhs=x_raw[2 * i][:, :, P * v:P * (v + 1)].rearrange("p j (e k) -> p j e k", k=K), start=True, stop=False)
+                nc.tensor.matmul(part, lhsT=negb[:, v:v + 1].to_broadcast([P, P]), rhs=murow[:].rearrange("p (e k) -> p k e", k=K).unsqueeze(3).to_broadcast([P, K, 32, J]), start=False, stop=True)
 
         def a_exit(i, z, e):
             copier(e)(out=xa_tile(i)[:, :, 64 * z:64 * (z + 1), :].rearrange("p k (y e) j -> p y k e j", y=2), in_=xp[i, "a", z][:])
 
         def x_fill(i, *vs):
             for v in vs:
-                xp[i, v] = psum.tile([P, J, P], F32, name="bank", bufs=8)
+                xp[i, v] = bank([P, J, P], F32)
                 for j in range(J):
                     nc.tensor.matmul(xp[i, v][:, j, :], lhsT=negmu[:, v:v + 1].to_broadcast([P, P]), rhs=ident[:], start=(j == 0), stop=False, is_transpose=True)
             for v in vs:
@@ -205,7 +212,7 @@ def tile_clusternorm1dv3_v_kernel(tc, x, mu, w, g, dx, dw):
         def dw_mm(b, lo, hi):
             t, k = divmod(b, K)
             if lo == 0:
-                acc["w", b] = psum.tile([P, D], F32, name="bank", bufs=8)
+                acc["w", b] = bank([P, D], F32)
             for z in range(lo, hi):
                 i = z
                 nc.tensor.matmul_mx(out=acc["w", b][:], lhsT=gq[:, t, i, k, :].bitcast(E5M2), lhsT_scale=gs[:, t, i, k, :],
@@ -221,7 +228,7 @@ def tile_clusternorm1dv3_v_kernel(tc, x, mu, w, g, dx, dw):
             t, k = divmod(lo, K)
             nc.sync.dma_start(out=dwv[t, :, k:k + hi - lo, :], in_=ow[t][:, k:k + hi - lo, :])
 
-        depth = {"bank": 8, "graw": 2, "o": 3, "m": 2, "ga": 1, "gd": 2, "gdq": 5, "xa": 1}
+        depth = {"graw": 2, "o": 3, "m": 2, "ga": 1, "gd": 2, "gdq": 5, "xa": 1}
 
         def unit_of(n, k):
             return n
@@ -301,7 +308,20 @@ def tile_clusternorm1dv3_v_kernel(tc, x, mu, w, g, dx, dw):
                     reads, writes = touches(step)
                     for piece in reads + [piece for piece, s in writes]:
                         users.setdefault(slot[piece], []).append(step)
-            done, taken, ring = set(), set(), {tag: [] for tag in list(depth) + ["turns"]}
+            halves = [step for step in queues[1] if step[0] is a_fill]
+            recent, holder, seat_before = list(range(8)), {}, {}
+            for step in queues[1]:
+                for piece, s in touches(step)[1]:
+                    if s not in seat_before:
+                        free = [b for b in recent if (b >= 6) == (step[0] is a_fill) or not halves]
+                        recent.remove(free[0])
+                        recent.append(free[0])
+                        seats.append(free[0])
+                        seat_before[s] = [holder[free[0]]] if free[0] in holder else []
+                        holder[free[0]] = s
+                if step in halves:
+                    halves.remove(step)
+            done, taken, ring = set(), set(), {tag: [] for tag in list(depth) + ["turns", "bank"]}
             at = [0] * len(queues)
             while any(at[z] < len(q) for z, q in enumerate(queues)):
                 moved = False
@@ -314,6 +334,7 @@ def tile_clusternorm1dv3_v_kernel(tc, x, mu, w, g, dx, dw):
                             if s is not None and s not in taken and s not in fresh:
                                 fresh.append(s)
                         before = [ring[s[0]][len(ring[s[0]]) + y - depth[s[0]]] for y, s in enumerate(fresh) if s[0] in depth and len(ring[s[0]]) + y >= depth[s[0]]]
+                        before = before + [r for s in fresh for r in seat_before.get(s, [])]
                         before = before + [r for s in fresh if s[0] == "turns" for r in ring["turns"] if place[r[1:]][0] < place[s[1:]][1] and place[s[1:]][0] < place[r[1:]][1]]
                         if any(writer[piece] not in done for piece in reads) or any(u not in done for s in before for u in users[s]):
                             break

@@ -20,7 +20,8 @@ G = B // (P * J)
 DK = D * K
 N = G * J
 HALF = DK // 2
-NA = [2, 2, 3]
+NA = [2, 2, 2]
+NS = [9, 9, 8]
 
 
 def tile_clusternorm1dv3_v_kernel(tc, x, mu, w, g, dx, dw):
@@ -53,11 +54,11 @@ def tile_clusternorm1dv3_v_kernel(tc, x, mu, w, g, dx, dw):
 
         g_raw, x_raw, w_raw, ga, gd, gdq, gds, acc, m, xa, wa, tr, xp, ow, mt, o = ({} for i in range(16))
 
-        ROW = 8192
-        place = {("x", h): (ROW * (h % 5), ROW * (h % 5 + 1)) for h in range(2 * G)}
-        place["g", G - 1] = (ROW, 3 * ROW)
+        KB = 1024
+        place = {("x", 0): (0, 9 * KB), ("x", 1): (9 * KB, 16 * KB), ("x", 2): (16 * KB, 25 * KB), ("x", 3): (25 * KB, 32 * KB), ("x", 4): (32 * KB, 41 * KB), ("x", 5): (0, 8 * KB)}
+        place["g", G - 1] = (9 * KB, 25 * KB)
         for t in range(4):
-            place["ow", t] = (ROW * (3, 4, 0)[t % 3], ROW * (3, 4, 0)[t % 3] + ROW)
+            place["ow", t] = ((25 * KB, 33 * KB), (33 * KB, 41 * KB), (0, 8 * KB))[t % 3]
 
         order, seats = [], []
 
@@ -79,8 +80,9 @@ def tile_clusternorm1dv3_v_kernel(tc, x, mu, w, g, dx, dw):
 
         def load_x(h):
             i, b = divmod(h, 2)
-            x_raw[h] = turns.tile([P, J, HALF], BF16, name="x%d" % h, offset=place["x", h][0])
-            nc.sync.dma_start(out=x_raw[h][:], in_=xv[i, :, :, b * HALF:(b + 1) * HALF])
+            lo, hi = ((0, P * NS[i]), (P * NS[i], DK))[b]
+            x_raw[h] = turns.tile([P, J, hi - lo], BF16, name="x%d" % h, offset=place["x", h][0])
+            nc.sync.dma_start(out=x_raw[h][:], in_=xv[i, :, :, lo:hi])
 
         def load_w(k):
             if k % 2 == 0:
@@ -109,23 +111,23 @@ def tile_clusternorm1dv3_v_kernel(tc, x, mu, w, g, dx, dw):
         def mu_out(e):
             copier(e)(out=mub[:].bitcast(F32), in_=mt[2][:].rearrange("p z n -> p (z n)"))
 
-        def w_sort(lo, hi):
-            if lo % 2 == 0:
+        def w_sort(lo, hi, e="V"):
+            if lo // 2 not in wa:
                 wa[lo // 2] = stage.tile([P, 2, D, J], BF16, align_bytes=64, name="wa", tag="m", bufs=2)
             a, b = lo % 2, lo % 2 + hi - lo
-            nc.vector.tensor_copy(out=wa[lo // 2][:, a:b].rearrange("p k (c i) j -> p k c j i", i=4), in_=w_raw[lo // 2][:, a:b].rearrange("p k j (c i) -> p k c j i", i=4))
+            copier(e)(out=wa[lo // 2][:, a:b].rearrange("p k (c i) j -> p k c j i", i=4), in_=w_raw[lo // 2][:, a:b].rearrange("p k j (c i) -> p k c j i", i=4))
 
         def w_quant(z):
             nc.vector.quantize_mx(out=wq[:, 2 * z:2 * z + 2, :].rearrange("p k e -> p (k e)").bitcast(E4M3), scales=ws[:, 2 * z:2 * z + 2, :].rearrange("p k e -> p (k e)"),
                                   in_=wa[z][:].rearrange("p k e j -> p (k e j)"))
 
-        def interleave(out, in_):
-            nc.vector.tensor_copy(out=out.rearrange("p k e (c j) -> p e c k j", j=2), in_=in_.rearrange("p (c j) e k -> p e c k j", j=2))
+        def interleave(out, in_, e="V"):
+            copier(e)(out=out.rearrange("p k e (c j) -> p e c k j", j=2), in_=in_.rearrange("p (c j) e k -> p e c k j", j=2))
 
-        def g_sort(i, c):
-            if i == 0:
+        def g_sort(i, c, e="V"):
+            if c not in ga:
                 ga[c] = stage.tile([P, G, K, P, J], BF16, align_bytes=64, name="ga", bufs=1)
-            interleave(ga[c][:, i], g_raw[i][:, :, 512 * c:512 * (c + 1)].rearrange("p j (e k) -> p j e k", k=K))
+            interleave(ga[c][:, i], g_raw[i][:, :, 512 * c:512 * (c + 1)].rearrange("p j (e k) -> p j e k", k=K), e)
 
         def g_quant(c, lo, hi):
             nc.vector.quantize_mx(out=gq[:, c, lo:hi].rearrange("p i k d -> p (i k d)").bitcast(E5M2), scales=gs[:, c, lo:hi].rearrange("p i k d -> p (i k d)"),
@@ -200,10 +202,10 @@ def tile_clusternorm1dv3_v_kernel(tc, x, mu, w, g, dx, dw):
 
         def x_sub(i):
             part = x_raw[2 * i + 1][:]
-            nc.vector.tensor_tensor(out=part, in0=part, in1=mub[:].unsqueeze(1).to_broadcast([P, J, HALF]), op=ALU.subtract)
+            nc.vector.tensor_tensor(out=part, in0=part, in1=mub[:, P * NS[i] - HALF:].unsqueeze(1).to_broadcast([P, J, DK - P * NS[i]]), op=ALU.subtract)
 
         def x_sort(i):
-            interleave(xa_tile(i)[:, :, D // 2:, :], x_raw[2 * i + 1][:].rearrange("p j (e k) -> p j e k", k=K))
+            interleave(xa_tile(i)[:, :, 32 * NS[i]:, :], x_raw[2 * i + 1][:].rearrange("p j (e k) -> p j e k", k=K))
 
         def x_quant(i, z):
             nc.vector.quantize_mx(out=xq[:, i, 2 * z:2 * z + 2].rearrange("p k e -> p (k e)").bitcast(E4M3), scales=xs[:, i, 2 * z:2 * z + 2].rearrange("p k e -> p (k e)"),
@@ -252,11 +254,11 @@ def tile_clusternorm1dv3_v_kernel(tc, x, mu, w, g, dx, dw):
             if f is mu_out:
                 return [("mt", 2)], [(("mub",), None)]
             if f is w_sort:
-                return [("w", k) for k in range(*a)], [(("wa", k), ("m", "wa", k // 2)) for k in range(*a)]
+                return [("w", k) for k in range(*a[:2])], [(("wa", k), ("m", "wa", k // 2)) for k in range(*a[:2])]
             if f is w_quant:
                 return [("wa", 2 * a[0]), ("wa", 2 * a[0] + 1)], [(("wq", 2 * a[0]), None), (("wq", 2 * a[0] + 1), None)]
             if f is g_sort:
-                return [("g", a[0], j) for j in range(J)], [(("ga",) + a, ("ga", a[1]))]
+                return [("g", a[0], j) for j in range(J)], [(("ga",) + a[:2], ("ga", a[1]))]
             if f is g_quant:
                 return [("ga", i, a[0]) for i in range(a[1], a[2])], [(("gq", i, a[0]), None) for i in range(a[1], a[2])]
             if f is T:
@@ -277,7 +279,7 @@ def tile_clusternorm1dv3_v_kernel(tc, x, mu, w, g, dx, dw):
             if f is x_fill:
                 return [("x", 2 * a[0]), ("mucol",)], [(("xp", a[0], v), ("bank", "xp", a[0], v)) for v in a[1:]]
             if f is a_fill:
-                return [("x", 2 * a[0]), ("mu",)], [(("ap",) + a, ("bank", "ap") + a)]
+                return [("x", 2 * a[0]), ("mucol",)], [(("ap",) + a, ("bank", "ap") + a)]
             if f is x_exit:
                 return [("xp",) + a[:2]], [(("xa",) + a[:2], ("xa", a[0]))]
             if f is a_exit:
@@ -285,9 +287,9 @@ def tile_clusternorm1dv3_v_kernel(tc, x, mu, w, g, dx, dw):
             if f is x_sub:
                 return [("x", 2 * a[0] + 1), ("mub",)], [(("xc", a[0]), ("turns", "x", 2 * a[0] + 1))]
             if f is x_sort:
-                return [("xc", a[0])], [(("xa", a[0], 8), ("xa", a[0]))]
+                return [("xc", a[0])], [(("xa", a[0], NS[a[0]]), ("xa", a[0]))]
             if f is x_quant:
-                return [("xa", a[0], v) for v in range(9)], [(("xq", a[0], a[1]), None)]
+                return [("xa", a[0], v) for v in range(NS[a[0]] + 1)], [(("xq", a[0], a[1]), None)]
             if f is dw_mm:
                 groups = [z for z in range(a[1], a[2])]
                 return ([("gq", i, a[0] // K) for i in groups] + [("xq", i, a[0] % K // 2) for i in groups] + [("aw", a[0], z) for z in range(a[1])],
@@ -364,10 +366,10 @@ def tile_clusternorm1dv3_v_kernel(tc, x, mu, w, g, dx, dw):
                 return [(E, n, k, 0, D, "S") for k in range(K)]
 
             def Xs(i):
-                return [(a_exit, i, z, "S") for z in range(NA[i])] + [(x_exit, i, v, "S") for v in range(2 * NA[i], 8)]
+                return [(a_exit, i, z, "S") for z in range(NA[i])] + [(x_exit, i, v, "S") for v in range(2 * NA[i], NS[i])]
 
             def Fs(i):
-                return [(a_fill, i, z) for z in range(NA[i])] + [(x_fill, i, v, v + 1) for v in range(2 * NA[i], 8, 2)]
+                return [(a_fill, i, z) for z in range(NA[i])] + [(x_fill, i) + tuple(range(v, min(v + 2, NS[i]))) for v in range(2 * NA[i], NS[i], 2)]
 
             def Ms(n):
                 return [(M, n, 0, 1, 2, 3)]
@@ -416,8 +418,8 @@ def tile_clusternorm1dv3_v_kernel(tc, x, mu, w, g, dx, dw):
             FA, FB = [Fs(i)[:NA[i]] for i in range(G)], [Fs(i)[NA[i]:] for i in range(G)]
             sq = sq + Es(0)[:2] + XA[0][:1] + Es(0)[2:] + XB[0][:2] + Es(1)[:2] + XA[0][1:] + Es(1)[2:] + XB[0][2:] + Cs(4)
             tq = tq + [(M, 0, 0, 1)] + FA[0][:1] + [(M, 0, 2, 3)] + FB[0][:1] + [(M, 1, 0, 1)] + FA[0][1:] + [(M, 1, 2, 3)] + FB[0][1:] + Ts(4)
-            sq = sq + Es(2)[:2] + XA[1][:1] + Es(2)[2:] + XA[1][1:] + XB[1] + Cs(5) + Es(3) + Cs(6) + weave(Es(4), XA[2]) + XB[2]
-            tq = tq + [(M, 2, 0, 1)] + FA[1][:1] + [(M, 2, 2, 3)] + FA[1][1:] + FB[1] + Ts(5) + Ms(3) + Ts(6) + weave(M1(4), FA[2]) + FB[2]
+            sq = sq + Es(2)[:2] + XA[1][:1] + Es(2)[2:] + XA[1][1:] + XB[1] + Cs(5) + Es(3) + Cs(6) + XB[2][:2] + Es(4)[:2] + XA[2][:1] + XB[2][2:] + Es(4)[2:] + XA[2][1:]
+            tq = tq + [(M, 2, 0, 1)] + FA[1][:1] + [(M, 2, 2, 3)] + FA[1][1:] + FB[1] + Ts(5) + Ms(3) + Ts(6) + FB[2][:1] + M1(4)[:2] + FA[2][:1] + FB[2][1:] + M1(4)[2:] + FA[2][1:]
             for n in range(5, N):
                 ds = [(dw_out, b, "S") for b in range(first[n], first[n + 1]) if b not in ONV]
                 if n + 2 < N - 1:

@@ -17,11 +17,16 @@ ALU = mybir.AluOpType
 P = 128
 J = 4
 G = B // (P * J)
-DK = D * K
 N = G * J
+DK = D * K
 HALF = DK // 2
-NA = [2, 2, 2]
-NS = [9, 9, 8]
+KB = 1024
+NARROW = 2
+PLAIN = 38
+WIDE = PLAIN - 2 * 2 * NARROW * G
+UNITS = [2 * NARROW + (WIDE + G - 1 - i) // G for i in range(G)]
+LEAD = 2
+FOUR = 8
 
 
 def tile_clusternorm1dv3_v_kernel(tc, x, mu, w, g, dx, dw):
@@ -29,7 +34,10 @@ def tile_clusternorm1dv3_v_kernel(tc, x, mu, w, g, dx, dw):
     xv = x.rearrange("(g p j) d k -> g p j (d k)", p=P, j=J)
     gv = g.rearrange("(g p j) d k -> g p j (d k)", p=P, j=J)
     dxv = dx.rearrange("(g p j) d k -> g p j (d k)", p=P, j=J)
-    dwv = dw.rearrange("k (t q) e -> t q k e", t=4)
+    dwv = dw.rearrange("k (c q) e -> c q k e", c=4)
+    mu_units = mu.rearrange("(u e) k -> u (e k)", u=DK // P)
+    mu_pairs = mu.rearrange("(u e) k -> u (e k)", u=DK // (2 * P))
+    rows = max(UNITS)
 
     with ExitStack() as ctx:
         keep = ctx.enter_context(tc.tile_pool(name="keep", bufs=1))
@@ -48,24 +56,26 @@ def tile_clusternorm1dv3_v_kernel(tc, x, mu, w, g, dx, dw):
         xs = keep.tile([P, G, K, D], U8, align_bytes=64)
         wq = keep.tile([P, K, D], U32, align_bytes=64)
         ws = keep.tile([P, K, D], U8, align_bytes=64)
-        mucol = keep.tile([P, 8], F32)
-        negmu = keep.tile([P, 16], F32)
+        mucol = keep.tile([P, 4], F32)
+        negmu = keep.tile([P, rows - 2 * NARROW], F32)
         mub = keep.tile([P, HALF], BF16)
 
         g_raw, x_raw, w_raw, ga, gd, gdq, gds, acc, m, xa, wa, tr, xp, ow, mt, o = ({} for i in range(16))
 
-        KB = 1024
-        place = {("x", 0): (0, 9 * KB), ("x", 1): (9 * KB, 16 * KB), ("x", 2): (16 * KB, 25 * KB), ("x", 3): (25 * KB, 32 * KB), ("x", 4): (32 * KB, 41 * KB), ("x", 5): (0, 8 * KB)}
-        place["g", G - 1] = (9 * KB, 25 * KB)
-        for t in range(4):
-            place["ow", t] = ((25 * KB, 33 * KB), (33 * KB, 41 * KB), (0, 8 * KB))[t % 3]
+        size = [KB * (UNITS[h // 2] if h % 2 == 0 else DK // P - UNITS[h // 2]) for h in range(2 * G)]
+        place = {("x", h): (sum(size[:h]), sum(size[:h + 1])) for h in range(2 * G - 1)}
+        place["x", 2 * G - 1] = (0, size[-1])
+        place["g", G - 1] = (size[0], size[0] + 16 * KB)
+        for c in range(4):
+            at = (sum(size[:3]), sum(size[:3]) + 8 * KB, 0)[c % 3]
+            place["ow", c] = (at, at + 8 * KB)
+        depth = {"graw": 2, "o": 3, "m": 2, "ga": 1, "gd": 2, "gdq": 5, "xa": 1}
 
-        order, seats = [], []
+        seats, seated = [], []
 
         def bank(shape, dtype):
-            b = seats[len(order)]
-            order.append(b)
-            return psum.tile(shape, dtype, name="bank%d" % b, bufs=1)
+            seated.append(seats[len(seated)])
+            return psum.tile(shape, dtype, name="bank%d" % seated[-1], bufs=1)
 
         def copier(e):
             return nc.vector.tensor_copy if e == "V" else nc.scalar.copy
@@ -73,25 +83,25 @@ def tile_clusternorm1dv3_v_kernel(tc, x, mu, w, g, dx, dw):
         def load_g(i, lo, hi):
             if lo == 0:
                 if i < G - 1:
-                    g_raw[i] = stage.tile([P, J, DK], BF16, name="graw", bufs=2)
+                    g_raw[i] = stage.tile([P, J, DK], BF16, name="graw", bufs=depth["graw"])
                 else:
                     g_raw[i] = turns.tile([P, J, DK], BF16, name="g2", offset=place["g", i][0])
             nc.sync.dma_start(out=g_raw[i][:, lo:hi, :], in_=gv[i, :, lo:hi, :])
 
         def load_x(h):
             i, b = divmod(h, 2)
-            lo, hi = ((0, P * NS[i]), (P * NS[i], DK))[b]
+            lo, hi = ((0, P * UNITS[i]), (P * UNITS[i], DK))[b]
             x_raw[h] = turns.tile([P, J, hi - lo], BF16, name="x%d" % h, offset=place["x", h][0])
             nc.sync.dma_start(out=x_raw[h][:], in_=xv[i, :, :, lo:hi])
 
         def load_w(k):
             if k % 2 == 0:
-                w_raw[k // 2] = stage.tile([P, 2, J, D], BF16, name="wraw", tag="o", bufs=3)
+                w_raw[k // 2] = stage.tile([P, 2, J, D], BF16, name="wraw", tag="o", bufs=depth["o"])
             nc.sync.dma_start(out=w_raw[k // 2][:, k % 2], in_=w[k].rearrange("(p j) e -> p j e", j=J))
 
         def load_mu():
-            nc.sync.dma_start(out=murow[0:16, :], in_=mu.rearrange("(b d) k -> b (d k)", b=16))
-            nc.sync.dma_start(out=muwords[0:8, :], in_=mu.rearrange("(b d) k -> b (d k)", b=8))
+            nc.sync.dma_start(out=murow[0:rows, :], in_=mu_units[0:rows, :])
+            nc.sync.dma_start(out=muwords[0:4, :], in_=mu_pairs[4:8, :])
 
         def mu_turn():
             mt[0] = bank([P, P], BF16)
@@ -100,74 +110,74 @@ def tile_clusternorm1dv3_v_kernel(tc, x, mu, w, g, dx, dw):
             nc.tensor.transpose(mt[1][:], muwords[:].bitcast(F32), ident[:])
 
         def mu_cols():
-            nc.vector.tensor_scalar(out=negmu[:], in0=mt[0][:, 0:16], scalar1=-1.0, scalar2=None, op0=ALU.mult)
-            nc.vector.tensor_copy(out=mucol[:], in_=mt[1][:, 0:8])
+            nc.vector.tensor_scalar(out=negmu[:], in0=mt[0][:, 2 * NARROW:rows], scalar1=-1.0, scalar2=None, op0=ALU.mult)
+            nc.vector.tensor_copy(out=mucol[:], in_=mt[1][:, 0:4])
 
         def mu_spread():
             mt[2] = bank([P, 4, P], F32)
-            for z, row in enumerate((4, 5, 6, 7)):
-                nc.tensor.transpose(mt[2][:, z, :], mucol[:, row:row + 1].to_broadcast([P, P]), ident[:])
+            for z in range(4):
+                nc.tensor.transpose(mt[2][:, z, :], mucol[:, z:z + 1].to_broadcast([P, P]), ident[:])
 
-        def mu_out(e):
-            copier(e)(out=mub[:].bitcast(F32), in_=mt[2][:].rearrange("p z n -> p (z n)"))
+        def mu_out():
+            nc.scalar.copy(out=mub[:].bitcast(F32), in_=mt[2][:].rearrange("p z n -> p (z n)"))
 
-        def w_sort(lo, hi, e="V"):
-            if lo // 2 not in wa:
-                wa[lo // 2] = stage.tile([P, 2, D, J], BF16, align_bytes=64, name="wa", tag="m", bufs=2)
-            a, b = lo % 2, lo % 2 + hi - lo
-            copier(e)(out=wa[lo // 2][:, a:b].rearrange("p k (c i) j -> p k c j i", i=4), in_=w_raw[lo // 2][:, a:b].rearrange("p k j (c i) -> p k c j i", i=4))
+        def quantize(codes, scales, values, dtype):
+            nc.vector.quantize_mx(out=codes.bitcast(dtype), scales=scales, in_=values)
+
+        def w_sort(k):
+            if k % 2 == 0:
+                wa[k // 2] = stage.tile([P, 2, D, J], BF16, align_bytes=64, name="wa", tag="m", bufs=depth["m"])
+            nc.vector.tensor_copy(out=wa[k // 2][:, k % 2:k % 2 + 1].rearrange("p k (c i) j -> p k c j i", i=4),
+                                  in_=w_raw[k // 2][:, k % 2:k % 2 + 1].rearrange("p k j (c i) -> p k c j i", i=4))
 
         def w_quant(z):
-            nc.vector.quantize_mx(out=wq[:, 2 * z:2 * z + 2, :].rearrange("p k e -> p (k e)").bitcast(E4M3), scales=ws[:, 2 * z:2 * z + 2, :].rearrange("p k e -> p (k e)"),
-                                  in_=wa[z][:].rearrange("p k e j -> p (k e j)"))
+            quantize(wq[:, 2 * z:2 * z + 2, :].rearrange("p k e -> p (k e)"), ws[:, 2 * z:2 * z + 2, :].rearrange("p k e -> p (k e)"),
+                     wa[z][:].rearrange("p k e j -> p (k e j)"), E4M3)
 
-        def interleave(out, in_, e="V"):
-            copier(e)(out=out.rearrange("p k e (c j) -> p e c k j", j=2), in_=in_.rearrange("p (c j) e k -> p e c k j", j=2))
+        def interleave(out, in_):
+            nc.vector.tensor_copy(out=out.rearrange("p k e (c j) -> p e c k j", j=2), in_=in_.rearrange("p (c j) e k -> p e c k j", j=2))
 
-        def g_sort(i, c, e="V"):
-            if c not in ga:
-                ga[c] = stage.tile([P, G, K, P, J], BF16, align_bytes=64, name="ga", bufs=1)
-            interleave(ga[c][:, i], g_raw[i][:, :, 512 * c:512 * (c + 1)].rearrange("p j (e k) -> p j e k", k=K), e)
+        def g_sort(i, c):
+            if i == 0:
+                ga[c] = stage.tile([P, G, K, P, J], BF16, align_bytes=64, name="ga", bufs=depth["ga"])
+            interleave(ga[c][:, i], g_raw[i][:, :, 512 * c:512 * (c + 1)].rearrange("p j (e k) -> p j e k", k=K))
 
         def g_quant(c, lo, hi):
-            nc.vector.quantize_mx(out=gq[:, c, lo:hi].rearrange("p i k d -> p (i k d)").bitcast(E5M2), scales=gs[:, c, lo:hi].rearrange("p i k d -> p (i k d)"),
-                                  in_=ga[c][:, lo:hi].rearrange("p i k d j -> p (i k d j)"))
+            quantize(gq[:, c, lo:hi].rearrange("p i k d -> p (i k d)"), gs[:, c, lo:hi].rearrange("p i k d -> p (i k d)"),
+                     ga[c][:, lo:hi].rearrange("p i k d j -> p (i k d j)"), E5M2)
 
-        def T(n, z):
+        def g_turn(n, z):
             i, j = divmod(n, J)
             tr[n, z] = bank([P, 4, P], F32)
             for t in range(4):
-                nc.tensor.transpose(tr[n, z][:, t, :], g_raw[i][:].bitcast(F32)[:, j, 2 * t + z:1024:8], ident[:])
+                nc.tensor.transpose(tr[n, z][:, t, :], g_raw[i][:].bitcast(F32)[:, j, 2 * t + z:DK // 2:8], ident[:])
 
-        def C(u, z, e):
+        def turned_out(n, z):
             if z == 0:
-                gd[u] = stage.tile([P, 2, 2, P, 4], BF16, align_bytes=64, name="gd", bufs=2)
-            copier(e)(out=gd[u][:, z], in_=tr[u, z][:].bitcast(BF16).rearrange("q t (m e) -> q e m t", e=2))
+                gd[n] = stage.tile([P, 2, 2, P, 4], BF16, align_bytes=64, name="gd", bufs=depth["gd"])
+            nc.scalar.copy(out=gd[n][:, z], in_=tr[n, z][:].bitcast(BF16).rearrange("q t (m e) -> q e m t", e=2))
 
-        def Q(u):
-            gdq[u] = stage.tile([P, 2, 2, P], U32, align_bytes=64, name="gdq", bufs=5)
-            gds[u] = stage.tile([P, 2, 2, P], U8, align_bytes=64, name="gds", bufs=5)
-            nc.vector.quantize_mx(out=gdq[u][:].rearrange("p a b m -> p (a b m)").bitcast(E5M2),
-                                  scales=gds[u][:].rearrange("p a b m -> p (a b m)"),
-                                  in_=gd[u][:].rearrange("p a b m t -> p (a b m t)"))
+        def tile_quant(n):
+            gdq[n] = stage.tile([P, K, P], U32, align_bytes=64, name="gdq", bufs=depth["gdq"])
+            gds[n] = stage.tile([P, K, P], U8, align_bytes=64, name="gds", bufs=depth["gdq"])
+            quantize(gdq[n][:].rearrange("p k m -> p (k m)"), gds[n][:].rearrange("p k m -> p (k m)"),
+                     gd[n][:].rearrange("p a b m t -> p (a b m t)"), E5M2)
 
-        def M(n, *ks):
-            for k in ks:
-                u, a, b = n, k // 2, k % 2
-                acc[n, k] = bank([P, D], F32)
-                nc.tensor.matmul_mx(out=acc[n, k][:], lhsT=gdq[u][:, a, b, :].bitcast(E5M2), lhsT_scale=gds[u][:, a, b, :],
-                                    rhs=wq[:, k, :].bitcast(E4M3), rhs_scale=ws[:, k, :], start=True, stop=True)
+        def dx_mm(n, k):
+            acc[n, k] = bank([P, D], F32)
+            nc.tensor.matmul_mx(out=acc[n, k][:], lhsT=gdq[n][:, k, :].bitcast(E5M2), lhsT_scale=gds[n][:, k, :],
+                                rhs=wq[:, k, :].bitcast(E4M3), rhs_scale=ws[:, k, :], start=True, stop=True)
 
-        def E(n, k, lo, hi, e):
+        def dx_out(n, k, lo, hi, e):
             if n not in m:
-                m[n] = stage.tile([P, D // 4, K, 4], F32, align_bytes=64, name="m", tag="m", bufs=2)
+                m[n] = stage.tile([P, D // 4, K, 4], F32, align_bytes=64, name="m", tag="m", bufs=depth["m"])
             copier(e)(out=m[n][:, lo // 4:hi // 4, k, :], in_=acc[n, k][:, lo:hi].rearrange("p (q i) -> p q i", i=4))
 
-        def I(n, lo, hi, e="V"):
+        def dx_sort(n, lo, hi):
             if n not in o:
-                o[n] = stage.tile([P, D, K], F32, name="o", tag="o", bufs=3)
-            copier(e)(out=o[n][:, lo:hi].rearrange("p (q i) (c k) -> p q c i k", i=4, k=2),
-                      in_=m[n][:, lo // 4:hi // 4].rearrange("p q (c k) i -> p q c i k", k=2))
+                o[n] = stage.tile([P, D, K], F32, name="o", tag="o", bufs=depth["o"])
+            nc.vector.tensor_copy(out=o[n][:, lo:hi].rearrange("p (q i) (c k) -> p q c i k", i=4, k=2),
+                                  in_=m[n][:, lo // 4:hi // 4].rearrange("p q (c k) i -> p q c i k", k=2))
 
         def store_x(n, lo, hi):
             i, j = divmod(n, J)
@@ -175,65 +185,62 @@ def tile_clusternorm1dv3_v_kernel(tc, x, mu, w, g, dx, dw):
 
         def xa_tile(i):
             if i not in xa:
-                xa[i] = stage.tile([P, K, D, J], BF16, align_bytes=64, name="xa", tag="xa", bufs=1)
+                xa[i] = stage.tile([P, K, D, J], BF16, align_bytes=64, name="xa", tag="xa", bufs=depth["xa"])
             return xa[i][:]
 
-        def a_fill(i, z):
-            xp[i, "a", z] = bank([P, 2, K, 32, J], BF16)
+        def narrow_fill(i, z):
+            xp[i, "narrow", z] = bank([P, 2, K, 32, J], BF16)
             for y in range(2):
-                v = 2 * z + y
-                part = xp[i, "a", z][:, y]
-                nc.tensor.matmul(part.rearrange("p k e j -> p j e k"), lhsT=identb[:], rhs=x_raw[2 * i][:, :, P * v:P * (v + 1)].rearrange("p j (e k) -> p j e k", k=K), start=True, stop=False)
-                nc.tensor.matmul(part, lhsT=negb[:, v:v + 1].to_broadcast([P, P]), rhs=murow[:].rearrange("p (e k) -> p k e", k=K).unsqueeze(3).to_broadcast([P, K, 32, J]), start=False, stop=True)
+                u = 2 * z + y
+                part = xp[i, "narrow", z][:, y]
+                nc.tensor.matmul(part.rearrange("p k e j -> p j e k"), lhsT=identb[:],
+                                 rhs=x_raw[2 * i][:, :, P * u:P * (u + 1)].rearrange("p j (e k) -> p j e k", k=K), start=True, stop=False)
+                nc.tensor.matmul(part, lhsT=negb[:, u:u + 1].to_broadcast([P, P]),
+                                 rhs=murow[:].rearrange("p (e k) -> p k e", k=K).unsqueeze(3).to_broadcast([P, K, 32, J]), start=False, stop=True)
 
-        def a_exit(i, z, e):
-            copier(e)(out=xa_tile(i)[:, :, 64 * z:64 * (z + 1), :].rearrange("p k (y e) j -> p y k e j", y=2), in_=xp[i, "a", z][:])
+        def narrow_out(i, z):
+            nc.scalar.copy(out=xa_tile(i)[:, :, 64 * z:64 * (z + 1), :].rearrange("p k (y e) j -> p y k e j", y=2), in_=xp[i, "narrow", z][:])
 
-        def x_fill(i, *vs):
-            for v in vs:
-                xp[i, v] = bank([P, J, P], F32)
+        def wide_fill(i, *units):
+            for u in units:
+                xp[i, u] = bank([P, J, P], F32)
                 for j in range(J):
-                    nc.tensor.matmul(xp[i, v][:, j, :], lhsT=negmu[:, v:v + 1].to_broadcast([P, P]), rhs=ident[:], start=(j == 0), stop=False, is_transpose=True)
-            for v in vs:
-                nc.tensor.matmul(xp[i, v][:], lhsT=identb[:], rhs=x_raw[2 * i][:, :, P * v:P * (v + 1)], start=False, stop=True)
+                    nc.tensor.matmul(xp[i, u][:, j, :], lhsT=negmu[:, u - 2 * NARROW:u - 2 * NARROW + 1].to_broadcast([P, P]), rhs=ident[:],
+                                     start=(j == 0), stop=False, is_transpose=True)
+            for u in units:
+                nc.tensor.matmul(xp[i, u][:], lhsT=identb[:], rhs=x_raw[2 * i][:, :, P * u:P * (u + 1)], start=False, stop=True)
 
-        def x_exit(i, v, e):
-            copier(e)(out=xa_tile(i)[:, :, 32 * v:32 * (v + 1), :], in_=xp[i, v][:].rearrange("p j (e k) -> p k e j", k=K))
+        def wide_out(i, u):
+            nc.scalar.copy(out=xa_tile(i)[:, :, 32 * u:32 * (u + 1), :], in_=xp[i, u][:].rearrange("p j (e k) -> p k e j", k=K))
 
         def x_sub(i):
             part = x_raw[2 * i + 1][:]
-            nc.vector.tensor_tensor(out=part, in0=part, in1=mub[:, P * NS[i] - HALF:].unsqueeze(1).to_broadcast([P, J, DK - P * NS[i]]), op=ALU.subtract)
+            nc.vector.tensor_tensor(out=part, in0=part, in1=mub[:, P * UNITS[i] - HALF:].unsqueeze(1).to_broadcast([P, J, DK - P * UNITS[i]]), op=ALU.subtract)
 
         def x_sort(i):
-            interleave(xa_tile(i)[:, :, 32 * NS[i]:, :], x_raw[2 * i + 1][:].rearrange("p j (e k) -> p j e k", k=K))
+            interleave(xa_tile(i)[:, :, 32 * UNITS[i]:, :], x_raw[2 * i + 1][:].rearrange("p j (e k) -> p j e k", k=K))
 
         def x_quant(i, z):
-            nc.vector.quantize_mx(out=xq[:, i, 2 * z:2 * z + 2].rearrange("p k e -> p (k e)").bitcast(E4M3), scales=xs[:, i, 2 * z:2 * z + 2].rearrange("p k e -> p (k e)"),
-                                  in_=xa_tile(i)[:, 2 * z:2 * z + 2].rearrange("p k e j -> p (k e j)"))
+            quantize(xq[:, i, 2 * z:2 * z + 2].rearrange("p k e -> p (k e)"), xs[:, i, 2 * z:2 * z + 2].rearrange("p k e -> p (k e)"),
+                     xa_tile(i)[:, 2 * z:2 * z + 2].rearrange("p k e j -> p (k e j)"), E4M3)
 
         def dw_mm(b, lo, hi):
-            t, k = divmod(b, K)
+            c, k = divmod(b, K)
             if lo == 0:
                 acc["w", b] = bank([P, D], F32)
-            for z in range(lo, hi):
-                i = z
-                nc.tensor.matmul_mx(out=acc["w", b][:], lhsT=gq[:, t, i, k, :].bitcast(E5M2), lhsT_scale=gs[:, t, i, k, :],
-                                    rhs=xq[:, i, k, :].bitcast(E4M3), rhs_scale=xs[:, i, k, :], start=(z == 0), stop=(z == G - 1))
+            for i in range(lo, hi):
+                nc.tensor.matmul_mx(out=acc["w", b][:], lhsT=gq[:, c, i, k, :].bitcast(E5M2), lhsT_scale=gs[:, c, i, k, :],
+                                    rhs=xq[:, i, k, :].bitcast(E4M3), rhs_scale=xs[:, i, k, :], start=(i == 0), stop=(i == G - 1))
 
         def dw_out(b, e):
-            t, k = divmod(b, K)
-            if t not in ow:
-                ow[t] = turns.tile([P, K, D], F32, name="ow%d" % t, offset=place["ow", t][0])
-            copier(e)(out=ow[t][:, k, :], in_=acc["w", b][:])
+            c, k = divmod(b, K)
+            if c not in ow:
+                ow[c] = turns.tile([P, K, D], F32, name="ow%d" % c, offset=place["ow", c][0])
+            copier(e)(out=ow[c][:, k, :], in_=acc["w", b][:])
 
-        def store_w(lo, hi):
-            t, k = divmod(lo, K)
-            nc.sync.dma_start(out=dwv[t, :, k:k + hi - lo, :], in_=ow[t][:, k:k + hi - lo, :])
-
-        depth = {"graw": 2, "o": 3, "m": 2, "ga": 1, "gd": 2, "gdq": 5, "xa": 1}
-
-        def unit_of(n, k):
-            return n
+        def store_w(b):
+            c, k = divmod(b, K)
+            nc.sync.dma_start(out=dwv[c, :, k:k + 2, :], in_=ow[c][:, k:k + 2, :])
 
         def touches(step):
             f, a = step[0], step[1:]
@@ -254,76 +261,87 @@ def tile_clusternorm1dv3_v_kernel(tc, x, mu, w, g, dx, dw):
             if f is mu_out:
                 return [("mt", 2)], [(("mub",), None)]
             if f is w_sort:
-                return [("w", k) for k in range(*a[:2])], [(("wa", k), ("m", "wa", k // 2)) for k in range(*a[:2])]
+                return [("w", a[0])], [(("wa", a[0]), ("m", "wa", a[0] // 2))]
             if f is w_quant:
-                return [("wa", 2 * a[0]), ("wa", 2 * a[0] + 1)], [(("wq", 2 * a[0]), None), (("wq", 2 * a[0] + 1), None)]
+                return [("wa", 2 * a[0] + y) for y in range(2)], [(("wq", 2 * a[0] + y), None) for y in range(2)]
             if f is g_sort:
-                return [("g", a[0], j) for j in range(J)], [(("ga",) + a[:2], ("ga", a[1]))]
+                return [("g", a[0], j) for j in range(J)], [(("ga",) + a, ("ga", a[1]))]
             if f is g_quant:
                 return [("ga", i, a[0]) for i in range(a[1], a[2])], [(("gq", i, a[0]), None) for i in range(a[1], a[2])]
-            if f is T:
-                i, r = divmod(a[0], J)
-                return [("g", i, r)], [(("tr",) + a, ("bank", "tr") + a)]
-            if f is C:
-                return [("tr",) + a[:2]], [(("gd",) + a[:2], ("gd", a[0]))]
-            if f is Q:
+            if f is g_turn:
+                return [("g",) + divmod(a[0], J)], [(("tr",) + a, ("bank", "tr") + a)]
+            if f is turned_out:
+                return [("tr",) + a], [(("gd",) + a, ("gd", a[0]))]
+            if f is tile_quant:
                 return [("gd", a[0], z) for z in range(2)], [(("gdq", a[0]), ("gdq", a[0]))]
-            if f is M:
-                return [("gdq", unit_of(a[0], k)) for k in a[1:]] + [("wq", k) for k in a[1:]], [(("acc", a[0], k), ("bank", "acc", a[0], k)) for k in a[1:]]
-            if f is E:
-                return [("acc",) + a[:2]], [(("m", a[0], a[1], c), ("m", a[0])) for c in range(a[2], a[3], P)]
-            if f is I:
-                return [("m", a[0], k, c) for k in range(K) for c in range(a[1], a[2], P)], [(("o", a[0], c), ("o", a[0])) for c in range(a[1], a[2], P)]
+            if f is dx_mm:
+                return [("gdq", a[0]), ("wq", a[1])], [(("acc",) + a, ("bank", "acc") + a)]
+            if f is dx_out:
+                return [("acc",) + a[:2]], [(("m", a[0], a[1], e), ("m", a[0])) for e in range(a[2], a[3], P)]
+            if f is dx_sort:
+                return [("m", a[0], k, e) for k in range(K) for e in range(a[1], a[2], P)], [(("o", a[0], e), ("o", a[0])) for e in range(a[1], a[2], P)]
             if f is store_x:
-                return [("o", a[0], c) for c in range(a[1], a[2], P)], []
-            if f is x_fill:
-                return [("x", 2 * a[0]), ("mucol",)], [(("xp", a[0], v), ("bank", "xp", a[0], v)) for v in a[1:]]
-            if f is a_fill:
-                return [("x", 2 * a[0]), ("mucol",)], [(("ap",) + a, ("bank", "ap") + a)]
-            if f is x_exit:
-                return [("xp",) + a[:2]], [(("xa",) + a[:2], ("xa", a[0]))]
-            if f is a_exit:
-                return [("ap",) + a[:2]], [(("xa", a[0], 2 * a[1] + y), ("xa", a[0])) for y in range(2)]
+                return [("o", a[0], e) for e in range(a[1], a[2], P)], []
+            if f is wide_fill:
+                return [("x", 2 * a[0]), ("mucol",)], [(("xp", a[0], u), ("bank", "xp", a[0], u)) for u in a[1:]]
+            if f is narrow_fill:
+                return [("x", 2 * a[0]), ("mu",)], [(("narrow",) + a, ("bank", "narrow") + a)]
+            if f is wide_out:
+                return [("xp",) + a], [(("xa",) + a, ("xa", a[0]))]
+            if f is narrow_out:
+                return [("narrow",) + a], [(("xa", a[0], 2 * a[1] + y), ("xa", a[0])) for y in range(2)]
             if f is x_sub:
                 return [("x", 2 * a[0] + 1), ("mub",)], [(("xc", a[0]), ("turns", "x", 2 * a[0] + 1))]
             if f is x_sort:
-                return [("xc", a[0])], [(("xa", a[0], NS[a[0]]), ("xa", a[0]))]
+                return [("xc", a[0])], [(("xa", a[0], UNITS[a[0]]), ("xa", a[0]))]
             if f is x_quant:
-                return [("xa", a[0], v) for v in range(NS[a[0]] + 1)], [(("xq", a[0], a[1]), None)]
+                return [("xa", a[0], u) for u in range(UNITS[a[0]] + 1)], [(("xq",) + a, None)]
             if f is dw_mm:
-                groups = [z for z in range(a[1], a[2])]
-                return ([("gq", i, a[0] // K) for i in groups] + [("xq", i, a[0] % K // 2) for i in groups] + [("aw", a[0], z) for z in range(a[1])],
-                        [(("aw", a[0], z), ("bank", "aw", a[0])) for z in range(a[1], a[2])])
+                groups = range(a[1], a[2])
+                return ([("gq", i, a[0] // K) for i in groups] + [("xq", i, a[0] % K // 2) for i in groups] + [("aw", a[0], i) for i in range(a[1])],
+                        [(("aw", a[0], i), ("bank", "aw", a[0])) for i in groups])
             if f is dw_out:
-                return [("aw", a[0], z) for z in range(G)], [(("ow", a[0]), ("turns", "ow", a[0] // K))]
-            return [("ow", b) for b in range(a[0], a[1])], []
+                return [("aw", a[0], i) for i in range(G)], [(("ow", a[0]), ("turns", "ow", a[0] // K))]
+            return [("ow", a[0]), ("ow", a[0] + 1)], []
 
-        def emit(queues):
-            writer, slot, users = {}, {}, {}
-            for q in queues:
-                for step in q:
-                    for piece, s in touches(step)[1]:
-                        writer[piece] = step
-                        slot[piece] = s
-            for q in queues:
-                for step in q:
-                    reads, writes = touches(step)
-                    for piece in reads + [piece for piece, s in writes]:
-                        users.setdefault(slot[piece], []).append(step)
-            halves = [step for step in queues[1] if step[0] is a_fill]
-            recent, holder, seat_before = list(range(8)), {}, {}
-            for step in queues[1]:
-                for piece, s in touches(step)[1]:
-                    if s not in seat_before:
-                        free = [b for b in recent if (b >= 6) == (step[0] is a_fill) or not halves]
-                        recent.remove(free[0])
-                        recent.append(free[0])
-                        seats.append(free[0])
-                        seat_before[s] = [holder[free[0]]] if free[0] in holder else []
-                        holder[free[0]] = s
-                if step in halves:
-                    halves.remove(step)
-            done, taken, ring = set(), set(), {tag: [] for tag in list(depth) + ["turns", "bank"]}
+        def deal_banks(tensor):
+            left = [step for step in tensor if step[0] in (narrow_fill, wide_fill)]
+            recent, holder, before = list(range(8)), {}, {}
+            for step in tensor:
+                for piece, buf in touches(step)[1]:
+                    if buf not in before:
+                        b = [b for b in recent if (b >= 6) == (step[0] is narrow_fill) or not left][0]
+                        recent.remove(b)
+                        recent.append(b)
+                        seats.append(b)
+                        before[buf] = [holder[b]] if b in holder else []
+                        holder[b] = buf
+                if step in left:
+                    left.remove(step)
+            return before
+
+        def emit(dma, tensor, scalar, vector):
+            queues = [dma, tensor, scalar, vector]
+            writer, home, users = {}, {}, {}
+            for step in dma + tensor + scalar + vector:
+                for piece, buf in touches(step)[1]:
+                    writer[piece] = step
+                    home[piece] = buf
+            for step in dma + tensor + scalar + vector:
+                reads, writes = touches(step)
+                for piece in reads + [piece for piece, buf in writes]:
+                    users.setdefault(home[piece], []).append(step)
+            banks_before = deal_banks(tensor)
+            done, taken = set(), {tag: [] for tag in list(depth) + ["turns", "bank"]}
+
+            def forerunners(buf):
+                earlier = taken[buf[0]]
+                if buf[0] == "bank":
+                    return banks_before[buf]
+                if buf[0] == "turns":
+                    return [r for r in earlier if place[r[1:]][0] < place[buf[1:]][1] and place[buf[1:]][0] < place[r[1:]][1]]
+                return earlier[-depth[buf[0]]:][:1] if len(earlier) >= depth[buf[0]] else []
+
             at = [0] * len(queues)
             while any(at[z] < len(q) for z, q in enumerate(queues)):
                 moved = False
@@ -332,22 +350,98 @@ def tile_clusternorm1dv3_v_kernel(tc, x, mu, w, g, dx, dw):
                         step = q[at[z]]
                         reads, writes = touches(step)
                         fresh = []
-                        for piece, s in writes:
-                            if s is not None and s not in taken and s not in fresh:
-                                fresh.append(s)
-                        before = [ring[s[0]][len(ring[s[0]]) + y - depth[s[0]]] for y, s in enumerate(fresh) if s[0] in depth and len(ring[s[0]]) + y >= depth[s[0]]]
-                        before = before + [r for s in fresh for r in seat_before.get(s, [])]
-                        before = before + [r for s in fresh if s[0] == "turns" for r in ring["turns"] if place[r[1:]][0] < place[s[1:]][1] and place[s[1:]][0] < place[r[1:]][1]]
-                        if any(writer[piece] not in done for piece in reads) or any(u not in done for s in before for u in users[s]):
+                        for piece, buf in writes:
+                            if buf is not None and buf not in taken[buf[0]] and buf not in fresh:
+                                fresh.append(buf)
+                        if any(writer[piece] not in done for piece in reads) or any(u not in done for buf in fresh for r in forerunners(buf) for u in users[r]):
                             break
                         step[0](*step[1:])
                         done.add(step)
-                        for s in fresh:
-                            taken.add(s)
-                            ring[s[0]].append(s)
+                        for buf in fresh:
+                            taken[buf[0]].append(buf)
                         at[z] = at[z] + 1
                         moved = True
-                assert moved, [q[at[z]][1:] for z, q in enumerate(queues) if at[z] < len(q)]
+                assert moved
+
+        def turned(n):
+            return [(turned_out, n, z) for z in range(2)]
+
+        def products(n):
+            return [(dx_out, n, k, 0, D, "S") for k in range(K)]
+
+        def weave(a, b):
+            return [s for z in range(max(len(a), len(b))) for s in a[z:z + 1] + b[z:z + 1]]
+
+        last, half = N - 1, D // 2
+        xtiles = 2 * G
+        banks = {n: 4 if n == FOUR else 2 for n in range(xtiles, last)}
+        first = {n: sum(banks[z] for z in range(xtiles, n)) for n in range(xtiles, N)}
+        end = first[last]
+
+        dma = [(load_g, 0, 0, 1), (load_w, 0), (load_mu,), (load_w, 1)]
+        for j in range(1, J):
+            dma = dma + [(load_g, 0, j, j + 1)] + ([(load_w, j + 1)] if j + 1 < K else [])
+        dma = dma + [(load_x, 0), (load_x, 1), (load_g, 1, 0, J), (load_x, 3), (load_x, 2), (store_x, 0, 0, D), (load_x, 5), (store_x, 1, 0, D),
+                     (load_x, 4), (store_x, 2, 0, D), (load_g, 2, 0, J)]
+        for n in range(3, last):
+            dma = dma + [(store_x, n, 0, D)]
+            if n + 1 in banks:
+                dma = dma + [(store_w, b) for b in range(first[n + 1], first[n + 2], 2)]
+        dma = dma + [(store_w, b) for b in range(end, 4 * K, 2)] + [(store_x, last, 0, half), (store_x, last, half, D)]
+
+        scalar = turned(0) + turned(1) + turned(2) + [(mu_out,)] + turned(3)
+        for n in range(last):
+            scalar = scalar + (turned(n + LEAD) if J <= n + LEAD < last else []) + products(n)[:2]
+            if n < xtiles:
+                i, y = divmod(n, 2)
+                wide = [(wide_out, i, u) for u in range(2 * NARROW, UNITS[i])]
+                scalar = scalar + [(narrow_out, i, y)] + products(n)[2:] + (wide[2:] if y else wide[:2])
+            else:
+                scalar = scalar + weave(products(n)[2:], [(dw_out, b, "S") for b in range(first[n], first[n + 1])])
+        scalar = scalar + turned(last)
+
+        tensor = []
+        for step in scalar:
+            f, a = step[0], step[1:]
+            if f is turned_out:
+                tensor = tensor + [(g_turn,) + a] + ([((mu_turn, mu_spread)[a[0]],)] if a[0] < 2 and a[1] == 1 else [])
+            if f is dx_out:
+                tensor = tensor + [(dx_mm,) + a[:2]]
+            if f is narrow_out:
+                tensor = tensor + [(narrow_fill,) + a]
+            if f is wide_out and a[1] % 2 == 0:
+                tensor = tensor + [(wide_fill, a[0]) + tuple(range(a[1], min(a[1] + 2, UNITS[a[0]])))]
+            if f is dw_out:
+                tensor = tensor + [(dw_mm, a[0], 0, G)]
+
+        vector = [(w_sort, 0), (mu_cols,), (w_sort, 1), (tile_quant, 0), (w_quant, 0), (w_sort, 2), (w_sort, 3), (tile_quant, 1), (w_quant, 1),
+                  (tile_quant, 2), (g_sort, 0, 0), (tile_quant, 3), (g_quant, 0, 0, 1), (x_sub, 0)]
+        for n in range(last):
+            i, y = divmod(n, 2)
+            c = (n - 3) // 2
+            ahead = [(tile_quant, n + LEAD)] if J <= n + LEAD < last else []
+            sort = [(dx_sort, n, 0, D)]
+            codes = [(x_quant, i, z) for z in range(2)]
+            if n == 0:
+                vector = vector + sort + [(x_sort, i)]
+            elif n == 1:
+                vector = vector + sort + codes + [(x_sub, i + 1)]
+            elif n < xtiles and y == 0:
+                vector = vector + ahead + [(x_sort, i)] + sort
+            elif n < xtiles - 1:
+                vector = vector + [(g_sort, i, 0)] + ahead + [(x_sub, i + 1)] + sort + codes
+            elif n < xtiles:
+                vector = vector + [(g_sort, i, 0)] + ahead + [(g_quant, 0, 1, G), (g_sort, 0, c), (g_sort, 1, c)] + sort + codes + [(g_quant, c, 0, 2)]
+            elif y == 0:
+                vector = vector + [(g_sort, 2, c)] + ahead + sort + [(g_quant, c, 2, G)]
+            else:
+                vector = vector + [(g_sort, 0, c), (g_sort, 1, c)] + ahead + sort + [(g_quant, c, 0, 2)]
+
+        tensor = tensor + [(dw_mm, b, 0, G - 1) for b in range(end, 4 * K)] + [(dw_mm, b, G - 1, G) for b in range(end, 4 * K)]
+        tensor = tensor + [(dx_mm, last, (k - 1) % K) for k in range(K)]
+        scalar = scalar + [(dw_out, b, "S") for b in range(end, 4 * K - 1)]
+        scalar = scalar + [(dx_out, last, k, lo, lo + half, "S") for lo in (0, half) for k in range(K - 1)]
+        vector = vector + [(tile_quant, last), (dw_out, 4 * K - 1, "V"), (dx_out, last, K - 1, 0, D, "V"), (dx_sort, last, 0, half), (dx_sort, last, half, D)]
 
         with tc.manual_schedule():
             nc.vector.memset(murow[:], 0.0)
@@ -355,89 +449,4 @@ def tile_clusternorm1dv3_v_kernel(tc, x, mu, w, g, dx, dw):
             make_identity(nc, ident[:])
             make_identity(nc, identb[:])
             nc.vector.tensor_scalar(out=negb[:], in0=identb[:], scalar1=-1.0, scalar2=None, op0=ALU.mult)
-
-            def Cs(u, e="S"):
-                return [(C, u, z, e) for z in range(2)]
-
-            def Ts(u):
-                return [(T, u, z) for z in range(2)]
-
-            def Es(n):
-                return [(E, n, k, 0, D, "S") for k in range(K)]
-
-            def Xs(i):
-                return [(a_exit, i, z, "S") for z in range(NA[i])] + [(x_exit, i, v, "S") for v in range(2 * NA[i], NS[i])]
-
-            def Fs(i):
-                return [(a_fill, i, z) for z in range(NA[i])] + [(x_fill, i) + tuple(range(v, min(v + 2, NS[i]))) for v in range(2 * NA[i], NS[i], 2)]
-
-            def Ms(n):
-                return [(M, n, 0, 1, 2, 3)]
-
-            def Ws(lo, hi):
-                return [(dw_mm, b, 0, G) for b in range(lo, hi)]
-
-            def Ds(lo, hi, e="S"):
-                return [(dw_out, b, e) for b in range(lo, hi)]
-
-            def St(n):
-                return [(store_x, n, 0, D)]
-
-            def Sw(lo):
-                return [(store_w, lo, lo + 2)]
-
-            def Iv(n):
-                return [(I, n, 0, D)]
-
-            def weave(a, b):
-                out = []
-                for z in range(max(len(a), len(b))):
-                    out = out + a[z:z + 1] + b[z:z + 1]
-                return out
-
-            def M1(n):
-                return [(M, n, k) for k in range(K)]
-
-            def S3(c):
-                return [(g_sort, i, c) for i in range(G)]
-
-            dq = [(load_g, 0, 0, 1), (load_mu,), (load_w, 0), (load_g, 0, 1, 2), (load_w, 1), (load_g, 0, 2, 3), (load_w, 2), (load_g, 0, 3, 4), (load_w, 3),
-                  (load_x, 0), (load_x, 1), (load_g, 1, 0, 2), (load_x, 2), (load_x, 3)] + St(0) + [(load_g, 1, 2, 4), (load_x, 4)] + St(1)
-            dq = dq + [(load_x, 5)] + St(2) + [(load_g, 2, 0, 2), (load_g, 2, 2, 4)] + St(3) + St(4) + St(5)
-            NW = {5: 0, 6: 2, 7: 3, 8: 3, 9: 4, 10: 0, 11: 4}
-            ONV = (14, 15)
-            first = {n: sum(NW[z] for z in range(5, n)) for n in range(5, N + 1)}
-            for n in range(6, N - 1):
-                ws_ = [(store_w, b - 1, b + 1) for b in range(first[n], first[n + 1]) if b % 2 == 1]
-                dq = dq + ws_[:1] + St(n) + ws_[1:]
-            dq = dq + Sw(12) + Sw(14) + [(store_x, N - 1, 0, 256), (store_x, N - 1, 256, D)]
-
-            tq = Ts(0)[:1] + [(mu_turn,)] + Ts(0)[1:] + [(mu_spread,)] + Ts(1) + Ts(2) + Ts(3)
-            sq = Cs(0) + Cs(1) + Cs(2) + Cs(3)
-            XA, XB = [Xs(i)[:NA[i]] for i in range(G)], [Xs(i)[NA[i]:] for i in range(G)]
-            FA, FB = [Fs(i)[:NA[i]] for i in range(G)], [Fs(i)[NA[i]:] for i in range(G)]
-            sq = sq + Es(0)[:2] + XA[0][:1] + Es(0)[2:] + XB[0][:2] + Es(1)[:2] + XA[0][1:] + Es(1)[2:] + XB[0][2:] + Cs(4)
-            tq = tq + [(M, 0, 0, 1)] + FA[0][:1] + [(M, 0, 2, 3)] + FB[0][:1] + [(M, 1, 0, 1)] + FA[0][1:] + [(M, 1, 2, 3)] + FB[0][1:] + Ts(4)
-            sq = sq + Es(2)[:2] + XA[1][:1] + Es(2)[2:] + XA[1][1:] + XB[1] + Cs(5) + Es(3) + Cs(6) + XB[2][:2] + Es(4)[:2] + XA[2][:1] + XB[2][2:] + Es(4)[2:] + XA[2][1:]
-            tq = tq + [(M, 2, 0, 1)] + FA[1][:1] + [(M, 2, 2, 3)] + FA[1][1:] + FB[1] + Ts(5) + Ms(3) + Ts(6) + FB[2][:1] + M1(4)[:2] + FA[2][:1] + FB[2][1:] + M1(4)[2:] + FA[2][1:]
-            for n in range(5, N):
-                ds = [(dw_out, b, "S") for b in range(first[n], first[n + 1]) if b not in ONV]
-                if n + 2 < N - 1:
-                    sq = sq + Cs(n + 2)
-                    tq = tq + Ts(n + 2)
-                if n < N - 1:
-                    sq = sq + Es(n)[:2] + weave(Es(n)[2:], ds)
-                    tq = tq + M1(n)[:2] + weave(M1(n)[2:], Ws(first[n], first[n + 1]))
-                    if n == N - 2:
-                        sq = sq + Cs(N - 1)
-                        tq = tq + Ts(N - 1)
-                else:
-                    sq = sq + ds + [(E, n, k, lo, lo + 256, "S") for lo in (0, 256) for k in range(K)]
-                    tq = tq + [(dw_mm, b, 0, 2) for b in range(12, 16)] + [(dw_mm, b, 2, 3) for b in range(12, 16)] + Ms(n)
-
-            vq = [(mu_cols,), (w_sort, 0, 1), (mu_out, "V"), (w_sort, 1, 2), (Q, 0), (w_quant, 0), (Q, 1), (w_sort, 2, 3), (w_sort, 3, 4), (Q, 2), (w_quant, 1), (g_sort, 0, 0), (Q, 3), (x_sub, 0)]
-            vq = vq + Iv(0) + [(x_sort, 0), (g_quant, 0, 0, 1), (x_quant, 0, 0), (x_quant, 0, 1)] + Iv(1) + [(x_sub, 1), (Q, 4), (x_sort, 1)] + Iv(2) + [(x_quant, 1, 0), (x_quant, 1, 1), (x_sub, 2), (Q, 5), (x_sort, 2)]
-            vq = vq + Iv(3) + [(Q, 6), (g_sort, 1, 0), (g_sort, 2, 0)] + Iv(4) + [(x_quant, 2, 0), (x_quant, 2, 1), (g_quant, 0, 1, 3), (Q, 7)] + S3(1)[:2] + Iv(5)
-            vq = vq + [(g_quant, 1, 0, 2), (Q, 8)] + S3(1)[2:] + Iv(6) + [(g_quant, 1, 2, 3), (Q, 9)] + S3(2)[:2] + Iv(7) + S3(2)[2:] + [(g_quant, 2, 0, 2), (Q, 10), (g_quant, 2, 2, 3)] + Iv(8)
-            vq = vq + S3(3)[:2] + Iv(9) + [(g_quant, 3, 0, 2)] + S3(3)[2:] + Iv(10) + [(g_quant, 3, 2, 3), (Q, 11)] + Ds(14, 16, "V") + [(I, 11, 0, 256), (I, 11, 256, D)]
-            emit([dq, tq, sq, vq])
+            emit(dma, tensor, scalar, vector)

@@ -57,7 +57,7 @@ def tile_clusternorm1dv3_v_kernel(tc, x, mu, w, g, dx, dw):
         wq = keep.tile([P, K, D], U32, align_bytes=64)
         ws = keep.tile([P, K, D], U8, align_bytes=64)
         mucol = keep.tile([P, 4], F32)
-        negmu = keep.tile([P, rows - 2 * NARROW], F32)
+        negmu = keep.tile([P, rows], F32)
         mub = keep.tile([P, HALF], BF16)
 
         g_raw, x_raw, w_raw, ga, gd, gdq, gds, acc, m, xa, wa, tr, xp, ow, mt, o = ({} for i in range(16))
@@ -110,7 +110,7 @@ def tile_clusternorm1dv3_v_kernel(tc, x, mu, w, g, dx, dw):
             nc.tensor.transpose(mt[1][:], muwords[:].bitcast(F32), ident[:])
 
         def mu_cols():
-            nc.vector.tensor_scalar(out=negmu[:], in0=mt[0][:, 2 * NARROW:rows], scalar1=-1.0, scalar2=None, op0=ALU.mult)
+            nc.vector.tensor_scalar(out=negmu[:], in0=mt[0][:, 0:rows], scalar1=-1.0, scalar2=None, op0=ALU.mult)
             nc.vector.tensor_copy(out=mucol[:], in_=mt[1][:, 0:4])
 
         def mu_spread():
@@ -205,7 +205,7 @@ def tile_clusternorm1dv3_v_kernel(tc, x, mu, w, g, dx, dw):
             for u in units:
                 xp[i, u] = bank([P, J, P], F32)
                 for j in range(J):
-                    nc.tensor.matmul(xp[i, u][:, j, :], lhsT=negmu[:, u - 2 * NARROW:u - 2 * NARROW + 1].to_broadcast([P, P]), rhs=ident[:],
+                    nc.tensor.matmul(xp[i, u][:, j, :], lhsT=negmu[:, u:u + 1].to_broadcast([P, P]), rhs=ident[:],
                                      start=(j == 0), stop=False, is_transpose=True)
             for u in units:
                 nc.tensor.matmul(xp[i, u][:], lhsT=identb[:], rhs=x_raw[2 * i][:, :, P * u:P * (u + 1)], start=False, stop=True)

@@ -26,7 +26,7 @@ PLAIN = 38
 WIDE = PLAIN - 2 * 2 * NARROW * G
 UNITS = [2 * NARROW + (WIDE + G - 1 - i) // G for i in range(G)]
 LEAD = 2
-FOUR = 8
+FOUR = 9
 
 
 def tile_clusternorm1dv3_v_kernel(tc, x, mu, w, g, dx, dw):
@@ -381,8 +381,8 @@ def tile_clusternorm1dv3_v_kernel(tc, x, mu, w, g, dx, dw):
         dma = [(load_g, 0, 0, 1), (load_w, 0), (load_mu,), (load_w, 1)]
         for j in range(1, J):
             dma = dma + [(load_g, 0, j, j + 1)] + ([(load_w, j + 1)] if j + 1 < K else [])
-        dma = dma + [(load_x, 0), (load_x, 1), (load_g, 1, 0, J), (load_x, 3), (load_x, 2), (store_x, 0, 0, D), (load_x, 5), (store_x, 1, 0, D),
-                     (load_x, 4), (store_x, 2, 0, D), (load_g, 2, 0, J)]
+        dma = dma + [(load_x, 0), (load_x, 1), (load_g, 1, 0, J)] + [(load_x, 2 * i + b) for i in range(1, G) for b in (1, 0)]
+        dma = dma + [(store_x, 0, 0, D), (store_x, 1, 0, D), (load_g, 2, 0, J), (store_x, 2, 0, D)]
         for n in range(3, last):
             dma = dma + [(store_x, n, 0, D)]
             if n + 1 in banks:
@@ -390,14 +390,14 @@ def tile_clusternorm1dv3_v_kernel(tc, x, mu, w, g, dx, dw):
         dma = dma + [(store_w, b) for b in range(end, 4 * K, 2)] + [(store_x, last, 0, half), (store_x, last, half, D)]
 
         scalar = turned(0) + turned(1) + turned(2) + [(mu_out,)] + turned(3)
-        for n in range(last):
-            scalar = scalar + (turned(n + LEAD) if J <= n + LEAD < last else []) + products(n)[:2]
-            if n < xtiles:
-                i, y = divmod(n, 2)
-                wide = [(wide_out, i, u) for u in range(2 * NARROW, UNITS[i])]
-                scalar = scalar + [(narrow_out, i, y)] + products(n)[2:] + (wide[2:] if y else wide[:2])
-            else:
-                scalar = scalar + weave(products(n)[2:], [(dw_out, b, "S") for b in range(first[n], first[n + 1])])
+        for i in range(G):
+            n = 2 * i
+            wide = [(wide_out, i, u) for u in range(2 * NARROW, UNITS[i])]
+            scalar = scalar + products(n) + (turned(n + LEAD) + turned(n + LEAD + 1) if i else [])
+            scalar = scalar + wide[:2] + products(n + 1)[:2] + [(narrow_out, i, 0)] + wide[2:4] + products(n + 1)[2:] + [(narrow_out, i, 1)] + wide[4:]
+        for n in range(xtiles, last):
+            outs = [(dw_out, b, "S") for b in range(first[n], first[n + 1])]
+            scalar = scalar + (turned(n + LEAD) if n + LEAD < last else []) + products(n)[:2] + weave(products(n)[2:], outs)
         scalar = scalar + turned(last)
 
         tensor = []
@@ -416,26 +416,27 @@ def tile_clusternorm1dv3_v_kernel(tc, x, mu, w, g, dx, dw):
 
         vector = [(w_sort, 0), (mu_cols,), (w_sort, 1), (tile_quant, 0), (w_quant, 0), (w_sort, 2), (w_sort, 3), (tile_quant, 1), (w_quant, 1),
                   (tile_quant, 2), (g_sort, 0, 0), (tile_quant, 3), (g_quant, 0, 0, 1), (x_sub, 0)]
-        for n in range(last):
-            i, y = divmod(n, 2)
-            c = (n - 3) // 2
-            ahead = [(tile_quant, n + LEAD)] if J <= n + LEAD < last else []
-            sort = [(dx_sort, n, 0, D)]
-            codes = [(x_quant, i, z) for z in range(2)]
-            if n == 0:
-                vector = vector + sort + [(x_sort, i)]
-            elif n == 1:
-                vector = vector + sort + codes + [(x_sub, i + 1)]
-            elif n < xtiles and y == 0:
-                vector = vector + ahead + [(x_sort, i)] + sort
-            elif n < xtiles - 1:
-                vector = vector + [(g_sort, i, 0)] + ahead + [(x_sub, i + 1)] + sort + codes
-            elif n < xtiles:
-                vector = vector + [(g_sort, i, 0)] + ahead + [(g_quant, 0, 1, G), (g_sort, 0, c), (g_sort, 1, c)] + sort + codes + [(g_quant, c, 0, 2)]
-            elif y == 0:
-                vector = vector + [(g_sort, 2, c)] + ahead + sort + [(g_quant, c, 2, G)]
+        for i in range(G):
+            n = 2 * i
+            codes, sort = [(x_quant, i, z) for z in range(2)], [(dx_sort, n + 1, 0, D)]
+            vector = vector + [(dx_sort, n, 0, D)]
+            if i == 0:
+                vector = vector + [(x_sort, i)] + sort + codes
+                continue
+            if i == 1:
+                vector = vector + [(x_sub, i)]
+            vector = vector + [(tile_quant, n + LEAD), (x_sort, i), (g_sort, i, 0), (tile_quant, n + LEAD + 1)]
+            if i + 1 < G:
+                vector = vector + [(x_sub, i + 1)] + sort + codes
             else:
-                vector = vector + [(g_sort, 0, c), (g_sort, 1, c)] + ahead + sort + [(g_quant, c, 0, 2)]
+                vector = vector + [(g_quant, 0, 1, G), (g_sort, 0, 1), (g_sort, 1, 1)] + codes + sort + [(g_quant, 1, 0, 2)]
+        for n in range(xtiles, last):
+            c = (n - 3) // 2
+            ahead = [(tile_quant, n + LEAD)] if n + LEAD < last else []
+            if n % 2 == 0:
+                vector = vector + [(g_sort, 2, c)] + ahead + [(dx_sort, n, 0, D), (g_quant, c, 2, G)]
+            else:
+                vector = vector + [(g_sort, 0, c), (g_sort, 1, c)] + ahead + [(dx_sort, n, 0, D), (g_quant, c, 0, 2)]
 
         tensor = tensor + [(dw_mm, b, 0, G - 1) for b in range(end, 4 * K)] + [(dw_mm, b, G - 1, G) for b in range(end, 4 * K)]
         tensor = tensor + [(dx_mm, last, (k - 1) % K) for k in range(K)]

@@ -17,16 +17,14 @@ ALU = mybir.AluOpType
 P = 128
 J = 4
 G = B // (P * J)
-N = G * J
+PAIRS = 2 * G
 DK = D * K
-HALF = DK // 2
 KB = 1024
-NARROW = 2
-PLAIN = 38
-WIDE = PLAIN - 2 * 2 * NARROW * G
-UNITS = [2 * NARROW + (WIDE + G - 1 - i) // G for i in range(G)]
-LEAD = 2
-FOUR = 9
+E = 64
+STRIPS = D // E
+ON_TENSOR = (7, 6, 6)
+EARLY = (1,)
+LATE = tuple(i for i in range(G) if i not in EARLY)
 
 
 def tile_clusternorm1dv3_v_kernel(tc, x, mu, w, g, dx, dw):
@@ -34,420 +32,313 @@ def tile_clusternorm1dv3_v_kernel(tc, x, mu, w, g, dx, dw):
     xv = x.rearrange("(g p j) d k -> g p j (d k)", p=P, j=J)
     gv = g.rearrange("(g p j) d k -> g p j (d k)", p=P, j=J)
     dxv = dx.rearrange("(g p j) d k -> g p j (d k)", p=P, j=J)
-    dwv = dw.rearrange("k (c q) e -> c q k e", c=4)
-    mu_units = mu.rearrange("(u e) k -> u (e k)", u=DK // P)
-    mu_pairs = mu.rearrange("(u e) k -> u (e k)", u=DK // (2 * P))
-    rows = max(UNITS)
+    dwv = dw.rearrange("k (q t) e -> t q k e", t=J)
+    mu_rows = mu.rearrange("(b e) k -> b (e k)", b=STRIPS)
 
     with ExitStack() as ctx:
-        keep = ctx.enter_context(tc.tile_pool(name="keep", bufs=1))
-        stage = ctx.enter_context(tc.tile_pool(name="stage", bufs=2))
-        turns = ctx.enter_context(tc.tile_pool(name="turns", bufs=1))
-        psum = ctx.enter_context(tc.psum_pool(name="psum", bufs=2))
+        sbuf = ctx.enter_context(tc.tile_pool(name="sbuf", bufs=1))
+        psum = ctx.enter_context(tc.psum_pool(name="psum", bufs=1))
 
-        murow = keep.tile([P, P], BF16)
-        muwords = keep.tile([P, 2 * P], BF16)
-        ident = keep.tile([P, P], F32)
-        identb = keep.tile([P, P], BF16)
-        negb = keep.tile([P, P], BF16)
-        gq = keep.tile([P, 4, G, K, P], U32, align_bytes=64)
-        gs = keep.tile([P, 4, G, K, P], U8, align_bytes=64)
-        xq = keep.tile([P, G, K, D], U32, align_bytes=64)
-        xs = keep.tile([P, G, K, D], U8, align_bytes=64)
-        wq = keep.tile([P, K, D], U32, align_bytes=64)
-        ws = keep.tile([P, K, D], U8, align_bytes=64)
-        mucol = keep.tile([P, 4], F32)
-        negmu = keep.tile([P, rows], F32)
-        mub = keep.tile([P, HALF], BF16)
+        spec, t = {}, {}
 
-        g_raw, x_raw, w_raw, ga, gd, gdq, gds, acc, m, xa, wa, tr, xp, ow, mt, o = ({} for i in range(16))
+        def lay(key, shape, dtype, size, at):
+            spec[key] = (shape, dtype, at, at + size)
 
-        size = [KB * (UNITS[h // 2] if h % 2 == 0 else DK // P - UNITS[h // 2]) for h in range(2 * G)]
-        place = {("x", h): (sum(size[:h]), sum(size[:h + 1])) for h in range(2 * G - 1)}
-        place["x", 2 * G - 1] = (0, size[-1])
-        place["g", G - 1] = (size[0], size[0] + 16 * KB)
-        for c in range(4):
-            at = (sum(size[:3]), sum(size[:3]) + 8 * KB, 0)[c % 3]
-            place["ow", c] = (at, at + 8 * KB)
-        depth = {"graw": 2, "o": 3, "m": 2, "ga": 1, "gd": 2, "gdq": 5, "xa": 1}
+        at = 0
+        for i in range(G):
+            lay(("gq", i), [P, J, K, P], U32, 8 * KB, at)
+            lay(("xq", i), [P, K, D], U32, 8 * KB, at + 8 * KB)
+            lay(("gs", i), [P, J, K, P], U8, 2 * KB, at + 16 * KB)
+            lay(("xs", i), [P, K, D], U8, 2 * KB, at + 18 * KB)
+            at = at + 20 * KB
+        lay("wq", [P, K, D], U32, 8 * KB, at)
+        lay("ws", [P, K, D], U8, 2 * KB, at + 8 * KB)
+        lay("mu2", [P, STRIPS, K, E, 2], BF16, 8 * KB, at + 10 * KB)
+        lay("ident", [P, P], F32, 512, at + 18 * KB)
+        lay("identb", [P, P], BF16, 256, at + 18 * KB + 512)
+        lay("mucol", [P, 2, STRIPS], F32, 64, at + 18 * KB + 768)
+        raw = at + 19 * KB
+        sort, xsort, turned, codes, out = raw + 64 * KB, raw + 80 * KB, raw + 96 * KB, raw + 112 * KB, raw + 127 * KB
+        for slot, key in ((0, ("g", 0)), (1, ("g", 1)), (2, ("x", 0)), (3, ("g", 2)), (1, ("x", 1)), (2, ("x", 2))):
+            lay(key, [P, J, DK], BF16, 16 * KB, raw + 16 * KB * slot)
+        lay("murow", [P, K * E], BF16, 512, xsort + 8 * KB)
+        lay("mudup", [P, K, E, 2], BF16, KB, xsort + 9 * KB)
+        for k in range(K):
+            lay(("w", k), [P, J, D], BF16, 4 * KB, out + 16 * KB + 4 * KB * k)
+        for z in range(2):
+            lay(("wa", z), [P, 2, D, J], BF16, 8 * KB, sort + 8 * KB * z)
+        for i in EARLY:
+            lay(("ga", i), [P, J, K, P, J], BF16, 16 * KB, sort)
+        blocks = [(i, c) for c in range(J) for i in LATE]
+        for y, (i, c) in enumerate(blocks):
+            lay(("gb", i, c), [P, K, P, J], BF16, 4 * KB, xsort if y == 0 else sort + 4 * KB * (y % 4))
+        for i in range(G):
+            lay(("xa", i), [P, K, D, J], BF16, 16 * KB, xsort)
+        for r in range(PAIRS):
+            lay(("gd", r), [P, 2, K, P, J], BF16, 8 * KB, turned + 8 * KB * (r % 2))
+            lay(("gdq", r), [P, 2, K, P], U32, 4 * KB, codes + 5 * KB * (r % 3))
+            lay(("gds", r), [P, 2, K, P], U8, KB, codes + 5 * KB * (r % 3) + 4 * KB)
+        leaving = [("o", n) for n in range(2 * PAIRS - 3)]
+        for c in range(J):
+            leaving = leaving + [("ow", c)] + ([("o", 2 * PAIRS - 3 + c)] if c < J - 1 else [])
+        for y, key in enumerate(leaving):
+            lay(key, [P, D, K] if key[0] == "o" else [P, K, D], F32, 8 * KB, out + 8 * KB * (y % 4))
 
-        seats, seated = [], []
+        def bank(key, shape, dtype):
+            spec[key] = (shape, dtype)
+            return key
 
-        def bank(shape, dtype):
-            seated.append(seats[len(seated)])
-            return psum.tile(shape, dtype, name="bank%d" % seated[-1], bufs=1)
+        def step(run, reads, writes):
+            return (run, tuple(reads), tuple(writes))
 
         def copier(e):
             return nc.vector.tensor_copy if e == "V" else nc.scalar.copy
 
-        def load_g(i, lo, hi):
-            if lo == 0:
-                if i < G - 1:
-                    g_raw[i] = stage.tile([P, J, DK], BF16, name="graw", bufs=depth["graw"])
-                else:
-                    g_raw[i] = turns.tile([P, J, DK], BF16, name="g2", offset=place["g", i][0])
-            nc.sync.dma_start(out=g_raw[i][:, lo:hi, :], in_=gv[i, :, lo:hi, :])
-
-        def load_x(h):
-            i, b = divmod(h, 2)
-            lo, hi = ((0, P * UNITS[i]), (P * UNITS[i], DK))[b]
-            x_raw[h] = turns.tile([P, J, hi - lo], BF16, name="x%d" % h, offset=place["x", h][0])
-            nc.sync.dma_start(out=x_raw[h][:], in_=xv[i, :, :, lo:hi])
-
-        def load_w(k):
-            if k % 2 == 0:
-                w_raw[k // 2] = stage.tile([P, 2, J, D], BF16, name="wraw", tag="o", bufs=depth["o"])
-            nc.sync.dma_start(out=w_raw[k // 2][:, k % 2], in_=w[k].rearrange("(p j) e -> p j e", j=J))
-
-        def load_mu():
-            nc.sync.dma_start(out=murow[0:rows, :], in_=mu_units[0:rows, :])
-            nc.sync.dma_start(out=muwords[0:4, :], in_=mu_pairs[4:8, :])
-
-        def mu_turn():
-            mt[0] = bank([P, P], BF16)
-            nc.tensor.transpose(mt[0][:], murow[:], identb[:])
-            mt[1] = bank([P, P], F32)
-            nc.tensor.transpose(mt[1][:], muwords[:].bitcast(F32), ident[:])
-
-        def mu_cols():
-            nc.vector.tensor_scalar(out=negmu[:], in0=mt[0][:, 0:rows], scalar1=-1.0, scalar2=None, op0=ALU.mult)
-            nc.vector.tensor_copy(out=mucol[:], in_=mt[1][:, 0:4])
-
-        def mu_spread():
-            mt[2] = bank([P, 4, P], F32)
-            for z in range(4):
-                nc.tensor.transpose(mt[2][:, z, :], mucol[:, z:z + 1].to_broadcast([P, P]), ident[:])
-
-        def mu_out():
-            nc.scalar.copy(out=mub[:].bitcast(F32), in_=mt[2][:].rearrange("p z n -> p (z n)"))
-
         def quantize(codes, scales, values, dtype):
             nc.vector.quantize_mx(out=codes.bitcast(dtype), scales=scales, in_=values)
 
+        def load(name, view, i, lo, hi):
+            return step(lambda: nc.sync.dma_start(out=t[name, i][:, lo:hi, :], in_=view[i, :, lo:hi, :]),
+                        [], [((name, i, j), (name, i)) for j in range(lo, hi)])
+
+        def load_w(k):
+            return step(lambda: nc.sync.dma_start(out=t["w", k][:], in_=w[k].rearrange("(p j) e -> p j e", j=J)), [], [(("w", k), ("w", k))])
+
+        def load_mu():
+            return step(lambda: nc.sync.dma_start(out=t["murow"][0:STRIPS, :], in_=mu_rows), [], [("murow", "murow")])
+
+        def identities():
+            def run():
+                make_identity(nc, t["ident"][:])
+                make_identity(nc, t["identb"][:])
+            return step(run, [], [("ident", "ident"), ("identb", "identb")])
+
+        def mu_zero():
+            return step(lambda: nc.vector.memset(t["mudup"][:], 0.0), [], [("muzero", "mudup")])
+
+        def mu_double():
+            return step(lambda: nc.vector.tensor_copy(out=t["mudup"][0:STRIPS], in_=t["murow"][0:STRIPS, :].rearrange("p (e k) -> p k e", k=K).unsqueeze(3).to_broadcast([STRIPS, K, E, 2])),
+                        ["murow", "muzero"], [("mudup", "mudup")])
+
+        def mu_turn():
+            def run():
+                for h in range(2):
+                    nc.tensor.transpose(t["mt"][:, h, :], t["mudup"][:].rearrange("p k e j -> p (k e j)").bitcast(F32)[:, P * h:P * (h + 1)], t["ident"][:])
+            return step(run, ["mudup", "ident"], [("mt", bank("mt", [P, 2, P], F32))])
+
+        def mu_cols():
+            return step(lambda: nc.vector.tensor_copy(out=t["mucol"][:], in_=t["mt"][:, :, 0:STRIPS]), ["mt"], [("mucol", "mucol")])
+
+        def mu_spread(q):
+            def run():
+                for y in range(4):
+                    b, h = 2 * q + y // 2, y % 2
+                    nc.tensor.transpose(t["ms", q][:, y, :], t["mucol"][:, h, b:b + 1].to_broadcast([P, P]), t["ident"][:])
+            return step(run, ["mucol", "ident"], [(("ms", q), bank(("ms", q), [P, 4, P], F32))])
+
+        def mu_out(q, e):
+            return step(lambda: copier(e)(out=t["mu2"][:, 2 * q:2 * q + 2].rearrange("p b k e j -> p (b k e j)").bitcast(F32), in_=t["ms", q][:].rearrange("p y n -> p (y n)")),
+                        [("ms", q)], [(("mu2", 2 * q + y), "mu2") for y in range(2)])
+
         def w_sort(k):
-            if k % 2 == 0:
-                wa[k // 2] = stage.tile([P, 2, D, J], BF16, align_bytes=64, name="wa", tag="m", bufs=depth["m"])
-            nc.vector.tensor_copy(out=wa[k // 2][:, k % 2:k % 2 + 1].rearrange("p k (c i) j -> p k c j i", i=4),
-                                  in_=w_raw[k // 2][:, k % 2:k % 2 + 1].rearrange("p k j (c i) -> p k c j i", i=4))
+            return step(lambda: nc.vector.tensor_copy(out=t["wa", k // 2][:, k % 2].rearrange("p (c i) j -> p c j i", i=4), in_=t["w", k][:].rearrange("p j (c i) -> p c j i", i=4)),
+                        [("w", k)], [(("wa", k), ("wa", k // 2))])
 
         def w_quant(z):
-            quantize(wq[:, 2 * z:2 * z + 2, :].rearrange("p k e -> p (k e)"), ws[:, 2 * z:2 * z + 2, :].rearrange("p k e -> p (k e)"),
-                     wa[z][:].rearrange("p k e j -> p (k e j)"), E4M3)
+            return step(lambda: quantize(t["wq"][:, 2 * z:2 * z + 2].rearrange("p k e -> p (k e)"), t["ws"][:, 2 * z:2 * z + 2].rearrange("p k e -> p (k e)"),
+                                         t["wa", z][:].rearrange("p k e j -> p (k e j)"), E4M3),
+                        [("wa", 2 * z), ("wa", 2 * z + 1)], [(("wq", z), "wq"), (("ws", z), "ws")])
 
         def interleave(out, in_):
             nc.vector.tensor_copy(out=out.rearrange("p k e (c j) -> p e c k j", j=2), in_=in_.rearrange("p (c j) e k -> p e c k j", j=2))
 
+        def sorted_g(i, c):
+            return t["ga", i][:, c] if i in EARLY else t["gb", i, c][:]
+
         def g_sort(i, c):
-            if i == 0:
-                ga[c] = stage.tile([P, G, K, P, J], BF16, align_bytes=64, name="ga", bufs=depth["ga"])
-            interleave(ga[c][:, i], g_raw[i][:, :, 512 * c:512 * (c + 1)].rearrange("p j (e k) -> p j e k", k=K))
+            return step(lambda: interleave(sorted_g(i, c), t["g", i][:].rearrange("p j (q c k) -> p c j q k", c=J, k=K)[:, c]),
+                        [("g", i, j) for j in range(J)], [(("ga", i, c), ("ga", i) if i in EARLY else ("gb", i, c))])
 
-        def g_quant(c, lo, hi):
-            quantize(gq[:, c, lo:hi].rearrange("p i k d -> p (i k d)"), gs[:, c, lo:hi].rearrange("p i k d -> p (i k d)"),
-                     ga[c][:, lo:hi].rearrange("p i k d j -> p (i k d j)"), E5M2)
+        def g_quant(i, c):
+            return step(lambda: quantize(t["gq", i][:, c].rearrange("p k q -> p (k q)"), t["gs", i][:, c].rearrange("p k q -> p (k q)"),
+                                         sorted_g(i, c).rearrange("p k q j -> p (k q j)"), E5M2),
+                        [("ga", i, c)], [(("gq", i, c), ("gq", i)), (("gs", i, c), ("gs", i))])
 
-        def g_turn(n, z):
-            i, j = divmod(n, J)
-            tr[n, z] = bank([P, 4, P], F32)
-            for t in range(4):
-                nc.tensor.transpose(tr[n, z][:, t, :], g_raw[i][:].bitcast(F32)[:, j, 2 * t + z:DK // 2:8], ident[:])
+        def g_turn(r, y):
+            i, z = divmod(r, 2)
 
-        def turned_out(n, z):
-            if z == 0:
-                gd[n] = stage.tile([P, 2, 2, P, 4], BF16, align_bytes=64, name="gd", bufs=depth["gd"])
-            nc.scalar.copy(out=gd[n][:, z], in_=tr[n, z][:].bitcast(BF16).rearrange("q t (m e) -> q e m t", e=2))
+            def run():
+                for c in range(J):
+                    if i in EARLY:
+                        words = t["ga", i][:, c, y].rearrange("p q j -> p (q j)").bitcast(F32)[:, z:2 * P:2]
+                    else:
+                        words = t["g", i][:].bitcast(F32)[:, 2 * z + y // 2, 2 * c + y % 2:DK // 2:8]
+                    nc.tensor.transpose(t["tr", r, y][:, c, :], words, t["ident"][:])
+            reads = [("ga", i, c) for c in range(J)] if i in EARLY else [("g", i, 2 * z + y // 2)]
+            return step(run, reads + ["ident"], [(("tr", r, y), bank(("tr", r, y), [P, J, P], F32))])
 
-        def tile_quant(n):
-            gdq[n] = stage.tile([P, K, P], U32, align_bytes=64, name="gdq", bufs=depth["gdq"])
-            gds[n] = stage.tile([P, K, P], U8, align_bytes=64, name="gds", bufs=depth["gdq"])
-            quantize(gdq[n][:].rearrange("p k m -> p (k m)"), gds[n][:].rearrange("p k m -> p (k m)"),
-                     gd[n][:].rearrange("p a b m t -> p (a b m t)"), E5M2)
+        def turned_out(r, y):
+            def run():
+                part = t["gd", r][:, :, y] if r // 2 in EARLY else t["gd", r][:, y // 2, 2 * (y % 2):2 * (y % 2) + 2]
+                nc.scalar.copy(out=part, in_=t["tr", r, y][:].bitcast(BF16).rearrange("q c (m e) -> q e m c", e=2))
+            return step(run, [("tr", r, y)], [(("gd", r, y), ("gd", r))])
 
-        def dx_mm(n, k):
-            acc[n, k] = bank([P, D], F32)
-            nc.tensor.matmul_mx(out=acc[n, k][:], lhsT=gdq[n][:, k, :].bitcast(E5M2), lhsT_scale=gds[n][:, k, :],
-                                rhs=wq[:, k, :].bitcast(E4M3), rhs_scale=ws[:, k, :], start=True, stop=True)
+        def tile_quant(r, lo, hi):
+            reads = range(4) if r // 2 in EARLY else range(2 * lo, 2 * hi)
+            return step(lambda: quantize(t["gdq", r][:, lo:hi].rearrange("p e k m -> p (e k m)"), t["gds", r][:, lo:hi].rearrange("p e k m -> p (e k m)"),
+                                         t["gd", r][:, lo:hi].rearrange("p e k m c -> p (e k m c)"), E5M2),
+                        [("gd", r, y) for y in reads], [(("gdq", r, e), ("gdq", r)) for e in range(lo, hi)] + [(("gds", r, e), ("gds", r)) for e in range(lo, hi)])
 
-        def dx_out(n, k, lo, hi, e):
-            if n not in m:
-                m[n] = stage.tile([P, D // 4, K, 4], F32, align_bytes=64, name="m", tag="m", bufs=depth["m"])
-            copier(e)(out=m[n][:, lo // 4:hi // 4, k, :], in_=acc[n, k][:, lo:hi].rearrange("p (q i) -> p q i", i=4))
+        def dx_mm(n, c):
+            r, e = divmod(n, 2)
 
-        def dx_sort(n, lo, hi):
-            if n not in o:
-                o[n] = stage.tile([P, D, K], F32, name="o", tag="o", bufs=depth["o"])
-            nc.vector.tensor_copy(out=o[n][:, lo:hi].rearrange("p (q i) (c k) -> p q c i k", i=4, k=2),
-                                  in_=m[n][:, lo // 4:hi // 4].rearrange("p q (c k) i -> p q c i k", k=2))
+            def run():
+                for k in range(K):
+                    nc.tensor.matmul_mx(out=t["ax", n, c][:, k, :], lhsT=t["gdq", r][:, e, k, :].bitcast(E5M2), lhsT_scale=t["gds", r][:, e, k, :],
+                                        rhs=t["wq"][:, k, P * c:P * (c + 1)].bitcast(E4M3), rhs_scale=t["ws"][:, k, P * c:P * (c + 1)], start=True, stop=True)
+            return step(run, [("gdq", r, e), ("gds", r, e), ("wq", 0), ("wq", 1), ("ws", 0), ("ws", 1)], [(("ax", n, c), bank(("ax", n, c), [P, K, P], F32))])
+
+        def dx_out(n, c, e):
+            return step(lambda: copier(e)(out=t["o", n][:, P * c:P * (c + 1), :], in_=t["ax", n, c][:].rearrange("p k e -> p e k")),
+                        [("ax", n, c)], [(("o", n, c), ("o", n))])
 
         def store_x(n, lo, hi):
             i, j = divmod(n, J)
-            nc.sync.dma_start(out=dxv[i, :, j, K * lo:K * hi], in_=o[n][:, lo:hi].rearrange("p e k -> p (e k)"))
+            return step(lambda: nc.sync.dma_start(out=dxv[i, :, j, D * lo:D * hi], in_=t["o", n][:, P * lo:P * hi].rearrange("p e k -> p (e k)")),
+                        [("o", n, c) for c in range(lo, hi)], [])
 
-        def xa_tile(i):
-            if i not in xa:
-                xa[i] = stage.tile([P, K, D, J], BF16, align_bytes=64, name="xa", tag="xa", bufs=depth["xa"])
-            return xa[i][:]
+        def x_fill(i, b):
+            def run():
+                for c in range(2):
+                    nc.tensor.matmul(t["xp", i, b][:, :, :, 2 * c:2 * c + 2].rearrange("p k e j -> p e k j"), lhsT=t["identb"][:],
+                                     rhs=t["x", i][:, 2 * c:2 * c + 2, K * E * b:K * E * (b + 1)].rearrange("p j (e k) -> p e k j", k=K), start=True, stop=True)
+            return step(run, [("x", i, j) for j in range(J)] + ["identb"], [(("xp", i, b), bank(("xp", i, b), [P, K, E, J], BF16))])
 
-        def narrow_fill(i, z):
-            xp[i, "narrow", z] = bank([P, 2, K, 32, J], BF16)
-            for y in range(2):
-                u = 2 * z + y
-                part = xp[i, "narrow", z][:, y]
-                nc.tensor.matmul(part.rearrange("p k e j -> p j e k"), lhsT=identb[:],
-                                 rhs=x_raw[2 * i][:, :, P * u:P * (u + 1)].rearrange("p j (e k) -> p j e k", k=K), start=True, stop=False)
-                nc.tensor.matmul(part, lhsT=negb[:, u:u + 1].to_broadcast([P, P]),
-                                 rhs=murow[:].rearrange("p (e k) -> p k e", k=K).unsqueeze(3).to_broadcast([P, K, 32, J]), start=False, stop=True)
+        def subtract(i, b, values):
+            nc.vector.tensor_tensor(out=t["xa", i][:, :, E * b:E * (b + 1), :].rearrange("p k e (c j) -> p k e c j", j=2),
+                                    in0=values.rearrange("p k e (c j) -> p k e c j", j=2),
+                                    in1=t["mu2"][:, b].unsqueeze(3).to_broadcast([P, K, E, 2, 2]), op=ALU.subtract)
 
-        def narrow_out(i, z):
-            nc.scalar.copy(out=xa_tile(i)[:, :, 64 * z:64 * (z + 1), :].rearrange("p k (y e) j -> p y k e j", y=2), in_=xp[i, "narrow", z][:])
-
-        def wide_fill(i, *units):
-            for u in units:
-                xp[i, u] = bank([P, J, P], F32)
-                for j in range(J):
-                    nc.tensor.matmul(xp[i, u][:, j, :], lhsT=negmu[:, u:u + 1].to_broadcast([P, P]), rhs=ident[:],
-                                     start=(j == 0), stop=False, is_transpose=True)
-            for u in units:
-                nc.tensor.matmul(xp[i, u][:], lhsT=identb[:], rhs=x_raw[2 * i][:, :, P * u:P * (u + 1)], start=False, stop=True)
-
-        def wide_out(i, u):
-            nc.scalar.copy(out=xa_tile(i)[:, :, 32 * u:32 * (u + 1), :], in_=xp[i, u][:].rearrange("p j (e k) -> p k e j", k=K))
-
-        def x_sub(i):
-            part = x_raw[2 * i + 1][:]
-            nc.vector.tensor_tensor(out=part, in0=part, in1=mub[:, P * UNITS[i] - HALF:].unsqueeze(1).to_broadcast([P, J, DK - P * UNITS[i]]), op=ALU.subtract)
+        def x_out(i, b):
+            return step(lambda: subtract(i, b, t["xp", i, b][:]), [("xp", i, b), ("mu2", b)], [(("xa", i, b), ("xa", i))])
 
         def x_sort(i):
-            interleave(xa_tile(i)[:, :, 32 * UNITS[i]:, :], x_raw[2 * i + 1][:].rearrange("p j (e k) -> p j e k", k=K))
+            lo = ON_TENSOR[i]
+            return step(lambda: interleave(t["xa", i][:, :, E * lo:, :], t["x", i][:, :, K * E * lo:].rearrange("p j (e k) -> p j e k", k=K)),
+                        [("x", i, j) for j in range(J)], [(("xsorted", i), ("xa", i))])
+
+        def x_sub(i, b):
+            return step(lambda: subtract(i, b, t["xa", i][:, :, E * b:E * (b + 1), :]), [("xsorted", i), ("mu2", b)], [(("xa", i, b), ("xa", i))])
 
         def x_quant(i, z):
-            quantize(xq[:, i, 2 * z:2 * z + 2].rearrange("p k e -> p (k e)"), xs[:, i, 2 * z:2 * z + 2].rearrange("p k e -> p (k e)"),
-                     xa_tile(i)[:, 2 * z:2 * z + 2].rearrange("p k e j -> p (k e j)"), E4M3)
+            return step(lambda: quantize(t["xq", i][:, 2 * z:2 * z + 2].rearrange("p k e -> p (k e)"), t["xs", i][:, 2 * z:2 * z + 2].rearrange("p k e -> p (k e)"),
+                                         t["xa", i][:, 2 * z:2 * z + 2].rearrange("p k e j -> p (k e j)"), E4M3),
+                        [("xa", i, b) for b in range(STRIPS)], [(("xq", i, z), ("xq", i)), (("xs", i, z), ("xs", i))])
 
-        def dw_mm(b, lo, hi):
-            c, k = divmod(b, K)
-            if lo == 0:
-                acc["w", b] = bank([P, D], F32)
-            for i in range(lo, hi):
-                nc.tensor.matmul_mx(out=acc["w", b][:], lhsT=gq[:, c, i, k, :].bitcast(E5M2), lhsT_scale=gs[:, c, i, k, :],
-                                    rhs=xq[:, i, k, :].bitcast(E4M3), rhs_scale=xs[:, i, k, :], start=(i == 0), stop=(i == G - 1))
+        passes = EARLY + LATE
 
-        def dw_out(b, e):
-            c, k = divmod(b, K)
-            if c not in ow:
-                ow[c] = turns.tile([P, K, D], F32, name="ow%d" % c, offset=place["ow", c][0])
-            copier(e)(out=ow[c][:, k, :], in_=acc["w", b][:])
+        def dw_mm(c, k, lo, hi):
+            def run():
+                for y in range(lo, hi):
+                    i = passes[y]
+                    nc.tensor.matmul_mx(out=t["aw", c, k][:], lhsT=t["gq", i][:, c, k, :].bitcast(E5M2), lhsT_scale=t["gs", i][:, c, k, :],
+                                        rhs=t["xq", i][:, k, :].bitcast(E4M3), rhs_scale=t["xs", i][:, k, :], start=(y == 0), stop=(y == G - 1))
+            reads = [(name, i, c if name[0] == "g" else k // 2) for i in passes[lo:hi] for name in ("gq", "gs", "xq", "xs")]
+            return step(run, reads + [("aw", c, k, y) for y in range(lo)], [(("aw", c, k, y), bank(("aw", c, k), [P, D], F32)) for y in range(lo, hi)])
 
-        def store_w(b):
-            c, k = divmod(b, K)
-            nc.sync.dma_start(out=dwv[c, :, k:k + 2, :], in_=ow[c][:, k:k + 2, :])
+        def dw_out(c, k, e):
+            return step(lambda: copier(e)(out=t["ow", c][:, k, :], in_=t["aw", c, k][:]), [("aw", c, k, y) for y in range(G)], [(("ow", c, k), ("ow", c))])
 
-        def touches(step):
-            f, a = step[0], step[1:]
-            if f is load_g:
-                return [], [(("g", a[0], j), ("graw", a[0]) if a[0] < G - 1 else ("turns", "g", a[0])) for j in range(a[1], a[2])]
-            if f is load_x:
-                return [], [(("x", a[0]), ("turns", "x", a[0]))]
-            if f is load_w:
-                return [], [(("w", a[0]), ("o", "w", a[0] // 2))]
-            if f is load_mu:
-                return [], [(("mu",), None)]
-            if f is mu_turn:
-                return [("mu",)], [(("mt", z), ("bank", "mt", z)) for z in range(2)]
-            if f is mu_cols:
-                return [("mt", 0), ("mt", 1)], [(("mucol",), None)]
-            if f is mu_spread:
-                return [("mucol",)], [(("mt", 2), ("bank", "mt", 2))]
-            if f is mu_out:
-                return [("mt", 2)], [(("mub",), None)]
-            if f is w_sort:
-                return [("w", a[0])], [(("wa", a[0]), ("m", "wa", a[0] // 2))]
-            if f is w_quant:
-                return [("wa", 2 * a[0] + y) for y in range(2)], [(("wq", 2 * a[0] + y), None) for y in range(2)]
-            if f is g_sort:
-                return [("g", a[0], j) for j in range(J)], [(("ga",) + a, ("ga", a[1]))]
-            if f is g_quant:
-                return [("ga", i, a[0]) for i in range(a[1], a[2])], [(("gq", i, a[0]), None) for i in range(a[1], a[2])]
-            if f is g_turn:
-                return [("g",) + divmod(a[0], J)], [(("tr",) + a, ("bank", "tr") + a)]
-            if f is turned_out:
-                return [("tr",) + a], [(("gd",) + a, ("gd", a[0]))]
-            if f is tile_quant:
-                return [("gd", a[0], z) for z in range(2)], [(("gdq", a[0]), ("gdq", a[0]))]
-            if f is dx_mm:
-                return [("gdq", a[0]), ("wq", a[1])], [(("acc",) + a, ("bank", "acc") + a)]
-            if f is dx_out:
-                return [("acc",) + a[:2]], [(("m", a[0], a[1], e), ("m", a[0])) for e in range(a[2], a[3], P)]
-            if f is dx_sort:
-                return [("m", a[0], k, e) for k in range(K) for e in range(a[1], a[2], P)], [(("o", a[0], e), ("o", a[0])) for e in range(a[1], a[2], P)]
-            if f is store_x:
-                return [("o", a[0], e) for e in range(a[1], a[2], P)], []
-            if f is wide_fill:
-                return [("x", 2 * a[0]), ("mucol",)], [(("xp", a[0], u), ("bank", "xp", a[0], u)) for u in a[1:]]
-            if f is narrow_fill:
-                return [("x", 2 * a[0]), ("mu",)], [(("narrow",) + a, ("bank", "narrow") + a)]
-            if f is wide_out:
-                return [("xp",) + a], [(("xa",) + a, ("xa", a[0]))]
-            if f is narrow_out:
-                return [("narrow",) + a], [(("xa", a[0], 2 * a[1] + y), ("xa", a[0])) for y in range(2)]
-            if f is x_sub:
-                return [("x", 2 * a[0] + 1), ("mub",)], [(("xc", a[0]), ("turns", "x", 2 * a[0] + 1))]
-            if f is x_sort:
-                return [("xc", a[0])], [(("xa", a[0], UNITS[a[0]]), ("xa", a[0]))]
-            if f is x_quant:
-                return [("xa", a[0], u) for u in range(UNITS[a[0]] + 1)], [(("xq",) + a, None)]
-            if f is dw_mm:
-                groups = range(a[1], a[2])
-                return ([("gq", i, a[0] // K) for i in groups] + [("xq", i, a[0] % K // 2) for i in groups] + [("aw", a[0], i) for i in range(a[1])],
-                        [(("aw", a[0], i), ("bank", "aw", a[0])) for i in groups])
-            if f is dw_out:
-                return [("aw", a[0], i) for i in range(G)], [(("ow", a[0]), ("turns", "ow", a[0] // K))]
-            return [("ow", a[0]), ("ow", a[0] + 1)], []
+        def store_w(c, lo, hi):
+            return step(lambda: nc.sync.dma_start(out=dwv[c, :, lo:hi, :], in_=t["ow", c][:, lo:hi, :]), [("ow", c, k) for k in range(lo, hi)], [])
 
-        def deal_banks(tensor):
-            left = [step for step in tensor if step[0] in (narrow_fill, wide_fill)]
-            recent, holder, before = list(range(8)), {}, {}
-            for step in tensor:
-                for piece, buf in touches(step)[1]:
-                    if buf not in before:
-                        b = [b for b in recent if (b >= 6) == (step[0] is narrow_fill) or not left][0]
-                        recent.remove(b)
-                        recent.append(b)
-                        seats.append(b)
-                        before[buf] = [holder[b]] if b in holder else []
-                        holder[b] = buf
-                if step in left:
-                    left.remove(step)
-            return before
-
-        def emit(dma, tensor, scalar, vector):
-            queues = [dma, tensor, scalar, vector]
-            writer, home, users = {}, {}, {}
-            for step in dma + tensor + scalar + vector:
-                for piece, buf in touches(step)[1]:
-                    writer[piece] = step
-                    home[piece] = buf
-            for step in dma + tensor + scalar + vector:
-                reads, writes = touches(step)
-                for piece in reads + [piece for piece, buf in writes]:
-                    users.setdefault(home[piece], []).append(step)
-            banks_before = deal_banks(tensor)
-            done, taken = set(), {tag: [] for tag in list(depth) + ["turns", "bank"]}
-
-            def forerunners(buf):
-                earlier = taken[buf[0]]
-                if buf[0] == "bank":
-                    return banks_before[buf]
-                if buf[0] == "turns":
-                    return [r for r in earlier if place[r[1:]][0] < place[buf[1:]][1] and place[buf[1:]][0] < place[r[1:]][1]]
-                return earlier[-depth[buf[0]]:][:1] if len(earlier) >= depth[buf[0]] else []
-
-            at = [0] * len(queues)
+        def emit(queues, tensor):
+            home, writer, users, before = {}, {}, {}, {}
+            for q in queues:
+                for s in q:
+                    for piece, buf in s[2]:
+                        home[piece], writer[piece] = buf, s
+            for q in queues:
+                for s in q:
+                    for piece in s[1] + tuple(piece for piece, buf in s[2]):
+                        users.setdefault(home[piece], []).append(s)
+            laid = [key for key in spec if len(spec[key]) == 4]
+            for y, key in enumerate(laid):
+                before[key] = [o for o in laid[:y] if spec[o][2] < spec[key][3] and spec[key][2] < spec[o][3]]
+            seat, holder = {}, [None] * 8
+            for s in tensor:
+                for piece, buf in s[2]:
+                    if buf not in seat:
+                        seat[buf] = len(seat) % 8
+                        before[buf] = [] if holder[seat[buf]] is None else [holder[seat[buf]]]
+                        holder[seat[buf]] = buf
+            done, at = set(), [0] * len(queues)
             while any(at[z] < len(q) for z, q in enumerate(queues)):
                 moved = False
                 for z, q in enumerate(queues):
                     while at[z] < len(q):
-                        step = q[at[z]]
-                        reads, writes = touches(step)
-                        fresh = []
-                        for piece, buf in writes:
-                            if buf is not None and buf not in taken[buf[0]] and buf not in fresh:
-                                fresh.append(buf)
-                        if any(writer[piece] not in done for piece in reads) or any(u not in done for buf in fresh for r in forerunners(buf) for u in users[r]):
+                        s = q[at[z]]
+                        fresh = [buf for y, (piece, buf) in enumerate(s[2]) if buf not in t and buf not in [b for p, b in s[2][:y]]]
+                        if any(writer[piece] not in done for piece in s[1]) or any(u not in done for buf in fresh for o in before[buf] for u in users[o]):
                             break
-                        step[0](*step[1:])
-                        done.add(step)
                         for buf in fresh:
-                            taken[buf[0]].append(buf)
+                            if buf in seat:
+                                t[buf] = psum.tile(spec[buf][0], spec[buf][1], name="bank%d" % seat[buf])
+                            else:
+                                t[buf] = sbuf.tile(spec[buf][0], spec[buf][1], name="t%d" % laid.index(buf), offset=spec[buf][2], align_bytes=64)
+                        s[0]()
+                        done.add(s)
                         at[z] = at[z] + 1
                         moved = True
                 assert moved
 
-        def turned(n):
-            return [(turned_out, n, z) for z in range(2)]
-
-        def products(n):
-            return [(dx_out, n, k, 0, D, "S") for k in range(K)]
-
         def weave(a, b):
             return [s for z in range(max(len(a), len(b))) for s in a[z:z + 1] + b[z:z + 1]]
 
-        last, half = N - 1, D // 2
-        xtiles = 2 * G
-        banks = {n: 4 if n == FOUR else 2 for n in range(xtiles, last)}
-        first = {n: sum(banks[z] for z in range(xtiles, n)) for n in range(xtiles, N)}
-        end = first[last]
+        last = 2 * PAIRS - 1
 
-        dma = [(load_g, 0, 0, 1), (load_w, 0), (load_mu,), (load_w, 1)]
+        dma = [load("g", gv, 0, 0, 1), load_w(0), load_mu(), load_w(1)]
         for j in range(1, J):
-            dma = dma + [(load_g, 0, j, j + 1)] + ([(load_w, j + 1)] if j + 1 < K else [])
-        dma = dma + [(load_x, 0), (load_x, 1), (load_g, 1, 0, J)] + [(load_x, 2 * i + b) for i in range(1, G) for b in (1, 0)]
-        dma = dma + [(store_x, 0, 0, D), (store_x, 1, 0, D), (load_g, 2, 0, J), (store_x, 2, 0, D)]
-        for n in range(3, last):
-            dma = dma + [(store_x, n, 0, D)]
-            if n + 1 in banks:
-                dma = dma + [(store_w, b) for b in range(first[n + 1], first[n + 2], 2)]
-        dma = dma + [(store_w, b) for b in range(end, 4 * K, 2)] + [(store_x, last, 0, half), (store_x, last, half, D)]
+            dma = dma + [load("g", gv, 0, j, j + 1)] + ([load_w(j + 1)] if j + 1 < K else [])
+        dma = dma + [load("g", gv, 1, 0, J), load("x", xv, 0, 0, J), store_x(0, 0, 4), store_x(1, 0, 4), load("x", xv, 1, 0, J), load("g", gv, 2, 0, J),
+                     store_x(2, 0, 4), store_x(3, 0, 4), load("x", xv, 2, 0, J)]
+        dma = dma + [store_x(n, 0, 4) for n in range(4, last - 2)]
+        for c in range(J - 1):
+            dma = dma + [store_w(c, 0, K), store_x(last - 2 + c, 0, 4)]
+        dma = dma + [store_w(J - 1, 0, 2), store_w(J - 1, 2, K)]
 
-        scalar = turned(0) + turned(1) + turned(2) + [(mu_out,)] + turned(3)
-        for i in range(G):
-            n = 2 * i
-            wide = [(wide_out, i, u) for u in range(2 * NARROW, UNITS[i])]
-            scalar = scalar + products(n) + (turned(n + LEAD) + turned(n + LEAD + 1) if i else [])
-            scalar = scalar + wide[:2] + products(n + 1)[:2] + [(narrow_out, i, 0)] + wide[2:4] + products(n + 1)[2:] + [(narrow_out, i, 1)] + wide[4:]
-        for n in range(xtiles, last):
-            outs = [(dw_out, b, "S") for b in range(first[n], first[n + 1])]
-            scalar = scalar + (turned(n + LEAD) if n + LEAD < last else []) + products(n)[:2] + weave(products(n)[2:], outs)
-        scalar = scalar + turned(last)
-
-        tensor = []
-        for step in scalar:
-            f, a = step[0], step[1:]
-            if f is turned_out:
-                tensor = tensor + [(g_turn,) + a] + ([((mu_turn, mu_spread)[a[0]],)] if a[0] < 2 and a[1] == 1 else [])
-            if f is dx_out:
-                tensor = tensor + [(dx_mm,) + a[:2]]
-            if f is narrow_out:
-                tensor = tensor + [(narrow_fill,) + a]
-            if f is wide_out and a[1] % 2 == 0:
-                tensor = tensor + [(wide_fill, a[0]) + tuple(range(a[1], min(a[1] + 2, UNITS[a[0]])))]
-            if f is dw_out:
-                tensor = tensor + [(dw_mm, a[0], 0, G)]
-
-        vector = [(w_sort, 0), (mu_cols,), (w_sort, 1), (tile_quant, 0), (w_quant, 0), (w_sort, 2), (w_sort, 3), (tile_quant, 1), (w_quant, 1),
-                  (tile_quant, 2), (g_sort, 0, 0), (tile_quant, 3), (g_quant, 0, 0, 1), (x_sub, 0)]
-        for i in range(G):
-            n = 2 * i
-            codes, sort = [(x_quant, i, z) for z in range(2)], [(dx_sort, n + 1, 0, D)]
-            vector = vector + [(dx_sort, n, 0, D)]
-            if i == 0:
-                vector = vector + [(x_sort, i)] + sort + codes
-                continue
-            if i == 1:
-                vector = vector + [(x_sub, i)]
-            vector = vector + [(tile_quant, n + LEAD), (x_sort, i), (g_sort, i, 0), (tile_quant, n + LEAD + 1)]
-            if i + 1 < G:
-                vector = vector + [(x_sub, i + 1)] + sort + codes
+        scalar, tensor = [], []
+        for r in range(2):
+            scalar = scalar + [turned_out(r, y) for y in range(4)]
+        tensor = [g_turn(0, 0), g_turn(0, 1), mu_turn(), g_turn(0, 2), g_turn(0, 3)] + [g_turn(1, y) for y in range(4)]
+        for r in range(PAIRS - 2):
+            scalar = scalar + [dx_out(n, c, "S") for n in (2 * r, 2 * r + 1) for c in range(4)]
+            fills = [dx_mm(n, c) for n in (2 * r, 2 * r + 1) for c in range(4)]
+            turns = [g_turn(r + 2, y) for y in range(4)]
+            if r == 0:
+                scalar = scalar + [mu_out(q, "S") for q in range(4)]
+                tensor = tensor + fills + [mu_spread(q) for q in range(4)] + turns
             else:
-                vector = vector + [(g_quant, 0, 1, G), (g_sort, 0, 1), (g_sort, 1, 1)] + codes + sort + [(g_quant, 1, 0, 2)]
-        for n in range(xtiles, last):
-            c = (n - 3) // 2
-            ahead = [(tile_quant, n + LEAD)] if n + LEAD < last else []
-            if n % 2 == 0:
-                vector = vector + [(g_sort, 2, c)] + ahead + [(dx_sort, n, 0, D), (g_quant, c, 2, G)]
-            else:
-                vector = vector + [(g_sort, 0, c), (g_sort, 1, c)] + ahead + [(dx_sort, n, 0, D), (g_quant, c, 0, 2)]
+                tensor = tensor + weave(fills, [x_fill(r - 1, b) for b in range(ON_TENSOR[r - 1])]) + turns
+            scalar = scalar + [turned_out(r + 2, y) for y in range(4)]
+        for c in range(J):
+            n = last - 3 + c
+            scalar = scalar + [dx_out(n, y, "S") for y in range(4)] + [dw_out(c, k, "S") for k in range(K if c < J - 1 else 2)]
+            tensor = tensor + [dx_mm(n, y) for y in range(4)]
+            if c < J - 1:
+                tensor = tensor + [dw_mm(c, k, 0, G) for k in range(K)]
+        tensor = tensor + [dw_mm(J - 1, k, 0, G - 1) for k in range(K)] + [dw_mm(J - 1, k, G - 1, G) for k in (0, 2, 1, 3)]
 
-        tensor = tensor + [(dw_mm, b, 0, G - 1) for b in range(end, 4 * K)] + [(dw_mm, b, G - 1, G) for b in range(end, 4 * K)]
-        tensor = tensor + [(dx_mm, last, (k - 1) % K) for k in range(K)]
-        scalar = scalar + [(dw_out, b, "S") for b in range(end, 4 * K - 1)]
-        scalar = scalar + [(dx_out, last, k, lo, lo + half, "S") for lo in (0, half) for k in range(K - 1)]
-        vector = vector + [(tile_quant, last), (dw_out, 4 * K - 1, "V"), (dx_out, last, K - 1, 0, D, "V"), (dx_sort, last, 0, half), (dx_sort, last, half, D)]
+        vector = [mu_zero(), w_sort(0), mu_double(), w_sort(1), tile_quant(0, 0, 1), mu_cols(), w_quant(0), w_sort(2), tile_quant(0, 1, 2), w_sort(3), w_quant(1),
+                  g_sort(0, 0), tile_quant(1, 0, 2), g_quant(0, 0)]
+        vector = vector + [g_sort(1, c) for c in range(J)] + [g_quant(1, c) for c in range(J)]
+        for i in range(G):
+            vector = vector + [x_sort(i), tile_quant(i + 2, 0, 2)] + [x_out(i, b) for b in range(ON_TENSOR[i])] + [x_sub(i, b) for b in range(ON_TENSOR[i], STRIPS)]
+            vector = vector + [x_quant(i, z) for z in range(2)]
+        vector = vector + [g_sort(2, 0), tile_quant(PAIRS - 1, 0, 2), g_quant(2, 0)]
+        for c in range(1, J):
+            vector = vector + [g_sort(i, c) for i in LATE] + [g_quant(i, c) for i in LATE]
+        vector = vector + [dw_out(J - 1, k, "V") for k in range(2, K)]
 
         with tc.manual_schedule():
-            nc.vector.memset(murow[:], 0.0)
-            nc.vector.memset(muwords[:], 0.0)
-            make_identity(nc, ident[:])
-            make_identity(nc, identb[:])
-            nc.vector.tensor_scalar(out=negb[:], in0=identb[:], scalar1=-1.0, scalar2=None, op0=ALU.mult)
-            emit(dma, tensor, scalar, vector)
+            emit([[identities()], dma, tensor, scalar, vector], tensor)

@@ -22,7 +22,7 @@ DK = D * K
 KB = 1024
 E = 64
 STRIPS = D // E
-ON_TENSOR = (7, 6, 6)
+ON_TENSOR = (4, 4, 4)
 EARLY = (1,)
 LATE = tuple(i for i in range(G) if i not in EARLY)
 

@@ -22,8 +22,8 @@ DK = D * K
 KB = 1024
 E = 64
 STRIPS = D // E
-ON_TENSOR = (4, 4, 4)
-EARLY = (1,)
+ON_TENSOR = (0, 5, 4)
+EARLY = (1, 2)
 LATE = tuple(i for i in range(G) if i not in EARLY)
 
 
@@ -53,36 +53,35 @@ def tile_clusternorm1dv3_v_kernel(tc, x, mu, w, g, dx, dw):
             at = at + 20 * KB
         lay("wq", [P, K, D], U32, 8 * KB, at)
         lay("ws", [P, K, D], U8, 2 * KB, at + 8 * KB)
-        lay("mu2", [P, STRIPS, K, E, 2], BF16, 8 * KB, at + 10 * KB)
-        lay("ident", [P, P], F32, 512, at + 18 * KB)
-        lay("identb", [P, P], BF16, 256, at + 18 * KB + 512)
-        lay("mucol", [P, 2, STRIPS], F32, 64, at + 18 * KB + 768)
-        raw = at + 19 * KB
+        lay("mub", [P, DK], BF16, 4 * KB, at + 10 * KB)
+        lay("ident", [P, P], F32, 512, at + 14 * KB)
+        lay("identb", [P, P], BF16, 256, at + 14 * KB + 512)
+        lay("negb", [P, P], BF16, 256, at + 14 * KB + 768)
+        lay("murow", [P, K * E], BF16, 512, at + 15 * KB)
+        lay("mucol", [P, STRIPS], F32, 64, at + 15 * KB + 512)
+        raw = at + 16 * KB
         sort, xsort, turned, codes, out = raw + 64 * KB, raw + 80 * KB, raw + 96 * KB, raw + 112 * KB, raw + 127 * KB
-        for slot, key in ((0, ("g", 0)), (1, ("g", 1)), (2, ("x", 0)), (3, ("g", 2)), (1, ("x", 1)), (2, ("x", 2))):
+        for slot, key in ((0, ("g", 0)), (1, ("g", 1)), (2, ("x", 1)), (3, ("g", 2)), (2, ("x", 2)), (3, ("x", 0))):
             lay(key, [P, J, DK], BF16, 16 * KB, raw + 16 * KB * slot)
-        lay("murow", [P, K * E], BF16, 512, xsort + 8 * KB)
-        lay("mudup", [P, K, E, 2], BF16, KB, xsort + 9 * KB)
         for k in range(K):
             lay(("w", k), [P, J, D], BF16, 4 * KB, out + 16 * KB + 4 * KB * k)
         for z in range(2):
             lay(("wa", z), [P, 2, D, J], BF16, 8 * KB, sort + 8 * KB * z)
-        for i in EARLY:
-            lay(("ga", i), [P, J, K, P, J], BF16, 16 * KB, sort)
-        blocks = [(i, c) for c in range(J) for i in LATE]
-        for y, (i, c) in enumerate(blocks):
-            lay(("gb", i, c), [P, K, P, J], BF16, 4 * KB, xsort if y == 0 else sort + 4 * KB * (y % 4))
-        for i in range(G):
+        lay(("ga", 1), [P, J, K, P, J], BF16, 16 * KB, sort)
+        lay(("ga", 2), [P, J, K, P, J], BF16, 16 * KB, raw + 16 * KB)
+        lay(("gb", 0, 0), [P, K, P, J], BF16, 4 * KB, xsort)
+        for i in EARLY + LATE:
             lay(("xa", i), [P, K, D, J], BF16, 16 * KB, xsort)
+        for c in range(1, J):
+            lay(("gb", 0, c), [P, K, P, J], BF16, 4 * KB, raw + 32 * KB + 4 * KB * c)
         for r in range(PAIRS):
             lay(("gd", r), [P, 2, K, P, J], BF16, 8 * KB, turned + 8 * KB * (r % 2))
             lay(("gdq", r), [P, 2, K, P], U32, 4 * KB, codes + 5 * KB * (r % 3))
             lay(("gds", r), [P, 2, K, P], U8, KB, codes + 5 * KB * (r % 3) + 4 * KB)
-        leaving = [("o", n) for n in range(2 * PAIRS - 3)]
+        for n in range(2 * PAIRS):
+            lay(("o", n), [P, D, K], F32, 8 * KB, out + 8 * KB * (n % 4))
         for c in range(J):
-            leaving = leaving + [("ow", c)] + ([("o", 2 * PAIRS - 3 + c)] if c < J - 1 else [])
-        for y, key in enumerate(leaving):
-            lay(key, [P, D, K] if key[0] == "o" else [P, K, D], F32, 8 * KB, out + 8 * KB * (y % 4))
+            lay(("ow", c), [P, K, D], F32, 8 * KB, (raw + 48 * KB, raw + 56 * KB, xsort, xsort + 8 * KB)[c])
 
         def bank(key, shape, dtype):
             spec[key] = (shape, dtype)
@@ -105,7 +104,7 @@ def tile_clusternorm1dv3_v_kernel(tc, x, mu, w, g, dx, dw):
             return step(lambda: nc.sync.dma_start(out=t["w", k][:], in_=w[k].rearrange("(p j) e -> p j e", j=J)), [], [(("w", k), ("w", k))])
 
         def load_mu():
-            return step(lambda: nc.sync.dma_start(out=t["murow"][0:STRIPS, :], in_=mu_rows), [], [("murow", "murow")])
+            return step(lambda: nc.sync.dma_start(out=t["murow"][0:STRIPS, :], in_=mu_rows), ["muzero"], [("murow", "murow")])
 
         def identities():
             def run():
@@ -114,31 +113,26 @@ def tile_clusternorm1dv3_v_kernel(tc, x, mu, w, g, dx, dw):
             return step(run, [], [("ident", "ident"), ("identb", "identb")])
 
         def mu_zero():
-            return step(lambda: nc.vector.memset(t["mudup"][:], 0.0), [], [("muzero", "mudup")])
+            return step(lambda: nc.vector.memset(t["murow"][:], 0.0), [], [("muzero", "murow")])
 
-        def mu_double():
-            return step(lambda: nc.vector.tensor_copy(out=t["mudup"][0:STRIPS], in_=t["murow"][0:STRIPS, :].rearrange("p (e k) -> p k e", k=K).unsqueeze(3).to_broadcast([STRIPS, K, E, 2])),
-                        ["murow", "muzero"], [("mudup", "mudup")])
+        def negate():
+            return step(lambda: nc.vector.tensor_scalar(out=t["negb"][:], in0=t["identb"][:], scalar1=-1.0, scalar2=None, op0=ALU.mult), ["identb"], [("negb", "negb")])
 
         def mu_turn():
-            def run():
-                for h in range(2):
-                    nc.tensor.transpose(t["mt"][:, h, :], t["mudup"][:].rearrange("p k e j -> p (k e j)").bitcast(F32)[:, P * h:P * (h + 1)], t["ident"][:])
-            return step(run, ["mudup", "ident"], [("mt", bank("mt", [P, 2, P], F32))])
+            return step(lambda: nc.tensor.transpose(t["mt"][:], t["murow"][:].bitcast(F32), t["ident"][:]), ["murow", "ident"], [("mt", bank("mt", [P, P], F32))])
 
         def mu_cols():
-            return step(lambda: nc.vector.tensor_copy(out=t["mucol"][:], in_=t["mt"][:, :, 0:STRIPS]), ["mt"], [("mucol", "mucol")])
+            return step(lambda: nc.vector.tensor_copy(out=t["mucol"][:], in_=t["mt"][:, 0:STRIPS]), ["mt"], [("mucol", "mucol")])
 
         def mu_spread(q):
             def run():
                 for y in range(4):
-                    b, h = 2 * q + y // 2, y % 2
-                    nc.tensor.transpose(t["ms", q][:, y, :], t["mucol"][:, h, b:b + 1].to_broadcast([P, P]), t["ident"][:])
+                    nc.tensor.transpose(t["ms", q][:, y, :], t["mucol"][:, 4 * q + y:4 * q + y + 1].to_broadcast([P, P]), t["ident"][:])
             return step(run, ["mucol", "ident"], [(("ms", q), bank(("ms", q), [P, 4, P], F32))])
 
         def mu_out(q, e):
-            return step(lambda: copier(e)(out=t["mu2"][:, 2 * q:2 * q + 2].rearrange("p b k e j -> p (b k e j)").bitcast(F32), in_=t["ms", q][:].rearrange("p y n -> p (y n)")),
-                        [("ms", q)], [(("mu2", 2 * q + y), "mu2") for y in range(2)])
+            return step(lambda: copier(e)(out=t["mub"][:, DK // 2 * q:DK // 2 * (q + 1)].bitcast(F32), in_=t["ms", q][:].rearrange("p y n -> p (y n)")),
+                        [("ms", q)], [(("mub", q), "mub")])
 
         def w_sort(k):
             return step(lambda: nc.vector.tensor_copy(out=t["wa", k // 2][:, k % 2].rearrange("p (c i) j -> p c j i", i=4), in_=t["w", k][:].rearrange("p j (c i) -> p c j i", i=4)),
@@ -209,26 +203,27 @@ def tile_clusternorm1dv3_v_kernel(tc, x, mu, w, g, dx, dw):
 
         def x_fill(i, b):
             def run():
-                for c in range(2):
-                    nc.tensor.matmul(t["xp", i, b][:, :, :, 2 * c:2 * c + 2].rearrange("p k e j -> p e k j"), lhsT=t["identb"][:],
-                                     rhs=t["x", i][:, 2 * c:2 * c + 2, K * E * b:K * E * (b + 1)].rearrange("p j (e k) -> p e k j", k=K), start=True, stop=True)
-            return step(run, [("x", i, j) for j in range(J)] + ["identb"], [(("xp", i, b), bank(("xp", i, b), [P, K, E, J], BF16))])
-
-        def subtract(i, b, values):
-            nc.vector.tensor_tensor(out=t["xa", i][:, :, E * b:E * (b + 1), :].rearrange("p k e (c j) -> p k e c j", j=2),
-                                    in0=values.rearrange("p k e (c j) -> p k e c j", j=2),
-                                    in1=t["mu2"][:, b].unsqueeze(3).to_broadcast([P, K, E, 2, 2]), op=ALU.subtract)
+                for y in range(2):
+                    part = t["xp", i, b][:, y]
+                    nc.tensor.matmul(part, lhsT=t["negb"][:, b:b + 1].to_broadcast([P, P]),
+                                     rhs=t["murow"][:, P * y:P * (y + 1)].rearrange("p (e k) -> p k e", k=K).unsqueeze(3).to_broadcast([P, K, E // 2, J]), start=True, stop=False)
+                    nc.tensor.matmul(part.rearrange("p k e j -> p j e k"), lhsT=t["identb"][:],
+                                     rhs=t["x", i][:, :, K * E * b + P * y:K * E * b + P * (y + 1)].rearrange("p j (e k) -> p j e k", k=K), start=False, stop=True)
+            return step(run, [("x", i, j) for j in range(J)] + ["identb", "negb", "murow"], [(("xp", i, b), bank(("xp", i, b), [P, 2, K, E // 2, J], BF16))])
 
         def x_out(i, b):
-            return step(lambda: subtract(i, b, t["xp", i, b][:]), [("xp", i, b), ("mu2", b)], [(("xa", i, b), ("xa", i))])
+            return step(lambda: nc.scalar.copy(out=t["xa", i][:, :, E * b:E * (b + 1), :].rearrange("p k (y e) j -> p y k e j", y=2), in_=t["xp", i, b][:]),
+                        [("xp", i, b)], [(("xa", i, b), ("xa", i))])
 
-        def x_sort(i):
-            lo = ON_TENSOR[i]
-            return step(lambda: interleave(t["xa", i][:, :, E * lo:, :], t["x", i][:, :, K * E * lo:].rearrange("p j (e k) -> p j e k", k=K)),
-                        [("x", i, j) for j in range(J)], [(("xsorted", i), ("xa", i))])
+        def x_sub(i, lo, hi):
+            part = slice(K * E * lo, K * E * hi)
+            return step(lambda: nc.vector.tensor_tensor(out=t["x", i][:, :, part], in0=t["x", i][:, :, part],
+                                                        in1=t["mub"][:, part].unsqueeze(1).to_broadcast([P, J, K * E * (hi - lo)]), op=ALU.subtract),
+                        [("x", i, j) for j in range(J)] + [("mub", 0), ("mub", 1)], [(("xc", i, b), ("x", i)) for b in range(lo, hi)])
 
-        def x_sub(i, b):
-            return step(lambda: subtract(i, b, t["xa", i][:, :, E * b:E * (b + 1), :]), [("xsorted", i), ("mu2", b)], [(("xa", i, b), ("xa", i))])
+        def x_sort(i, lo, hi):
+            return step(lambda: interleave(t["xa", i][:, :, E * lo:E * hi, :], t["x", i][:, :, K * E * lo:K * E * hi].rearrange("p j (e k) -> p j e k", k=K)),
+                        [("xc", i, b) for b in range(lo, hi)], [(("xa", i, b), ("xa", i)) for b in range(lo, hi)])
 
         def x_quant(i, z):
             return step(lambda: quantize(t["xq", i][:, 2 * z:2 * z + 2].rearrange("p k e -> p (k e)"), t["xs", i][:, 2 * z:2 * z + 2].rearrange("p k e -> p (k e)"),
@@ -295,50 +290,49 @@ def tile_clusternorm1dv3_v_kernel(tc, x, mu, w, g, dx, dw):
         def weave(a, b):
             return [s for z in range(max(len(a), len(b))) for s in a[z:z + 1] + b[z:z + 1]]
 
-        last = 2 * PAIRS - 1
+        last, half = 2 * PAIRS - 1, STRIPS // 2
 
-        dma = [load("g", gv, 0, 0, 1), load_w(0), load_mu(), load_w(1)]
+        dma = [load("g", gv, 0, 0, 1), load_w(0), load_mu()]
         for j in range(1, J):
-            dma = dma + [load("g", gv, 0, j, j + 1)] + ([load_w(j + 1)] if j + 1 < K else [])
-        dma = dma + [load("g", gv, 1, 0, J), load("x", xv, 0, 0, J), store_x(0, 0, 4), store_x(1, 0, 4), load("x", xv, 1, 0, J), load("g", gv, 2, 0, J),
-                     store_x(2, 0, 4), store_x(3, 0, 4), load("x", xv, 2, 0, J)]
-        dma = dma + [store_x(n, 0, 4) for n in range(4, last - 2)]
-        for c in range(J - 1):
-            dma = dma + [store_w(c, 0, K), store_x(last - 2 + c, 0, 4)]
-        dma = dma + [store_w(J - 1, 0, 2), store_w(J - 1, 2, K)]
+            dma = dma + [load_w(j), load("g", gv, 0, j, j + 1)]
+        dma = dma + [load("g", gv, 1, 0, J), load("x", xv, 1, 0, J), load("g", gv, 2, 0, J)] + [store_x(n, 0, 4) for n in range(3)]
+        dma = dma + [load("x", xv, 2, 0, J), load("x", xv, 0, 0, J), store_x(3, 0, 4)] + [store_x(n, lo, lo + 2) for n in range(4, last - 1) for lo in (0, 2)]
+        dma = dma + [store_w(0, 0, 2), store_w(0, 2, 4), store_w(1, 0, 2), store_w(1, 2, 4), store_x(last - 1, 0, 2), store_x(last - 1, 2, 4),
+                     store_w(2, 0, 2), store_w(2, 2, 4), store_x(last, 0, 2), store_x(last, 2, 4), store_w(3, 0, 2), store_w(3, 2, 3), store_w(3, 3, 4)]
 
-        scalar, tensor = [], []
-        for r in range(2):
-            scalar = scalar + [turned_out(r, y) for y in range(4)]
-        tensor = [g_turn(0, 0), g_turn(0, 1), mu_turn(), g_turn(0, 2), g_turn(0, 3)] + [g_turn(1, y) for y in range(4)]
-        for r in range(PAIRS - 2):
-            scalar = scalar + [dx_out(n, c, "S") for n in (2 * r, 2 * r + 1) for c in range(4)]
-            fills = [dx_mm(n, c) for n in (2 * r, 2 * r + 1) for c in range(4)]
-            turns = [g_turn(r + 2, y) for y in range(4)]
-            if r == 0:
-                scalar = scalar + [mu_out(q, "S") for q in range(4)]
-                tensor = tensor + fills + [mu_spread(q) for q in range(4)] + turns
-            else:
-                tensor = tensor + weave(fills, [x_fill(r - 1, b) for b in range(ON_TENSOR[r - 1])]) + turns
-            scalar = scalar + [turned_out(r + 2, y) for y in range(4)]
-        for c in range(J):
-            n = last - 3 + c
-            scalar = scalar + [dx_out(n, y, "S") for y in range(4)] + [dw_out(c, k, "S") for k in range(K if c < J - 1 else 2)]
-            tensor = tensor + [dx_mm(n, y) for y in range(4)]
-            if c < J - 1:
-                tensor = tensor + [dw_mm(c, k, 0, G) for k in range(K)]
-        tensor = tensor + [dw_mm(J - 1, k, 0, G - 1) for k in range(K)] + [dw_mm(J - 1, k, G - 1, G) for k in (0, 2, 1, 3)]
+        helped = [(4, 0), (4, 1)]
 
-        vector = [mu_zero(), w_sort(0), mu_double(), w_sort(1), tile_quant(0, 0, 1), mu_cols(), w_quant(0), w_sort(2), tile_quant(0, 1, 2), w_sort(3), w_quant(1),
-                  g_sort(0, 0), tile_quant(1, 0, 2), g_quant(0, 0)]
-        vector = vector + [g_sort(1, c) for c in range(J)] + [g_quant(1, c) for c in range(J)]
-        for i in range(G):
-            vector = vector + [x_sort(i), tile_quant(i + 2, 0, 2)] + [x_out(i, b) for b in range(ON_TENSOR[i])] + [x_sub(i, b) for b in range(ON_TENSOR[i], STRIPS)]
-            vector = vector + [x_quant(i, z) for z in range(2)]
-        vector = vector + [g_sort(2, 0), tile_quant(PAIRS - 1, 0, 2), g_quant(2, 0)]
-        for c in range(1, J):
-            vector = vector + [g_sort(i, c) for i in LATE] + [g_quant(i, c) for i in LATE]
-        vector = vector + [dw_out(J - 1, k, "V") for k in range(2, K)]
+        def turns(r):
+            return [(g_turn(r, y), turned_out(r, y)) for y in range(4)]
+
+        def product(n):
+            return [(dx_mm(n, c), dx_out(n, c, "S") if (n, c) not in helped else None) for c in range(4)]
+
+        def products(r):
+            return product(2 * r) + product(2 * r + 1)
+
+        def strips(i):
+            return [(x_fill(i, b), x_out(i, b)) for b in range(ON_TENSOR[i])]
+
+        def block(c, lo):
+            return [(dw_mm(c, k, lo, G), dw_out(c, k, "S")) for k in range(K)]
+
+        banked = turns(0)[:2] + [(mu_turn(), None)] + [(mu_spread(q), mu_out(q, "S")) for q in range(2)] + turns(0)[2:] + turns(1) + products(0) + products(1)
+        banked = banked + weave(strips(1), turns(2)) + turns(3) + products(2) + weave(strips(2), turns(4)) + products(3) + products(4)
+        banked = banked + turns(5) + [(dw_mm(0, k, 0, G - 1), None) for k in range(K)] + block(0, G - 1) + block(1, 0) + product(last - 1) + block(2, 0) + product(last)
+        scalar = [s[1] for s in banked if s[1]] + [dw_out(J - 1, k, "S") for k in (0, 2)]
+        tensor = [s[0] for s in banked] + [dw_mm(J - 1, k, 0, G) for k in range(K)]
+
+        vector = [mu_zero(), negate(), w_sort(0), mu_cols(), w_sort(1), tile_quant(0, 0, 1), w_quant(0), w_sort(2), w_sort(3), tile_quant(0, 1, 2), w_quant(1),
+                  g_sort(0, 0), tile_quant(1, 0, 1), g_quant(0, 0)]
+        vector = vector + [g_sort(1, 0), tile_quant(1, 1, 2)] + [g_sort(1, c) for c in range(1, J)] + [x_sub(1, ON_TENSOR[1], STRIPS), g_quant(1, 0), x_sort(1, ON_TENSOR[1], STRIPS)]
+        vector = vector + [g_sort(2, c) for c in range(J)] + [tile_quant(2, 0, 2), x_quant(1, 0), x_quant(1, 1), g_quant(2, 0)]
+        vector = vector + [dx_out(4, 0, "V"), dx_out(4, 1, "V")] + [x_sub(2, ON_TENSOR[2], STRIPS), tile_quant(3, 0, 2), x_sort(2, ON_TENSOR[2], STRIPS), x_sub(0, 0, half), x_sub(0, half, STRIPS), tile_quant(4, 0, 2), x_quant(2, 0), x_quant(2, 1)]
+        vector = vector + [x_sort(0, 0, half), x_sort(0, half, STRIPS), x_quant(0, 0), x_quant(0, 1)]
+        vector = vector + [g_sort(0, 1), g_quant(1, 1), g_quant(2, 1), g_quant(0, 1), tile_quant(5, 0, 2)]
+        for c in range(2, J):
+            vector = vector + [g_sort(0, c), g_quant(1, c), g_quant(2, c), g_quant(0, c)]
+        vector = vector + [dw_out(J - 1, k, "V") for k in (1, 3)]
 
         with tc.manual_schedule():
-            emit([[identities()], dma, tensor, scalar, vector], tensor)
+            emit([[identities()], vector, dma, tensor, scalar], tensor)

@@ -81,7 +81,7 @@ def tile_clusternorm1dv3_v_kernel(tc, x, mu, w, g, dx, dw):
         for n in range(2 * PAIRS):
             lay(("o", n), [P, D, K], F32, 8 * KB, out + 8 * KB * (n % 4))
         for c in range(J):
-            lay(("ow", c), [P, K, D], F32, 8 * KB, (raw + 48 * KB, raw + 56 * KB, xsort, xsort + 8 * KB)[c])
+            lay(("ow", c), [P, K, D], F32, 8 * KB, (turned, turned + 8 * KB, xsort, xsort + 8 * KB)[c])
 
         def bank(key, shape, dtype):
             spec[key] = (shape, dtype)
@@ -171,10 +171,10 @@ def tile_clusternorm1dv3_v_kernel(tc, x, mu, w, g, dx, dw):
             reads = [("ga", i, c) for c in range(J)] if i in EARLY else [("g", i, 2 * z + y // 2)]
             return step(run, reads + ["ident"], [(("tr", r, y), bank(("tr", r, y), [P, J, P], F32))])
 
-        def turned_out(r, y):
+        def turned_out(r, y, e):
             def run():
                 part = t["gd", r][:, :, y] if r // 2 in EARLY else t["gd", r][:, y // 2, 2 * (y % 2):2 * (y % 2) + 2]
-                nc.scalar.copy(out=part, in_=t["tr", r, y][:].bitcast(BF16).rearrange("q c (m e) -> q e m c", e=2))
+                copier(e)(out=part, in_=t["tr", r, y][:].bitcast(BF16).rearrange("q c (m e) -> q e m c", e=2))
             return step(run, [("tr", r, y)], [(("gd", r, y), ("gd", r))])
 
         def tile_quant(r, lo, hi):
@@ -196,6 +196,20 @@ def tile_clusternorm1dv3_v_kernel(tc, x, mu, w, g, dx, dw):
             return step(lambda: copier(e)(out=t["o", n][:, P * c:P * (c + 1), :], in_=t["ax", n, c][:].rearrange("p k e -> p e k")),
                         [("ax", n, c)], [(("o", n, c), ("o", n))])
 
+        def wide_mm(n, k):
+            r, e = divmod(n, 2)
+            return step(lambda: nc.tensor.matmul_mx(out=t["ax", n, k][:], lhsT=t["gdq", r][:, e, k, :].bitcast(E5M2), lhsT_scale=t["gds", r][:, e, k, :],
+                                                    rhs=t["wq"][:, k, :].bitcast(E4M3), rhs_scale=t["ws"][:, k, :], start=True, stop=True),
+                        [("gdq", r, e), ("gds", r, e), ("wq", k // 2), ("ws", k // 2)], [(("ax", n, k), bank(("ax", n, k), [P, D], F32))])
+
+        def wide_out(n, k, e):
+            return step(lambda: copier(e)(out=t["m", n][:, :, k, :], in_=t["ax", n, k][:].rearrange("p (q i) -> p q i", i=4)), [("ax", n, k)], [(("m", n, k), ("m", n))])
+
+        def wide_sort(n, lo, hi):
+            return step(lambda: nc.vector.tensor_copy(out=t["o", n][:, P * lo:P * hi].rearrange("p (q i) (c k) -> p q c i k", i=4, k=2),
+                                                      in_=t["m", n][:, P // 4 * lo:P // 4 * hi].rearrange("p q (c k) i -> p q c i k", k=2)),
+                        [("m", n, k) for k in range(K)], [(("o", n, c), ("o", n)) for c in range(lo, hi)])
+
         def store_x(n, lo, hi):
             i, j = divmod(n, J)
             return step(lambda: nc.sync.dma_start(out=dxv[i, :, j, D * lo:D * hi], in_=t["o", n][:, P * lo:P * hi].rearrange("p e k -> p (e k)")),
@@ -211,8 +225,8 @@ def tile_clusternorm1dv3_v_kernel(tc, x, mu, w, g, dx, dw):
                                      rhs=t["x", i][:, :, K * E * b + P * y:K * E * b + P * (y + 1)].rearrange("p j (e k) -> p j e k", k=K), start=False, stop=True)
             return step(run, [("x", i, j) for j in range(J)] + ["identb", "negb", "murow"], [(("xp", i, b), bank(("xp", i, b), [P, 2, K, E // 2, J], BF16))])
 
-        def x_out(i, b):
-            return step(lambda: nc.scalar.copy(out=t["xa", i][:, :, E * b:E * (b + 1), :].rearrange("p k (y e) j -> p y k e j", y=2), in_=t["xp", i, b][:]),
+        def x_out(i, b, e):
+            return step(lambda: copier(e)(out=t["xa", i][:, :, E * b:E * (b + 1), :].rearrange("p k (y e) j -> p y k e j", y=2), in_=t["xp", i, b][:]),
                         [("xp", i, b)], [(("xa", i, b), ("xa", i))])
 
         def x_sub(i, lo, hi):
@@ -225,10 +239,14 @@ def tile_clusternorm1dv3_v_kernel(tc, x, mu, w, g, dx, dw):
             return step(lambda: interleave(t["xa", i][:, :, E * lo:E * hi, :], t["x", i][:, :, K * E * lo:K * E * hi].rearrange("p j (e k) -> p j e k", k=K)),
                         [("xc", i, b) for b in range(lo, hi)], [(("xa", i, b), ("xa", i)) for b in range(lo, hi)])
 
+        def x_pair(i, z):
+            return step(lambda: interleave(t["xa", i][:, 2 * z:2 * z + 2], t["x", i][:].rearrange("p j (e k) -> p j e k", k=K)[:, :, :, 2 * z:2 * z + 2]),
+                        [("xc", i, b) for b in range(STRIPS)], [(("xa", i, "pair", z), ("xa", i))])
+
         def x_quant(i, z):
             return step(lambda: quantize(t["xq", i][:, 2 * z:2 * z + 2].rearrange("p k e -> p (k e)"), t["xs", i][:, 2 * z:2 * z + 2].rearrange("p k e -> p (k e)"),
                                          t["xa", i][:, 2 * z:2 * z + 2].rearrange("p k e j -> p (k e j)"), E4M3),
-                        [("xa", i, b) for b in range(STRIPS)], [(("xq", i, z), ("xq", i)), (("xs", i, z), ("xs", i))])
+                        [("xa", i, b) for b in range(STRIPS)] if i in EARLY else [("xa", i, "pair", z)], [(("xq", i, z), ("xq", i)), (("xs", i, z), ("xs", i))])
 
         passes = EARLY + LATE
 
@@ -297,13 +315,14 @@ def tile_clusternorm1dv3_v_kernel(tc, x, mu, w, g, dx, dw):
             dma = dma + [load_w(j), load("g", gv, 0, j, j + 1)]
         dma = dma + [load("g", gv, 1, 0, J), load("x", xv, 1, 0, J), load("g", gv, 2, 0, J)] + [store_x(n, 0, 4) for n in range(3)]
         dma = dma + [load("x", xv, 2, 0, J), load("x", xv, 0, 0, J), store_x(3, 0, 4)] + [store_x(n, lo, lo + 2) for n in range(4, last - 1) for lo in (0, 2)]
-        dma = dma + [store_w(0, 0, 2), store_w(0, 2, 4), store_w(1, 0, 2), store_w(1, 2, 4), store_x(last - 1, 0, 2), store_x(last - 1, 2, 4),
-                     store_w(2, 0, 2), store_w(2, 2, 4), store_x(last, 0, 2), store_x(last, 2, 4), store_w(3, 0, 2), store_w(3, 2, 3), store_w(3, 3, 4)]
+        for c in range(2):
+            dma = dma + [store_w(c, 0, 2), store_x(last - 1 + c, 0, 2), store_x(last - 1 + c, 2, 4)]
+        dma = dma + [store_w(0, 2, 4), store_w(1, 2, 4), store_w(2, 0, 2), store_w(2, 2, 4), store_w(3, 0, 2), store_w(3, 2, 3), store_w(3, 3, 4)]
 
         helped = [(4, 0), (4, 1)]
 
         def turns(r):
-            return [(g_turn(r, y), turned_out(r, y)) for y in range(4)]
+            return [(g_turn(r, y), turned_out(r, y, "S") if ("turn", r, y) not in helped else None) for y in range(4)]
 
         def product(n):
             return [(dx_mm(n, c), dx_out(n, c, "S") if (n, c) not in helped else None) for c in range(4)]
@@ -312,25 +331,25 @@ def tile_clusternorm1dv3_v_kernel(tc, x, mu, w, g, dx, dw):
             return product(2 * r) + product(2 * r + 1)
 
         def strips(i):
-            return [(x_fill(i, b), x_out(i, b)) for b in range(ON_TENSOR[i])]
+            return [(x_fill(i, b), x_out(i, b, "S") if ("x", i, b) not in helped else None) for b in range(ON_TENSOR[i])]
 
-        def block(c, lo):
-            return [(dw_mm(c, k, lo, G), dw_out(c, k, "S")) for k in range(K)]
+        def block(c, lo, hi):
+            return [(dw_mm(c, k, 0, G), dw_out(c, k, "S")) for k in range(lo, hi)]
 
         banked = turns(0)[:2] + [(mu_turn(), None)] + [(mu_spread(q), mu_out(q, "S")) for q in range(2)] + turns(0)[2:] + turns(1) + products(0) + products(1)
-        banked = banked + weave(strips(1), turns(2)) + turns(3) + products(2) + weave(strips(2), turns(4)) + products(3) + products(4)
-        banked = banked + turns(5) + [(dw_mm(0, k, 0, G - 1), None) for k in range(K)] + block(0, G - 1) + block(1, 0) + product(last - 1) + block(2, 0) + product(last)
+        banked = banked + weave(strips(1), turns(2)) + turns(3) + products(2) + weave(strips(2), turns(4)) + products(3) + turns(5) + products(4)
+        banked = banked + block(0, 0, 2) + product(last - 1) + block(1, 0, 2) + product(last) + block(0, 2, K) + block(1, 2, K) + block(2, 0, K)
         scalar = [s[1] for s in banked if s[1]] + [dw_out(J - 1, k, "S") for k in (0, 2)]
-        tensor = [s[0] for s in banked] + [dw_mm(J - 1, k, 0, G) for k in range(K)]
+        tensor = [s[0] for s in banked if s[0]] + [dw_mm(J - 1, k, 0, G) for k in range(K)]
 
         vector = [mu_zero(), negate(), w_sort(0), mu_cols(), w_sort(1), tile_quant(0, 0, 1), w_quant(0), w_sort(2), w_sort(3), tile_quant(0, 1, 2), w_quant(1),
                   g_sort(0, 0), tile_quant(1, 0, 1), g_quant(0, 0)]
         vector = vector + [g_sort(1, 0), tile_quant(1, 1, 2)] + [g_sort(1, c) for c in range(1, J)] + [x_sub(1, ON_TENSOR[1], STRIPS), g_quant(1, 0), x_sort(1, ON_TENSOR[1], STRIPS)]
         vector = vector + [g_sort(2, c) for c in range(J)] + [tile_quant(2, 0, 2), x_quant(1, 0), x_quant(1, 1), g_quant(2, 0)]
-        vector = vector + [dx_out(4, 0, "V"), dx_out(4, 1, "V")] + [x_sub(2, ON_TENSOR[2], STRIPS), tile_quant(3, 0, 2), x_sort(2, ON_TENSOR[2], STRIPS), x_sub(0, 0, half), x_sub(0, half, STRIPS), tile_quant(4, 0, 2), x_quant(2, 0), x_quant(2, 1)]
-        vector = vector + [x_sort(0, 0, half), x_sort(0, half, STRIPS), x_quant(0, 0), x_quant(0, 1)]
-        vector = vector + [g_sort(0, 1), g_quant(1, 1), g_quant(2, 1), g_quant(0, 1), tile_quant(5, 0, 2)]
-        for c in range(2, J):
+        vector = vector + [dx_out(4, 0, "V"), dx_out(4, 1, "V")] + [x_sub(2, ON_TENSOR[2], STRIPS), tile_quant(3, 0, 2), x_sort(2, ON_TENSOR[2], STRIPS), x_sub(0, 0, half), x_sub(0, half, STRIPS), x_quant(2, 0), x_quant(2, 1), tile_quant(4, 0, 2)]
+        vector = vector + [x_pair(0, 0), g_sort(0, 1), x_quant(0, 0), tile_quant(5, 0, 2), g_quant(1, 1), g_quant(2, 1), g_quant(0, 1), x_pair(0, 1)]
+        vector = vector + [g_sort(0, 2), x_quant(0, 1), g_quant(1, 2), g_quant(2, 2), g_quant(0, 2)]
+        for c in range(3, J):
             vector = vector + [g_sort(0, c), g_quant(1, c), g_quant(2, c), g_quant(0, c)]
         vector = vector + [dw_out(J - 1, k, "V") for k in (1, 3)]
 

@@ -22,7 +22,7 @@ DK = D * K
 KB = 1024
 E = 64
 STRIPS = D // E
-ON_TENSOR = (0, 5, 4)
+ON_TENSOR = (0, 3, 4)
 EARLY = (1, 2)
 LATE = tuple(i for i in range(G) if i not in EARLY)
 
@@ -61,19 +61,19 @@ def tile_clusternorm1dv3_v_kernel(tc, x, mu, w, g, dx, dw):
         lay("mucol", [P, STRIPS], F32, 64, at + 15 * KB + 512)
         raw = at + 16 * KB
         sort, xsort, turned, codes, out = raw + 64 * KB, raw + 80 * KB, raw + 96 * KB, raw + 112 * KB, raw + 127 * KB
-        for slot, key in ((0, ("g", 0)), (1, ("g", 1)), (2, ("x", 1)), (3, ("g", 2)), (2, ("x", 2)), (3, ("x", 0))):
+        for slot, key in ((0, ("g", 0)), (1, ("g", 1)), (2, ("x", 1)), (3, ("x", 2)), (1, ("g", 2)), (1, ("x", 0))):
             lay(key, [P, J, DK], BF16, 16 * KB, raw + 16 * KB * slot)
         for k in range(K):
             lay(("w", k), [P, J, D], BF16, 4 * KB, out + 16 * KB + 4 * KB * k)
         for z in range(2):
             lay(("wa", z), [P, 2, D, J], BF16, 8 * KB, sort + 8 * KB * z)
         lay(("ga", 1), [P, J, K, P, J], BF16, 16 * KB, sort)
-        lay(("ga", 2), [P, J, K, P, J], BF16, 16 * KB, raw + 16 * KB)
+        lay(("ga", 2), [P, J, K, P, J], BF16, 16 * KB, raw + 32 * KB)
         lay(("gb", 0, 0), [P, K, P, J], BF16, 4 * KB, xsort)
         for i in EARLY + LATE:
             lay(("xa", i), [P, K, D, J], BF16, 16 * KB, xsort)
         for c in range(1, J):
-            lay(("gb", 0, c), [P, K, P, J], BF16, 4 * KB, raw + 32 * KB + 4 * KB * c)
+            lay(("gb", 0, c), [P, K, P, J], BF16, 4 * KB, raw + 48 * KB + 4 * KB * c)
         for r in range(PAIRS):
             lay(("gd", r), [P, 2, K, P, J], BF16, 8 * KB, turned + 8 * KB * (r % 2))
             lay(("gdq", r), [P, 2, K, P], U32, 4 * KB, codes + 5 * KB * (r % 3))
@@ -221,8 +221,9 @@ def tile_clusternorm1dv3_v_kernel(tc, x, mu, w, g, dx, dw):
                     part = t["xp", i, b][:, y]
                     nc.tensor.matmul(part, lhsT=t["negb"][:, b:b + 1].to_broadcast([P, P]),
                                      rhs=t["murow"][:, P * y:P * (y + 1)].rearrange("p (e k) -> p k e", k=K).unsqueeze(3).to_broadcast([P, K, E // 2, J]), start=True, stop=False)
-                    nc.tensor.matmul(part.rearrange("p k e j -> p j e k"), lhsT=t["identb"][:],
-                                     rhs=t["x", i][:, :, K * E * b + P * y:K * E * b + P * (y + 1)].rearrange("p j (e k) -> p j e k", k=K), start=False, stop=True)
+                    for c in range(2):
+                        nc.tensor.matmul(part[:, :, :, 2 * c:2 * c + 2].rearrange("p k e j -> p e k j"), lhsT=t["identb"][:],
+                                         rhs=t["x", i][:, 2 * c:2 * c + 2, K * E * b + P * y:K * E * b + P * (y + 1)].rearrange("p j (e k) -> p e k j", k=K), start=False, stop=(c == 1))
             return step(run, [("x", i, j) for j in range(J)] + ["identb", "negb", "murow"], [(("xp", i, b), bank(("xp", i, b), [P, 2, K, E // 2, J], BF16))])
 
         def x_out(i, b, e):
@@ -313,13 +314,13 @@ def tile_clusternorm1dv3_v_kernel(tc, x, mu, w, g, dx, dw):
         dma = [load("g", gv, 0, 0, 1), load_w(0), load_mu()]
         for j in range(1, J):
             dma = dma + [load_w(j), load("g", gv, 0, j, j + 1)]
-        dma = dma + [load("g", gv, 1, 0, J), load("x", xv, 1, 0, J), load("g", gv, 2, 0, J)] + [store_x(n, 0, 4) for n in range(3)]
-        dma = dma + [load("x", xv, 2, 0, J), load("x", xv, 0, 0, J), store_x(3, 0, 4)] + [store_x(n, lo, lo + 2) for n in range(4, last - 1) for lo in (0, 2)]
+        dma = dma + [load("g", gv, 1, 0, J), load("x", xv, 1, 0, J), load("x", xv, 2, 0, J), load("g", gv, 2, 0, J)] + [store_x(n, 0, 4) for n in range(4)]
+        dma = dma + [load("x", xv, 0, 0, J)] + [store_x(n, lo, lo + 2) for n in range(4, last - 1) for lo in (0, 2)]
         for c in range(2):
             dma = dma + [store_w(c, 0, 2), store_x(last - 1 + c, 0, 2), store_x(last - 1 + c, 2, 4)]
         dma = dma + [store_w(0, 2, 4), store_w(1, 2, 4), store_w(2, 0, 2), store_w(2, 2, 4), store_w(3, 0, 2), store_w(3, 2, 3), store_w(3, 3, 4)]
 
-        helped = [(4, 0), (4, 1)]
+        helped = []
 
         def turns(r):
             return [(g_turn(r, y), turned_out(r, y, "S") if ("turn", r, y) not in helped else None) for y in range(4)]
@@ -337,7 +338,7 @@ def tile_clusternorm1dv3_v_kernel(tc, x, mu, w, g, dx, dw):
             return [(dw_mm(c, k, 0, G), dw_out(c, k, "S")) for k in range(lo, hi)]
 
         banked = turns(0)[:2] + [(mu_turn(), None)] + [(mu_spread(q), mu_out(q, "S")) for q in range(2)] + turns(0)[2:] + turns(1) + products(0) + products(1)
-        banked = banked + weave(strips(1), turns(2)) + turns(3) + products(2) + weave(strips(2), turns(4)) + products(3) + turns(5) + products(4)
+        banked = banked + turns(2) + weave(strips(1), turns(3)) + products(2) + weave(strips(2), turns(4)) + products(3) + turns(5) + products(4)
         banked = banked + block(0, 0, 2) + product(last - 1) + block(1, 0, 2) + product(last) + block(0, 2, K) + block(1, 2, K) + block(2, 0, K)
         scalar = [s[1] for s in banked if s[1]] + [dw_out(J - 1, k, "S") for k in (0, 2)]
         tensor = [s[0] for s in banked if s[0]] + [dw_mm(J - 1, k, 0, G) for k in range(K)]
@@ -345,8 +346,8 @@ def tile_clusternorm1dv3_v_kernel(tc, x, mu, w, g, dx, dw):
         vector = [mu_zero(), negate(), w_sort(0), mu_cols(), w_sort(1), tile_quant(0, 0, 1), w_quant(0), w_sort(2), w_sort(3), tile_quant(0, 1, 2), w_quant(1),
                   g_sort(0, 0), tile_quant(1, 0, 1), g_quant(0, 0)]
         vector = vector + [g_sort(1, 0), tile_quant(1, 1, 2)] + [g_sort(1, c) for c in range(1, J)] + [x_sub(1, ON_TENSOR[1], STRIPS), g_quant(1, 0), x_sort(1, ON_TENSOR[1], STRIPS)]
-        vector = vector + [g_sort(2, c) for c in range(J)] + [tile_quant(2, 0, 2), x_quant(1, 0), x_quant(1, 1), g_quant(2, 0)]
-        vector = vector + [dx_out(4, 0, "V"), dx_out(4, 1, "V")] + [x_sub(2, ON_TENSOR[2], STRIPS), tile_quant(3, 0, 2), x_sort(2, ON_TENSOR[2], STRIPS), x_sub(0, 0, half), x_sub(0, half, STRIPS), x_quant(2, 0), x_quant(2, 1), tile_quant(4, 0, 2)]
+        vector = vector + [x_sub(2, ON_TENSOR[2], STRIPS), tile_quant(2, 0, 2)] + [g_sort(2, c) for c in range(J)] + [x_quant(1, 0), x_quant(1, 1), tile_quant(3, 0, 2)]
+        vector = vector + [g_quant(2, 0), x_sort(2, ON_TENSOR[2], STRIPS), x_sub(0, 0, half), x_sub(0, half, STRIPS), tile_quant(4, 0, 2), x_quant(2, 0), x_quant(2, 1)]
         vector = vector + [x_pair(0, 0), g_sort(0, 1), x_quant(0, 0), tile_quant(5, 0, 2), g_quant(1, 1), g_quant(2, 1), g_quant(0, 1), x_pair(0, 1)]
         vector = vector + [g_sort(0, 2), x_quant(0, 1), g_quant(1, 2), g_quant(2, 2), g_quant(0, 2)]
         for c in range(3, J):

@@ -22,7 +22,7 @@ DK = D * K
 KB = 1024
 E = 64
 STRIPS = D // E
-ON_TENSOR = (0, 3, 4)
+ON_TENSOR = (0, 3, 5)
 EARLY = (1, 2)
 LATE = tuple(i for i in range(G) if i not in EARLY)
 
@@ -339,7 +339,7 @@ def tile_clusternorm1dv3_v_kernel(tc, x, mu, w, g, dx, dw):
 
         banked = turns(0)[:2] + [(mu_turn(), None)] + [(mu_spread(q), mu_out(q, "S")) for q in range(2)] + turns(0)[2:] + turns(1) + products(0) + products(1)
         banked = banked + turns(2) + weave(strips(1), turns(3)) + products(2) + weave(strips(2), turns(4)) + products(3) + turns(5) + products(4)
-        banked = banked + block(0, 0, 2) + product(last - 1) + block(1, 0, 2) + product(last) + block(0, 2, K) + block(1, 2, K) + block(2, 0, K)
+        banked = banked + block(0, 0, 2) + product(last - 1) + block(1, 0, 2) + product(last) + [(dw_mm(c, k, 0, G - 1), None) for c in range(2) for k in range(2, K)] + [(dw_mm(c, k, G - 1, G), dw_out(c, k, "S")) for c in range(2) for k in range(2, K)] + block(2, 0, K)
         scalar = [s[1] for s in banked if s[1]] + [dw_out(J - 1, k, "S") for k in (0, 2)]
         tensor = [s[0] for s in banked if s[0]] + [dw_mm(J - 1, k, 0, G) for k in range(K)]
 

from contextlib import ExitStack

import concourse.mybir as mybir
from concourse.masks import make_identity

B, D, K = 1536, 512, 4
FLOPS = 2 * 2 * B * D * D * K

F32 = mybir.dt.float32
BF16 = mybir.dt.bfloat16
U32 = mybir.dt.uint32
U8 = mybir.dt.uint8
E4M3 = mybir.dt.float8_e4m3fn_x4
E5M2 = mybir.dt.float8_e5m2_x4
ALU = mybir.AluOpType

P = 128
J = 4
G = B // (P * J)
PAIRS = 2 * G
DK = D * K
KB = 1024
E = 64
STRIPS = D // E
ON_TENSOR = (0, 3, 5)
EARLY = (1, 2)
LATE = tuple(i for i in range(G) if i not in EARLY)


def tile_clusternorm1dv3_v_kernel(tc, x, mu, w, g, dx, dw):
    nc = tc.nc
    xv = x.rearrange("(g p j) d k -> g p j (d k)", p=P, j=J)
    gv = g.rearrange("(g p j) d k -> g p j (d k)", p=P, j=J)
    dxv = dx.rearrange("(g p j) d k -> g p j (d k)", p=P, j=J)
    dwv = dw.rearrange("k (q t) e -> t q k e", t=J)
    mu_rows = mu.rearrange("(b e) k -> b (e k)", b=STRIPS)

    with ExitStack() as ctx:
        sbuf = ctx.enter_context(tc.tile_pool(name="sbuf", bufs=1))
        psum = ctx.enter_context(tc.psum_pool(name="psum", bufs=1))

        spec, t = {}, {}

        def lay(key, shape, dtype, size, at):
            spec[key] = (shape, dtype, at, at + size)

        at = 0
        for i in range(G):
            lay(("gq", i), [P, J, K, P], U32, 8 * KB, at)
            lay(("xq", i), [P, K, D], U32, 8 * KB, at + 8 * KB)
            lay(("gs", i), [P, J, K, P], U8, 2 * KB, at + 16 * KB)
            lay(("xs", i), [P, K, D], U8, 2 * KB, at + 18 * KB)
            at = at + 20 * KB
        lay("wq", [P, K, D], U32, 8 * KB, at)
        lay("ws", [P, K, D], U8, 2 * KB, at + 8 * KB)
        lay("mub", [P, DK], BF16, 4 * KB, at + 10 * KB)
        lay("ident", [P, P], F32, 512, at + 14 * KB)
        lay("identb", [P, P], BF16, 256, at + 14 * KB + 512)
        lay("negb", [P, P], BF16, 256, at + 14 * KB + 768)
        lay("murow", [P, K * E], BF16, 512, at + 15 * KB)
        lay("mucol", [P, STRIPS], F32, 64, at + 15 * KB + 512)
        raw = at + 16 * KB
        sort, xsort, turned, codes, out = raw + 64 * KB, raw + 80 * KB, raw + 96 * KB, raw + 112 * KB, raw + 127 * KB
        for slot, key in ((0, ("g", 0)), (1, ("g", 1)), (2, ("x", 1)), (3, ("x", 2)), (1, ("g", 2)), (1, ("x", 0))):
            lay(key, [P, J, DK], BF16, 16 * KB, raw + 16 * KB * slot)
        for k in range(K):
            lay(("w", k), [P, J, D], BF16, 4 * KB, out + 16 * KB + 4 * KB * k)
        for z in range(2):
            lay(("wa", z), [P, 2, D, J], BF16, 8 * KB, sort + 8 * KB * z)
        lay(("ga", 1), [P, J, K, P, J], BF16, 16 * KB, sort)
        lay(("ga", 2), [P, J, K, P, J], BF16, 16 * KB, raw + 32 * KB)
        lay(("gb", 0, 0), [P, K, P, J], BF16, 4 * KB, xsort)
        for i in EARLY + LATE:
            lay(("xa", i), [P, K, D, J], BF16, 16 * KB, xsort)
        for c in range(1, J):
            lay(("gb", 0, c), [P, K, P, J], BF16, 4 * KB, raw + 48 * KB + 4 * KB * c)
        for r in range(PAIRS):
            lay(("gd", r), [P, 2, K, P, J], BF16, 8 * KB, turned + 8 * KB * (r % 2))
            lay(("gdq", r), [P, 2, K, P], U32, 4 * KB, codes + 5 * KB * (r % 3))
            lay(("gds", r), [P, 2, K, P], U8, KB, codes + 5 * KB * (r % 3) + 4 * KB)
        for n in range(2 * PAIRS):
            lay(("o", n), [P, D, K], F32, 8 * KB, out + 8 * KB * (n % 4))
        for c in range(J):
            lay(("ow", c), [P, K, D], F32, 8 * KB, (turned, turned + 8 * KB, xsort, xsort + 8 * KB)[c])

        def bank(key, shape, dtype):
            spec[key] = (shape, dtype)
            return key

        def step(run, reads, writes):
            return (run, tuple(reads), tuple(writes))

        def copier(e):
            return nc.vector.tensor_copy if e == "V" else nc.scalar.copy

        def quantize(codes, scales, values, dtype):
            nc.vector.quantize_mx(out=codes.bitcast(dtype), scales=scales, in_=values)

        def load(name, view, i, lo, hi):
            return step(lambda: nc.sync.dma_start(out=t[name, i][:, lo:hi, :], in_=view[i, :, lo:hi, :]),
                        [], [((name, i, j), (name, i)) for j in range(lo, hi)])

        def load_w(k):
            return step(lambda: nc.sync.dma_start(out=t["w", k][:], in_=w[k].rearrange("(p j) e -> p j e", j=J)), [], [(("w", k), ("w", k))])

        def load_mu():
            return step(lambda: nc.sync.dma_start(out=t["murow"][0:STRIPS, :], in_=mu_rows), ["muzero"], [("murow", "murow")])

        def identities():
            def run():
                make_identity(nc, t["ident"][:])
                make_identity(nc, t["identb"][:])
            return step(run, [], [("ident", "ident"), ("identb", "identb")])

        def mu_zero():
            return step(lambda: nc.vector.memset(t["murow"][:], 0.0), [], [("muzero", "murow")])

        def negate():
            return step(lambda: nc.vector.tensor_scalar(out=t["negb"][:], in0=t["identb"][:], scalar1=-1.0, scalar2=None, op0=ALU.mult), ["identb"], [("negb", "negb")])

        def mu_turn():
            return step(lambda: nc.tensor.transpose(t["mt"][:], t["murow"][:].bitcast(F32), t["ident"][:]), ["murow", "ident"], [("mt", bank("mt", [P, P], F32))])

        def mu_cols():
            return step(lambda: nc.vector.tensor_copy(out=t["mucol"][:], in_=t["mt"][:, 0:STRIPS]), ["mt"], [("mucol", "mucol")])

        def mu_spread(q):
            def run():
                for y in range(4):
                    nc.tensor.transpose(t["ms", q][:, y, :], t["mucol"][:, 4 * q + y:4 * q + y + 1].to_broadcast([P, P]), t["ident"][:])
            return step(run, ["mucol", "ident"], [(("ms", q), bank(("ms", q), [P, 4, P], F32))])

        def mu_out(q, e):
            return step(lambda: copier(e)(out=t["mub"][:, DK // 2 * q:DK // 2 * (q + 1)].bitcast(F32), in_=t["ms", q][:].rearrange("p y n -> p (y n)")),
                        [("ms", q)], [(("mub", q), "mub")])

        def w_sort(k):
            return step(lambda: nc.vector.tensor_copy(out=t["wa", k // 2][:, k % 2].rearrange("p (c i) j -> p c j i", i=4), in_=t["w", k][:].rearrange("p j (c i) -> p c j i", i=4)),
                        [("w", k)], [(("wa", k), ("wa", k // 2))])

        def w_quant(z):
            return step(lambda: quantize(t["wq"][:, 2 * z:2 * z + 2].rearrange("p k e -> p (k e)"), t["ws"][:, 2 * z:2 * z + 2].rearrange("p k e -> p (k e)"),
                                         t["wa", z][:].rearrange("p k e j -> p (k e j)"), E4M3),
                        [("wa", 2 * z), ("wa", 2 * z + 1)], [(("wq", z), "wq"), (("ws", z), "ws")])

        def interleave(out, in_):
            nc.vector.tensor_copy(out=out.rearrange("p k e (c j) -> p e c k j", j=2), in_=in_.rearrange("p (c j) e k -> p e c k j", j=2))

        def sorted_g(i, c):
            return t["ga", i][:, c] if i in EARLY else t["gb", i, c][:]

        def g_sort(i, c):
            return step(lambda: interleave(sorted_g(i, c), t["g", i][:].rearrange("p j (q c k) -> p c j q k", c=J, k=K)[:, c]),
                        [("g", i, j) for j in range(J)], [(("ga", i, c), ("ga", i) if i in EARLY else ("gb", i, c))])

        def g_quant(i, c):
            return step(lambda: quantize(t["gq", i][:, c].rearrange("p k q -> p (k q)"), t["gs", i][:, c].rearrange("p k q -> p (k q)"),
                                         sorted_g(i, c).rearrange("p k q j -> p (k q j)"), E5M2),
                        [("ga", i, c)], [(("gq", i, c), ("gq", i)), (("gs", i, c), ("gs", i))])

        def g_turn(r, y):
            i, z = divmod(r, 2)

            def run():
                for c in range(J):
                    if i in EARLY:
                        words = t["ga", i][:, c, y].rearrange("p q j -> p (q j)").bitcast(F32)[:, z:2 * P:2]
                    else:
                        words = t["g", i][:].bitcast(F32)[:, 2 * z + y // 2, 2 * c + y % 2:DK // 2:8]
                    nc.tensor.transpose(t["tr", r, y][:, c, :], words, t["ident"][:])
            reads = [("ga", i, c) for c in range(J)] if i in EARLY else [("g", i, 2 * z + y // 2)]
            return step(run, reads + ["ident"], [(("tr", r, y), bank(("tr", r, y), [P, J, P], F32))])

        def turned_out(r, y, e):
            def run():
                part = t["gd", r][:, :, y] if r // 2 in EARLY else t["gd", r][:, y // 2, 2 * (y % 2):2 * (y % 2) + 2]
                copier(e)(out=part, in_=t["tr", r, y][:].bitcast(BF16).rearrange("q c (m e) -> q e m c", e=2))
            return step(run, [("tr", r, y)], [(("gd", r, y), ("gd", r))])

        def tile_quant(r, lo, hi):
            reads = range(4) if r // 2 in EARLY else range(2 * lo, 2 * hi)
            return step(lambda: quantize(t["gdq", r][:, lo:hi].rearrange("p e k m -> p (e k m)"), t["gds", r][:, lo:hi].rearrange("p e k m -> p (e k m)"),
                                         t["gd", r][:, lo:hi].rearrange("p e k m c -> p (e k m c)"), E5M2),
                        [("gd", r, y) for y in reads], [(("gdq", r, e), ("gdq", r)) for e in range(lo, hi)] + [(("gds", r, e), ("gds", r)) for e in range(lo, hi)])

        def dx_mm(n, c):
            r, e = divmod(n, 2)

            def run():
                for k in range(K):
                    nc.tensor.matmul_mx(out=t["ax", n, c][:, k, :], lhsT=t["gdq", r][:, e, k, :].bitcast(E5M2), lhsT_scale=t["gds", r][:, e, k, :],
                                        rhs=t["wq"][:, k, P * c:P * (c + 1)].bitcast(E4M3), rhs_scale=t["ws"][:, k, P * c:P * (c + 1)], start=True, stop=True)
            return step(run, [("gdq", r, e), ("gds", r, e), ("wq", 0), ("wq", 1), ("ws", 0), ("ws", 1)], [(("ax", n, c), bank(("ax", n, c), [P, K, P], F32))])

        def dx_out(n, c, e):
            return step(lambda: copier(e)(out=t["o", n][:, P * c:P * (c + 1), :], in_=t["ax", n, c][:].rearrange("p k e -> p e k")),
                        [("ax", n, c)], [(("o", n, c), ("o", n))])

        def wide_mm(n, k):
            r, e = divmod(n, 2)
            return step(lambda: nc.tensor.matmul_mx(out=t["ax", n, k][:], lhsT=t["gdq", r][:, e, k, :].bitcast(E5M2), lhsT_scale=t["gds", r][:, e, k, :],
                                                    rhs=t["wq"][:, k, :].bitcast(E4M3), rhs_scale=t["ws"][:, k, :], start=True, stop=True),
                        [("gdq", r, e), ("gds", r, e), ("wq", k // 2), ("ws", k // 2)], [(("ax", n, k), bank(("ax", n, k), [P, D], F32))])

        def wide_out(n, k, e):
            return step(lambda: copier(e)(out=t["m", n][:, :, k, :], in_=t["ax", n, k][:].rearrange("p (q i) -> p q i", i=4)), [("ax", n, k)], [(("m", n, k), ("m", n))])

        def wide_sort(n, lo, hi):
            return step(lambda: nc.vector.tensor_copy(out=t["o", n][:, P * lo:P * hi].rearrange("p (q i) (c k) -> p q c i k", i=4, k=2),
                                                      in_=t["m", n][:, P // 4 * lo:P // 4 * hi].rearrange("p q (c k) i -> p q c i k", k=2)),
                        [("m", n, k) for k in range(K)], [(("o", n, c), ("o", n)) for c in range(lo, hi)])

        def store_x(n, lo, hi):
            i, j = divmod(n, J)
            return step(lambda: nc.sync.dma_start(out=dxv[i, :, j, D * lo:D * hi], in_=t["o", n][:, P * lo:P * hi].rearrange("p e k -> p (e k)")),
                        [("o", n, c) for c in range(lo, hi)], [])

        def x_fill(i, b):
            def run():
                for y in range(2):
                    part = t["xp", i, b][:, y]
                    nc.tensor.matmul(part, lhsT=t["negb"][:, b:b + 1].to_broadcast([P, P]),
                                     rhs=t["murow"][:, P * y:P * (y + 1)].rearrange("p (e k) -> p k e", k=K).unsqueeze(3).to_broadcast([P, K, E // 2, J]), start=True, stop=False)
                    for c in range(2):
                        nc.tensor.matmul(part[:, :, :, 2 * c:2 * c + 2].rearrange("p k e j -> p e k j"), lhsT=t["identb"][:],
                                         rhs=t["x", i][:, 2 * c:2 * c + 2, K * E * b + P * y:K * E * b + P * (y + 1)].rearrange("p j (e k) -> p e k j", k=K), start=False, stop=(c == 1))
            return step(run, [("x", i, j) for j in range(J)] + ["identb", "negb", "murow"], [(("xp", i, b), bank(("xp", i, b), [P, 2, K, E // 2, J], BF16))])

        def x_out(i, b, e):
            return step(lambda: copier(e)(out=t["xa", i][:, :, E * b:E * (b + 1), :].rearrange("p k (y e) j -> p y k e j", y=2), in_=t["xp", i, b][:]),
                        [("xp", i, b)], [(("xa", i, b), ("xa", i))])

        def x_sub(i, lo, hi):
            part = slice(K * E * lo, K * E * hi)
            return step(lambda: nc.vector.tensor_tensor(out=t["x", i][:, :, part], in0=t["x", i][:, :, part],
                                                        in1=t["mub"][:, part].unsqueeze(1).to_broadcast([P, J, K * E * (hi - lo)]), op=ALU.subtract),
                        [("x", i, j) for j in range(J)] + [("mub", 0), ("mub", 1)], [(("xc", i, b), ("x", i)) for b in range(lo, hi)])

        def x_sort(i, lo, hi):
            return step(lambda: interleave(t["xa", i][:, :, E * lo:E * hi, :], t["x", i][:, :, K * E * lo:K * E * hi].rearrange("p j (e k) -> p j e k", k=K)),
                        [("xc", i, b) for b in range(lo, hi)], [(("xa", i, b), ("xa", i)) for b in range(lo, hi)])

        def x_pair(i, z):
            return step(lambda: interleave(t["xa", i][:, 2 * z:2 * z + 2], t["x", i][:].rearrange("p j (e k) -> p j e k", k=K)[:, :, :, 2 * z:2 * z + 2]),
                        [("xc", i, b) for b in range(STRIPS)], [(("xa", i, "pair", z), ("xa", i))])

        def x_quant(i, z):
            return step(lambda: quantize(t["xq", i][:, 2 * z:2 * z + 2].rearrange("p k e -> p (k e)"), t["xs", i][:, 2 * z:2 * z + 2].rearrange("p k e -> p (k e)"),
                                         t["xa", i][:, 2 * z:2 * z + 2].rearrange("p k e j -> p (k e j)"), E4M3),
                        [("xa", i, b) for b in range(STRIPS)] if i in EARLY else [("xa", i, "pair", z)], [(("xq", i, z), ("xq", i)), (("xs", i, z), ("xs", i))])

        passes = EARLY + LATE

        def dw_mm(c, k, lo, hi):
            def run():
                for y in range(lo, hi):
                    i = passes[y]
                    nc.tensor.matmul_mx(out=t["aw", c, k][:], lhsT=t["gq", i][:, c, k, :].bitcast(E5M2), lhsT_scale=t["gs", i][:, c, k, :],
                                        rhs=t["xq", i][:, k, :].bitcast(E4M3), rhs_scale=t["xs", i][:, k, :], start=(y == 0), stop=(y == G - 1))
            reads = [(name, i, c if name[0] == "g" else k // 2) for i in passes[lo:hi] for name in ("gq", "gs", "xq", "xs")]
            return step(run, reads + [("aw", c, k, y) for y in range(lo)], [(("aw", c, k, y), bank(("aw", c, k), [P, D], F32)) for y in range(lo, hi)])

        def dw_out(c, k, e):
            return step(lambda: copier(e)(out=t["ow", c][:, k, :], in_=t["aw", c, k][:]), [("aw", c, k, y) for y in range(G)], [(("ow", c, k), ("ow", c))])

        def store_w(c, lo, hi):
            return step(lambda: nc.sync.dma_start(out=dwv[c, :, lo:hi, :], in_=t["ow", c][:, lo:hi, :]), [("ow", c, k) for k in range(lo, hi)], [])

        def emit(queues, tensor):
            home, writer, users, before = {}, {}, {}, {}
            for q in queues:
                for s in q:
                    for piece, buf in s[2]:
                        home[piece], writer[piece] = buf, s
            for q in queues:
                for s in q:
                    for piece in s[1] + tuple(piece for piece, buf in s[2]):
                        users.setdefault(home[piece], []).append(s)
            laid = [key for key in spec if len(spec[key]) == 4]
            for y, key in enumerate(laid):
                before[key] = [o for o in laid[:y] if spec[o][2] < spec[key][3] and spec[key][2] < spec[o][3]]
            seat, holder = {}, [None] * 8
            for s in tensor:
                for piece, buf in s[2]:
                    if buf not in seat:
                        seat[buf] = len(seat) % 8
                        before[buf] = [] if holder[seat[buf]] is None else [holder[seat[buf]]]
                        holder[seat[buf]] = buf
            done, at = set(), [0] * len(queues)
            while any(at[z] < len(q) for z, q in enumerate(queues)):
                moved = False
                for z, q in enumerate(queues):
                    while at[z] < len(q):
                        s = q[at[z]]
                        fresh = [buf for y, (piece, buf) in enumerate(s[2]) if buf not in t and buf not in [b for p, b in s[2][:y]]]
                        if any(writer[piece] not in done for piece in s[1]) or any(u not in done for buf in fresh for o in before[buf] for u in users[o]):
                            break
                        for buf in fresh:
                            if buf in seat:
                                t[buf] = psum.tile(spec[buf][0], spec[buf][1], name="bank%d" % seat[buf])
                            else:
                                t[buf] = sbuf.tile(spec[buf][0], spec[buf][1], name="t%d" % laid.index(buf), offset=spec[buf][2], align_bytes=64)
                        s[0]()
                        done.add(s)
                        at[z] = at[z] + 1
                        moved = True
                assert moved

        def weave(a, b):
            return [s for z in range(max(len(a), len(b))) for s in a[z:z + 1] + b[z:z + 1]]

        last, half = 2 * PAIRS - 1, STRIPS // 2

        dma = [load("g", gv, 0, 0, 1), load_w(0), load_mu()]
        for j in range(1, J):
            dma = dma + [load_w(j), load("g", gv, 0, j, j + 1)]
        dma = dma + [load("g", gv, 1, 0, J), load("x", xv, 1, 0, J), load("x", xv, 2, 0, J), load("g", gv, 2, 0, J)] + [store_x(n, 0, 4) for n in range(4)]
        dma = dma + [load("x", xv, 0, 0, J)] + [store_x(n, lo, lo + 2) for n in range(4, last - 1) for lo in (0, 2)]
        for c in range(2):
            dma = dma + [store_w(c, 0, 2), store_x(last - 1 + c, 0, 2), store_x(last - 1 + c, 2, 4)]
        dma = dma + [store_w(0, 2, 4), store_w(1, 2, 4), store_w(2, 0, 2), store_w(2, 2, 4), store_w(3, 0, 2), store_w(3, 2, 3), store_w(3, 3, 4)]

        helped = []

        def turns(r):
            return [(g_turn(r, y), turned_out(r, y, "S") if ("turn", r, y) not in helped else None) for y in range(4)]

        def product(n):
            return [(dx_mm(n, c), dx_out(n, c, "S") if (n, c) not in helped else None) for c in range(4)]

        def products(r):
            return product(2 * r) + product(2 * r + 1)

        def strips(i):
            return [(x_fill(i, b), x_out(i, b, "S") if ("x", i, b) not in helped else None) for b in range(ON_TENSOR[i])]

        def block(c, lo, hi):
            return [(dw_mm(c, k, 0, G), dw_out(c, k, "S")) for k in range(lo, hi)]

        banked = turns(0)[:2] + [(mu_turn(), None)] + [(mu_spread(q), mu_out(q, "S")) for q in range(2)] + turns(0)[2:] + turns(1) + products(0) + products(1)
        banked = banked + turns(2) + weave(strips(1), turns(3)) + products(2) + weave(strips(2), turns(4)) + products(3) + turns(5) + products(4)
        banked = banked + block(0, 0, 2) + product(last - 1) + block(1, 0, 2) + product(last) + [(dw_mm(c, k, 0, G - 1), None) for c in range(2) for k in range(2, K)] + [(dw_mm(c, k, G - 1, G), dw_out(c, k, "S")) for c in range(2) for k in range(2, K)] + block(2, 0, K)
        scalar = [s[1] for s in banked if s[1]] + [dw_out(J - 1, k, "S") for k in (0, 2)]
        tensor = [s[0] for s in banked if s[0]] + [dw_mm(J - 1, k, 0, G) for k in range(K)]

        vector = [mu_zero(), negate(), w_sort(0), mu_cols(), w_sort(1), tile_quant(0, 0, 1), w_quant(0), w_sort(2), w_sort(3), tile_quant(0, 1, 2), w_quant(1),
                  g_sort(0, 0), tile_quant(1, 0, 1), g_quant(0, 0)]
        vector = vector + [g_sort(1, 0), tile_quant(1, 1, 2)] + [g_sort(1, c) for c in range(1, J)] + [x_sub(1, ON_TENSOR[1], STRIPS), g_quant(1, 0), x_sort(1, ON_TENSOR[1], STRIPS)]
        vector = vector + [x_sub(2, ON_TENSOR[2], STRIPS), tile_quant(2, 0, 2)] + [g_sort(2, c) for c in range(J)] + [x_quant(1, 0), x_quant(1, 1), tile_quant(3, 0, 2)]
        vector = vector + [g_quant(2, 0), x_sort(2, ON_TENSOR[2], STRIPS), x_sub(0, 0, half), x_sub(0, half, STRIPS), tile_quant(4, 0, 2), x_quant(2, 0), x_quant(2, 1)]
        vector = vector + [x_pair(0, 0), g_sort(0, 1), x_quant(0, 0), tile_quant(5, 0, 2), g_quant(1, 1), g_quant(2, 1), g_quant(0, 1), x_pair(0, 1)]
        vector = vector + [g_sort(0, 2), x_quant(0, 1), g_quant(1, 2), g_quant(2, 2), g_quant(0, 2)]
        for c in range(3, J):
            vector = vector + [g_sort(0, c), g_quant(1, c), g_quant(2, c), g_quant(0, c)]
        vector = vector + [dw_out(J - 1, k, "V") for k in (1, 3)]

        with tc.manual_schedule():
            emit([[identities()], vector, dma, tensor, scalar], tensor)
